import numpy as np
import ml_dtypes


def mxq(x, axis, fmt="e4m3"):
    dtype, down = {"e4m3": (ml_dtypes.float8_e4m3fn, 7), "e5m2": (ml_dtypes.float8_e5m2, 14)}[fmt]
    v = np.moveaxis(np.asarray(x, np.float32).astype(ml_dtypes.bfloat16).astype(np.float64), axis, -1)
    blocks = v.reshape(v.shape[:-1] + (-1, 32))
    amax = np.abs(blocks).max(-1, keepdims=True)
    byte = np.maximum(np.where(amax > 0, np.frexp(amax)[1] - 1 + 127, 0) - down, 1)
    scale = np.exp2(byte - 127.0)
    codes = (blocks / scale).astype(np.float32).astype(dtype).astype(np.float64)
    return np.moveaxis((codes * scale).reshape(v.shape), -1, axis)


WIDE = False


def mx_kscale(k):
    if not WIDE:
        return np.ones(k)
    levels = np.array([10, -10, 5, -5, 0])
    if k % 512:
        return np.exp2(np.random.permutation(np.resize(levels, k // 32))).repeat(32)
    a = np.empty((k // 512, 16))
    for p in range(k // 512):
        a[p, :8] = np.random.permutation(np.resize(levels, 8))
        for g in range(8):
            far = levels[np.abs(levels - a[p, g]) >= 10]
            a[p, g + 8] = far[np.random.randint(len(far))]
    return np.exp2(a.ravel()).repeat(32)


BF16 = ml_dtypes.bfloat16


def bf(x):
    return np.asarray(x, np.float32).astype(BF16)


def f64(x):
    return np.asarray(x).astype(np.float64)


E2M1 = np.array([0.0, 0.5, 1.0, 1.5, 2.0, 3.0, 4.0, 6.0, -0.0, -0.5, -1.0, -1.5, -2.0, -3.0, -4.0, -6.0])


def pack_weight(w, fmt):
    k, n = w.shape
    w = f64(bf(w)).reshape(k // 32, 32, n)
    amax = np.abs(w).max(1)
    if fmt == "e4m3":
        byte = np.frexp(amax)[1] - 1 + 127 - 7
    else:
        mant, ex = np.frexp(amax / 6.0)
        byte = np.where(mant > 0.5, ex, ex - 1) + 127
    byte = np.clip(np.where(amax > 0, byte, 1), 1, 254)
    scaled = (w * np.exp2(127.0 - byte)[:, None, :]).reshape(k, n).astype(np.float32)
    by_word = np.ascontiguousarray(scaled.reshape(k // 512, 128, 4, n).transpose(0, 1, 3, 2))
    if fmt == "e4m3":
        words = by_word.astype(ml_dtypes.float8_e4m3fn).view(np.uint8)
    else:
        c = by_word.astype(ml_dtypes.float4_e2m1fn).view(np.uint8) & 0xF
        words = c[..., 0::2] | (c[..., 1::2] << 4)
    return np.ascontiguousarray(words), np.ascontiguousarray(byte.astype(np.uint8).reshape(k // 512, 16, n))


def unpack_weight(words, scales, fmt):
    g, p, n, _ = words.shape
    if fmt == "e4m3":
        vals = np.ascontiguousarray(words).view(ml_dtypes.float8_e4m3fn).astype(np.float64)
    else:
        nib = np.empty((g, p, n, 4), np.uint8)
        nib[..., 0::2] = words & 0xF
        nib[..., 1::2] = words >> 4
        vals = E2M1[nib]
    vals = vals * np.repeat(np.exp2(scales.astype(np.float64) - 127.0), 8, axis=1)[..., None]
    return vals.transpose(0, 1, 3, 2).reshape(g * 512, n)
def pack4(w):
    words, scales = pack_weight(w, "e2m1")
    return words.reshape(words.shape[0], 128, -1), scales


def unpack4(words, scales):
    return unpack_weight(words.reshape(words.shape[0], 128, -1, 2), scales, "e2m1")


B, S, D, E, WINDOW = 8, 512, 1024, 512, 10
HALF = WINDOW // 2


def draw0():
    s, t = mx_kscale(D), mx_kscale(E)
    x = bf(np.random.standard_normal((B, S, D)) * s)
    Wq = np.random.standard_normal((E, D)) / np.sqrt(D) / s[None, :] * t[:, None]
    words, scales = pack4(Wq.T)
    return {"x": x,
            "Wq_words": words,
            "Wq_scales": scales,
            "bq": bf(np.random.standard_normal(E) * 0.1 * t),
            "k": bf(np.random.standard_normal((B, S, E)) / t)}


def core(x, Wq_words, Wq_scales, bq, k):
    q = (mxq(f64(x), 2, "e4m3") @ unpack4(Wq_words, Wq_scales)) + f64(bq)
    scores = (mxq(q, 2, "e4m3") @ mxq(f64(k), 2, "e4m3").transpose(0, 2, 1)) / np.sqrt(E)
    i = np.arange(S)[:, None]
    j = np.arange(S)[None, :]
    mask = np.abs(i - j) <= HALF
    scores = np.where(mask[None, :, :], scores, -1e9)
    e = np.exp(scores - scores.max(-1, keepdims=True))
    return e / e.sum(-1, keepdims=True)


def e4m3fn_bytes(y):
    return np.clip(np.asarray(y, np.float64), -448.0, 448.0).astype(np.float32).astype(ml_dtypes.float8_e4m3fn).view(np.uint8)


def e4m3fn_values(b):
    return np.asarray(b, np.uint8).view(ml_dtypes.float8_e4m3fn).astype(np.float64)


def setup_inputs():
    d = draw0()
    x0 = np.asarray(d['x']).astype(np.float64)
    s = (np.max(np.abs(x0), axis=(0, 1), keepdims=True) / 448.0).astype(np.float32)
    out = {}
    for k, v in d.items():
        if k == 'x':
            out['x_bytes'] = e4m3fn_bytes(x0 / s.astype(np.float64))
            out['x_scale'] = s
        else:
            out[k] = v
    return out


def reference(x_bytes, x_scale, Wq_words, Wq_scales, bq, k):
    return core(e4m3fn_values(x_bytes) * x_scale.astype(np.float64), Wq_words, Wq_scales, bq, k)

@@ -1,0 +1,278 @@
+import math
+from contextlib import ExitStack
+
+import concourse.mybir as mybir
+from concourse.masks import make_identity
+
+B, S, D, E = 8, 512, 1024, 512
+HALF = 5
+FLOPS = 2 * B * S * D * E + 2 * B * S * S * E
+
+F32 = mybir.dt.float32
+BF16 = mybir.dt.bfloat16
+I32 = mybir.dt.int32
+U32 = mybir.dt.uint32
+U8 = mybir.dt.uint8
+FP8 = mybir.dt.float8_e4m3fn
+FP8X4 = mybir.dt.float8_e4m3fn_x4
+FP4X4 = mybir.dt.float4_e2m1fn_x4
+ALU = mybir.AluOpType
+ACT = mybir.ActivationFunctionType
+AX = mybir.AxisListType
+
+P = 128
+NT = S // P
+BAND = P + 2 * HALF
+EDGE = P + HALF
+KEYS = 256
+SCALE = 1.0 / math.sqrt(E)
+
+
+def tile_localattention_pa_t_w4_kernel(tc, x_bytes, x_scale, Wq_words, Wq_scales, bq, k, out):
+    nc = tc.nc
+    with ExitStack() as ctx:
+        keep = ctx.enter_context(tc.tile_pool(name="keep", bufs=1))
+        load = ctx.enter_context(tc.tile_pool(name="load", bufs=8))
+        work = ctx.enter_context(tc.tile_pool(name="work", bufs=2))
+        psum = ctx.enter_context(tc.psum_pool(name="psum", bufs=3))
+
+        ident = keep.tile([P, P], F32, name="ident")
+        scale_b = keep.tile([P, D], F32, name="scale_b", align_bytes=64)
+        w_raw = keep.tile([P, 2, 2 * E], U8, name="w_raw", align_bytes=64)
+        w_perm = keep.tile([P, 2, 2 * E], U8, name="w_perm", align_bytes=64)
+        ws_raw = keep.tile([P, 2, E], U8, name="ws_raw", align_bytes=64)
+        ws_perm = keep.tile([P, 2, E], U8, name="ws_perm", align_bytes=64)
+        bias = keep.tile([P, 4], BF16, name="bias")
+        mask_in = keep.tile([P, 2, BAND], F32, name="mask_in")
+        mask_edge = keep.tile([P, 2, EDGE], F32, name="mask_edge")
+        warm = keep.tile([P, 1], F32, name="warm")
+        stages = [keep.tile([P, NT, S], F32, name=f"stage{i}") for i in range(3)]
+
+        x_tiles = [load.tile([P, NT, D], U8, name="x_codes", align_bytes=64) for b in range(B)]
+        k_tiles = [load.tile([P, NT, E], BF16, name="k_rows", align_bytes=64) for b in range(B)]
+
+        xs = x_scale.rearrange("a b k -> (a b k)")
+        xv = x_bytes.rearrange("b (i p) k -> b p i k", p=P)
+        kv = k.rearrange("b (i p) e -> b p i e", p=P)
+        ov = out.rearrange("b (i p) j -> b p i j", p=P)
+
+        nc.sync.dma_start(out=x_tiles[0][:, 0, :], in_=xv[0][:, 0, :])
+        nc.scalar.dma_start(out=scale_b[:, 0:512], in_=xs[0:512].partition_broadcast(P))
+        nc.scalar.dma_start(out=scale_b[:, 512:1024], in_=xs[512:1024].partition_broadcast(P))
+        nc.scalar.dma_start(out=bias[:], in_=bq.rearrange("(p t) -> p t", t=4))
+        nc.gpsimd.memset(ws_raw[:].rearrange("p g n -> p (g n)").bitcast(I32), 0)
+        nc.sync.dma_start(out=w_raw[:], in_=Wq_words.rearrange("g p n -> p g n"))
+        nc.sync.dma_start(out=x_tiles[0][:, 1:4, :], in_=xv[0][:, 1:4, :])
+        nc.sync.dma_start(out=k_tiles[0][:], in_=kv[0])
+        for q in range(4):
+            nc.sync.dma_start(
+                out=ws_raw[32 * q : 32 * q + 4].bitcast(I32),
+                in_=Wq_scales[:, 4 * q : 4 * q + 4, :].rearrange("g r n -> r g n").bitcast(I32),
+            )
+        for b in range(1, B):
+            nc.sync.dma_start(out=x_tiles[b][:], in_=xv[b])
+            nc.sync.dma_start(out=k_tiles[b][:], in_=kv[b])
+
+        make_identity(nc, ident[:])
+        nc.vector.memset(warm[:], 0.0)
+        nc.scalar.activation(out=warm[:], in_=warm[:], func=ACT.Exp)
+        nc.vector.memset(stages[0][:], 0.0)
+        nc.gpsimd.memset(mask_in[:], 0.0)
+        m0 = mask_in[:, 0, :]
+        nc.gpsimd.affine_select(out=m0, in_=m0, pattern=[[1, BAND]], compare_op=ALU.is_ge, fill=-1e9, base=0, channel_multiplier=-1)
+        nc.gpsimd.affine_select(out=m0, in_=m0, pattern=[[-1, BAND]], compare_op=ALU.is_ge, fill=-1e9, base=2 * HALF, channel_multiplier=1)
+        nc.gpsimd.tensor_copy(out=mask_in[:, 1, :], in_=mask_in[:, 0, :])
+        nc.gpsimd.tensor_copy(out=mask_edge[:, 0, :], in_=mask_in[:, 0, 0:EDGE])
+        nc.gpsimd.tensor_copy(out=mask_edge[:, 1, :], in_=mask_in[:, 0, HALF:BAND])
+        nc.gpsimd.memset(stages[1][:], 0.0)
+        nc.gpsimd.memset(stages[2][:], 0.0)
+
+        xi, xc, xsc, kc, ksc, qp, qi, qc, qsc, xw, kt = {}, {}, {}, {}, {}, {}, {}, {}, {}, {}, {}
+        sm, st = {}, {}
+
+        def widen(u, i):
+            w = work.tile([P, D], BF16, name="xw", bufs=4, align_bytes=64)
+            xw[u, i] = w
+            halves = 2 if (u, i) == (0, 0) else 1
+            n = D // halves
+            for h in range(halves):
+                nc.vector.tensor_tensor(
+                    out=w[:, n * h : n * (h + 1)],
+                    in0=x_tiles[u][:, i, n * h : n * (h + 1)].bitcast(FP8),
+                    in1=scale_b[:, n * h : n * (h + 1)],
+                    op=ALU.mult,
+                )
+
+        def xpose(u, i):
+            if i == 0:
+                xi[u] = work.tile([P, 2, S, 2], F32, name="xi", align_bytes=64)
+            words = xw[u, i][:].bitcast(F32)
+            tp = psum.tile([P, 2, 2, P], F32, name="tp")
+            for g in range(2):
+                for h in range(2):
+                    nc.tensor.transpose(tp[:, g, h, :], words[:, 256 * g + h : 256 * (g + 1) : 2], ident[:])
+            nc.scalar.copy(out=xi[u][:, :, P * i : P * (i + 1), :], in_=tp[:].rearrange("p g h r -> p g r h"))
+
+        def quant_x(u):
+            xc[u] = work.tile([P, 2, S], U32, name="xc", align_bytes=64)
+            xsc[u] = work.tile([P, 2, S], U8, name="xsc", align_bytes=64)
+            for g in range(2):
+                nc.vector.quantize_mx(
+                    out=xc[u][:, g, :].bitcast(FP8X4),
+                    scales=xsc[u][:, g, :],
+                    in_=xi[u][:, g].rearrange("p n h -> p (n h)").bitcast(BF16),
+                )
+
+        def kpose(b, half):
+            if half == 0:
+                kt[b] = work.tile([P, S, 2], F32, name="kt", align_bytes=64)
+            tp = psum.tile([P, 2, 2, P], F32, name="tp")
+            for j in range(2):
+                words = k_tiles[b][:, 2 * half + j, :].bitcast(F32)
+                for h in range(2):
+                    nc.tensor.transpose(tp[:, j, h, :], words[:, h:256:2], ident[:])
+            dst = kt[b][:, 256 * half : 256 * (half + 1), :].rearrange("p (j r) h -> p j r h", j=2)
+            nc.scalar.copy(out=dst, in_=tp[:].rearrange("p j h r -> p j r h"))
+
+        def quant_k(b):
+            kc[b] = work.tile([P, S], U32, name="kc", bufs=3, align_bytes=64)
+            ksc[b] = work.tile([P, S], U8, name="ksc", bufs=3, align_bytes=64)
+            nc.vector.quantize_mx(
+                out=kc[b][:].bitcast(FP8X4),
+                scales=ksc[b][:],
+                in_=kt[b][:].rearrange("p n h -> p (n h)").bitcast(BF16),
+            )
+
+        def project(u, t):
+            if t == 0:
+                qp[u] = work.tile([P, 2, S], F32, name="qp", align_bytes=64)
+            acc = psum.tile([P, S], F32, name="acc")
+            for g in range(2):
+                nc.tensor.matmul_mx(
+                    out=acc[:],
+                    lhsT=w_perm[:, g, 256 * t : 256 * (t + 1)].bitcast(FP4X4),
+                    lhsT_scale=ws_perm[:, g, P * t : P * (t + 1)],
+                    rhs=xc[u][:, g, :].bitcast(FP8X4),
+                    rhs_scale=xsc[u][:, g, :],
+                    start=(g == 0),
+                    stop=(g == 1),
+                )
+            pair = qp[u][:, t // 2, :].bitcast(BF16)
+            nc.scalar.activation(out=pair[:, t % 2 :: 2], in_=acc[:], func=ACT.Identity, bias=bias[:, t : t + 1])
+
+        def interleave(u):
+            qi[u] = work.tile([P, S, 2], F32, name="qi", align_bytes=64)
+            nc.vector.tensor_copy(out=qi[u][:], in_=qp[u][:].rearrange("p h n -> p n h"))
+
+        def quant_q(u):
+            qc[u] = work.tile([P, S], U32, name="qc", align_bytes=64)
+            qsc[u] = work.tile([P, S], U8, name="qsc", align_bytes=64)
+            nc.vector.quantize_mx(
+                out=qc[u][:].bitcast(FP8X4),
+                scales=qsc[u][:],
+                in_=qi[u][:].rearrange("p n h -> p (n h)").bitcast(BF16),
+            )
+
+        PAIRS = (((1, 64), (2, 192)), ((3, 256), (0, 0)))
+
+        def scores(u, pair):
+            sc = psum.tile([P, 2, KEYS], F32, name="sc", bufs=2)
+            for h in range(2):
+                i, j0 = PAIRS[pair][h]
+                nc.tensor.matmul_mx(
+                    out=sc[:, h, :],
+                    lhsT=qc[u][:, P * i : P * (i + 1)].bitcast(FP8X4),
+                    lhsT_scale=qsc[u][:, P * i : P * (i + 1)],
+                    rhs=kc[u][:, j0 : j0 + KEYS].bitcast(FP8X4),
+                    rhs_scale=ksc[u][:, j0 : j0 + KEYS],
+                    start=True,
+                    stop=True,
+                )
+            if pair == 0:
+                width = BAND
+                m = work.tile([P, 2, BAND], F32, name="m0", bufs=3)
+                src, dst, msk = sc[:, :, 59 : 59 + BAND], m[:], mask_in[:]
+            else:
+                width = EDGE
+                m = work.tile([P, 2, EDGE], F32, name="m1", bufs=3)
+                src = sc[:].rearrange("p h j -> p (h j)")[:, 256 - EDGE : 256 + EDGE]
+                dst, msk = m[:].rearrange("p h j -> p (h j)"), mask_edge[:].rearrange("p h j -> p (h j)")
+            nc.vector.scalar_tensor_tensor(out=dst, in0=src, scalar=SCALE, in1=msk, op0=ALU.mult, op1=ALU.add)
+            nm = work.tile([P, 2], F32, name="nm", bufs=4)
+            sm[u, pair] = (m, nm)
+
+        def rowmax(u, pair):
+            m, nm = sm[u, pair]
+            nc.vector.tensor_reduce(out=nm[:], in_=m[:], axis=AX.X, op=ALU.max, negate=True)
+
+        def exps(u, pair):
+            m, nm = sm[u, pair]
+            ss = work.tile([P, 2], F32, name="ss", bufs=4)
+            for h in range(2):
+                nc.scalar.activation(out=m[:, h, :], in_=m[:, h, :], func=ACT.Exp, bias=nm[:, h : h + 1], accum_out=ss[:, h : h + 1])
+            st[u, pair] = ss
+
+        def finish(u, pair):
+            m, nm = sm[u, pair]
+            rs = work.tile([P, 2], F32, name="rs", bufs=4)
+            nc.vector.reciprocal(out=rs[:], in_=st[u, pair][:])
+            stage = stages[u % 3]
+            for h in range(2):
+                i = PAIRS[pair][h][0]
+                lo = max(0, P * i - HALF)
+                hi = min(S, P * (i + 1) + HALF)
+                nc.scalar.activation(out=stage[:, i, lo:hi], in_=m[:, h, :], func=ACT.Copy, scale=rs[:, h : h + 1])
+            tiles = slice(1, 3) if pair == 0 else slice(0, 4, 3)
+            nc.sync.dma_start(out=ov[u][:, tiles, :], in_=stage[:, tiles, :])
+
+        for s in range(B + 2):
+            new, mid, old = s < B, 0 <= s - 1 < B, 0 <= s - 2 < B
+            if new:
+                widen(s, 0)
+                xpose(s, 0)
+            if mid:
+                quant_x(s - 1)
+                project(s - 1, 0)
+                project(s - 1, 1)
+            if old:
+                scores(s - 2, 0)
+            if new:
+                widen(s, 1)
+                xpose(s, 1)
+            if old:
+                rowmax(s - 2, 0)
+                exps(s - 2, 0)
+                scores(s - 2, 1)
+            if mid:
+                project(s - 1, 2)
+                project(s - 1, 3)
+            if new:
+                kpose(s, 0)
+                widen(s, 2)
+                xpose(s, 2)
+            if s == 0:
+                for g in range(2):
+                    nc.vector.tensor_copy(
+                        out=w_perm[:, g, :].rearrange("p (t m c) -> p m t c", t=4, c=2),
+                        in_=w_raw[:, g, :].rearrange("p (m t c) -> p m t c", t=4, c=2),
+                    )
+                    nc.vector.tensor_copy(
+                        out=ws_perm[:, g, :].rearrange("p (t m) -> p m t", t=4),
+                        in_=ws_raw[:, g, :].rearrange("p (m t) -> p m t", t=4),
+                    )
+            if old:
+                rowmax(s - 2, 1)
+                finish(s - 2, 0)
+                exps(s - 2, 1)
+            if new:
+                kpose(s, 1)
+            if mid:
+                interleave(s - 1)
+            if new:
+                widen(s, 3)
+                xpose(s, 3)
+                quant_k(s)
+            if old:
+                finish(s - 2, 1)
+            if mid:
+                quant_q(s - 1)

@@ -22,9 +22,12 @@ AX = mybir.AxisListType
 
 P = 128
 NT = S // P
-BAND = P + 2 * HALF
-EDGE = P + HALF
-KEYS = 256
+G = D // 512
+Q = 64
+SHIFT = 32
+MARGIN = 8
+STRIP = Q + 2 * MARGIN
+MASKED = -1e9
 SCALE = 1.0 / math.sqrt(E)
 
 
@@ -32,247 +35,435 @@ def tile_localattention_pa_t_w4_kernel(tc, x_bytes, x_scale, Wq_words, Wq_scales
     nc = tc.nc
     with ExitStack() as ctx:
         keep = ctx.enter_context(tc.tile_pool(name="keep", bufs=1))
-        load = ctx.enter_context(tc.tile_pool(name="load", bufs=8))
         work = ctx.enter_context(tc.tile_pool(name="work", bufs=2))
-        psum = ctx.enter_context(tc.psum_pool(name="psum", bufs=3))
+        psum = ctx.enter_context(tc.psum_pool(name="psum", bufs=1))
+        ctx.enter_context(tc.manual_schedule())
 
         ident = keep.tile([P, P], F32, name="ident")
+        scale_p = keep.tile([P, G, 4], F32, name="scale_p")
         scale_b = keep.tile([P, D], F32, name="scale_b", align_bytes=64)
-        w_raw = keep.tile([P, 2, 2 * E], U8, name="w_raw", align_bytes=64)
-        w_perm = keep.tile([P, 2, 2 * E], U8, name="w_perm", align_bytes=64)
-        ws_raw = keep.tile([P, 2, E], U8, name="ws_raw", align_bytes=64)
-        ws_perm = keep.tile([P, 2, E], U8, name="ws_perm", align_bytes=64)
+        w_raw = keep.tile([P, G, 2 * E], U8, name="w_raw", align_bytes=64)
+        w_perm = keep.tile([P, G, 2 * E], U8, name="w_perm", align_bytes=64)
+        ws_raw = keep.tile([P, G, E], U8, name="ws_raw", align_bytes=64)
+        ws_perm = keep.tile([P, G, E], U8, name="ws_perm", align_bytes=64)
         bias = keep.tile([P, 4], BF16, name="bias")
-        mask_in = keep.tile([P, 2, BAND], F32, name="mask_in")
-        mask_edge = keep.tile([P, 2, EDGE], F32, name="mask_edge")
-        warm = keep.tile([P, 1], F32, name="warm")
-        stages = [keep.tile([P, NT, S], F32, name=f"stage{i}") for i in range(3)]
+        band = keep.tile([P, Q + STRIP], F32, name="band")
+        mask = keep.tile([P, NT, STRIP], F32, name="mask")
+        zeros = keep.tile([P, 2 * S], F32, name="zeros")
+        kc = keep.tile([P, B * S + Q], U32, name="kc", align_bytes=64)
+        ksc = keep.tile([P, B * S + Q], U8, name="ksc", align_bytes=64)
+        qc = [keep.tile([P, NT * 3 * Q], U32, name=f"qc{j}", align_bytes=64) for j in range(2)]
+        qsc = [keep.tile([P, NT * 3 * Q], U8, name=f"qsc{j}", align_bytes=64) for j in range(2)]
 
-        x_tiles = [load.tile([P, NT, D], U8, name="x_codes", align_bytes=64) for b in range(B)]
-        k_tiles = [load.tile([P, NT, E], BF16, name="k_rows", align_bytes=64) for b in range(B)]
+        x_first = keep.tile([P, D], U8, name="x_codes_first", align_bytes=64)
+        x_tiles = [keep.tile([P, NT, D], U8, name=f"x_codes{b}", align_bytes=64) for b in range(B)]
+        k_tiles = [keep.tile([P, NT, E], BF16, name=f"k_rows{b}", align_bytes=64) for b in range(B)]
 
-        xs = x_scale.rearrange("a b k -> (a b k)")
         xv = x_bytes.rearrange("b (i p) k -> b p i k", p=P)
-        kv = k.rearrange("b (i p) e -> b p i e", p=P)
-        ov = out.rearrange("b (i p) j -> b p i j", p=P)
+        kflat = k.rearrange("b s e -> (b s) e")
+        oflat = out.rearrange("b s j -> b (s j)")
 
-        nc.sync.dma_start(out=x_tiles[0][:, 0, :], in_=xv[0][:, 0, :])
-        nc.scalar.dma_start(out=scale_b[:, 0:512], in_=xs[0:512].partition_broadcast(P))
-        nc.scalar.dma_start(out=scale_b[:, 512:1024], in_=xs[512:1024].partition_broadcast(P))
-        nc.scalar.dma_start(out=bias[:], in_=bq.rearrange("(p t) -> p t", t=4))
-        nc.gpsimd.memset(ws_raw[:].rearrange("p g n -> p (g n)").bitcast(I32), 0)
-        nc.sync.dma_start(out=w_raw[:], in_=Wq_words.rearrange("g p n -> p g n"))
-        nc.sync.dma_start(out=x_tiles[0][:, 1:4, :], in_=xv[0][:, 1:4, :])
-        nc.sync.dma_start(out=k_tiles[0][:], in_=kv[0])
+        def load_k(b):
+            rows = kflat[S * b - SHIFT : S * (b + 1) - SHIFT, :]
+            nc.sync.dma_start(out=k_tiles[b][:], in_=rows.rearrange("(i p) e -> p i e", p=P))
+
+        nc.vector.memset(ws_raw[:].rearrange("p g n -> p (g n)").bitcast(I32), 0)
+        nc.sync.dma_start(out=scale_p[:], in_=x_scale.rearrange("a b (g p c) -> p (a b g) c", p=P, c=4))
+        nc.sync.dma_start(out=w_raw[:].bitcast(I32), in_=Wq_words.rearrange("g p n -> p g n").bitcast(I32))
+        nc.sync.dma_start(out=x_first[:], in_=xv[0][:, 0, :])
+        nc.sync.dma_start(out=x_tiles[0][:, 1:NT, :], in_=xv[0][:, 1:NT, :])
         for q in range(4):
             nc.sync.dma_start(
                 out=ws_raw[32 * q : 32 * q + 4].bitcast(I32),
                 in_=Wq_scales[:, 4 * q : 4 * q + 4, :].rearrange("g r n -> r g n").bitcast(I32),
             )
-        for b in range(1, B):
+        nc.sync.dma_start(out=k_tiles[0][0:SHIFT, 0, :], in_=kflat[B * S - SHIFT : B * S, :])
+        nc.sync.dma_start(out=k_tiles[0][SHIFT:P, 0, :], in_=kflat[0 : P - SHIFT, :])
+        nc.sync.dma_start(
+            out=k_tiles[0][:, 1:NT, :], in_=kflat[P - SHIFT : S - SHIFT, :].rearrange("(i p) e -> p i e", p=P)
+        )
+        load_k(1)
+        nc.sync.dma_start(out=x_tiles[1][:], in_=xv[1])
+        nc.sync.dma_start(out=bias[:], in_=bq.rearrange("(p t) -> p t", t=4))
+        load_k(2)
+        for b in range(2, B):
             nc.sync.dma_start(out=x_tiles[b][:], in_=xv[b])
-            nc.sync.dma_start(out=k_tiles[b][:], in_=kv[b])
+            if b + 1 < B:
+                load_k(b + 1)
 
         make_identity(nc, ident[:])
-        nc.vector.memset(warm[:], 0.0)
-        nc.scalar.activation(out=warm[:], in_=warm[:], func=ACT.Exp)
-        nc.vector.memset(stages[0][:], 0.0)
-        nc.gpsimd.memset(mask_in[:], 0.0)
-        m0 = mask_in[:, 0, :]
-        nc.gpsimd.affine_select(out=m0, in_=m0, pattern=[[1, BAND]], compare_op=ALU.is_ge, fill=-1e9, base=0, channel_multiplier=-1)
-        nc.gpsimd.affine_select(out=m0, in_=m0, pattern=[[-1, BAND]], compare_op=ALU.is_ge, fill=-1e9, base=2 * HALF, channel_multiplier=1)
-        nc.gpsimd.tensor_copy(out=mask_in[:, 1, :], in_=mask_in[:, 0, :])
-        nc.gpsimd.tensor_copy(out=mask_edge[:, 0, :], in_=mask_in[:, 0, 0:EDGE])
-        nc.gpsimd.tensor_copy(out=mask_edge[:, 1, :], in_=mask_in[:, 0, HALF:BAND])
-        nc.gpsimd.memset(stages[1][:], 0.0)
-        nc.gpsimd.memset(stages[2][:], 0.0)
+        for j in range(2):
+            nc.vector.memset(qc[j][:].bitcast(I32).rearrange("p (i u n) -> p i u n", i=NT, u=3)[:, :, 1, :], 0)
+            nc.vector.memset(qsc[j][:].bitcast(I32).rearrange("p (i u n) -> p i u n", i=NT, u=3)[:, :, 1, :], 0)
+        nc.vector.memset(zeros[:], 0.0)
+        for b in range(B):
+            nc.sync.dma_start(
+                out=oflat[b].rearrange("(p r n) -> p r n", p=P, r=2), in_=zeros[:].unsqueeze(1).to_broadcast([P, 2, 2 * S])
+            )
 
-        xi, xc, xsc, kc, ksc, qp, qi, qc, qsc, xw, kt = {}, {}, {}, {}, {}, {}, {}, {}, {}, {}, {}
-        sm, st = {}, {}
+        nc.gpsimd.memset(band[:], 0.0)
+        nc.gpsimd.affine_select(
+            out=band[:], in_=band[:], pattern=[[1, Q + STRIP]], compare_op=ALU.is_ge, fill=MASKED,
+            base=HALF - MARGIN, channel_multiplier=-1,
+        )
+        nc.gpsimd.affine_select(
+            out=band[:], in_=band[:], pattern=[[-1, Q + STRIP]], compare_op=ALU.is_ge, fill=MASKED,
+            base=HALF + MARGIN, channel_multiplier=1,
+        )
 
-        def widen(u, i):
-            w = work.tile([P, D], BF16, name="xw", bufs=4, align_bytes=64)
-            xw[u, i] = w
-            halves = 2 if (u, i) == (0, 0) else 1
-            n = D // halves
-            for h in range(halves):
-                nc.vector.tensor_tensor(
-                    out=w[:, n * h : n * (h + 1)],
-                    in0=x_tiles[u][:, i, n * h : n * (h + 1)].bitcast(FP8),
-                    in1=scale_b[:, n * h : n * (h + 1)],
-                    op=ALU.mult,
-                )
+        def build_mask():
+            for s in range(2):
+                rows = slice(Q * s, Q * (s + 1))
+                nc.scalar.copy(out=mask[rows], in_=band[rows, Q * s : Q * s + STRIP].unsqueeze(1).to_broadcast([Q, NT, STRIP]))
+            nc.scalar.copy(out=mask[0:Q, 0, 0:MARGIN], in_=band[0:Q, Q + STRIP - MARGIN : Q + STRIP])
+            nc.scalar.copy(out=mask[Q:P, NT - 1, STRIP - MARGIN : STRIP], in_=band[Q:P, 0:MARGIN])
 
-        def xpose(u, i):
-            if i == 0:
-                xi[u] = work.tile([P, 2, S, 2], F32, name="xi", align_bytes=64)
-            words = xw[u, i][:].bitcast(F32)
-            tp = psum.tile([P, 2, 2, P], F32, name="tp")
-            for g in range(2):
+        xw, xt, xi, xc, xsc, kt, ktp, acc, qp, qi = {}, {}, {}, {}, {}, {}, {}, {}, {}, {}
+        sc, sm, nm, ss, rs = {}, {}, {}, {}, {}
+
+        def permute_codes():
+            nc.vector.tensor_copy(
+                out=w_perm[:].rearrange("p g (t m c) -> p g t m c", t=4, c=2),
+                in_=w_raw[:].rearrange("p g (m t c) -> p g t m c", t=4, c=2),
+            )
+
+        def permute_scales():
+            nc.vector.tensor_copy(
+                out=ws_perm[:].rearrange("p g (t m) -> p g t m", t=4),
+                in_=ws_raw[:].rearrange("p g (m t) -> p g t m", t=4),
+            )
+
+        def spread_scale(g):
+            bank = psum.tile([P, 4, P], F32, name="tp", bufs=4)
+            for c in range(4):
+                nc.tensor.transpose(bank[:, c, :], scale_p[:, g, c : c + 1].to_broadcast([P, P]), ident[:])
+            dst = scale_b[:, 512 * g : 512 * (g + 1)].rearrange("m (p c) -> m p c", c=4)
+            nc.scalar.activation(out=dst, in_=bank[:].rearrange("m c p -> m p c"), func=ACT.Copy)
+
+        def widen(b, i):
+            xw[b, i] = work.tile([P, D], BF16, name="xw", bufs=4, align_bytes=64)
+            codes = x_first[:] if (b, i) == (0, 0) else x_tiles[b][:, i, :]
+            parts = G if (b, i) == (0, 0) else 1
+            for h in range(parts):
+                cols = slice(D // parts * h, D // parts * (h + 1))
+                nc.vector.tensor_tensor(out=xw[b, i][:, cols], in0=codes[:, cols].bitcast(FP8), in1=scale_b[:, cols], op=ALU.mult)
+
+        def turn_x(b, i):
+            words = xw[b, i][:].bitcast(F32)
+            xt[b, i] = psum.tile([P, G, 2, P], F32, name="tp", bufs=4)
+            for g in range(G):
                 for h in range(2):
-                    nc.tensor.transpose(tp[:, g, h, :], words[:, 256 * g + h : 256 * (g + 1) : 2], ident[:])
-            nc.scalar.copy(out=xi[u][:, :, P * i : P * (i + 1), :], in_=tp[:].rearrange("p g h r -> p g r h"))
+                    nc.tensor.transpose(xt[b, i][:, g, h, :], words[:, 256 * g + h : 256 * (g + 1) : 2], ident[:])
 
-        def quant_x(u):
-            xc[u] = work.tile([P, 2, S], U32, name="xc", align_bytes=64)
-            xsc[u] = work.tile([P, 2, S], U8, name="xsc", align_bytes=64)
-            for g in range(2):
+        def empty_x(b, i):
+            if i == 0:
+                xi[b] = work.tile([P, G, S, 2], F32, name="xi", align_bytes=64)
+            nc.scalar.copy(out=xi[b][:, :, P * i : P * (i + 1), :], in_=xt[b, i][:].rearrange("p g h r -> p g r h"))
+
+        def quant_x(b):
+            xc[b] = work.tile([P, G, S], U32, name="xc", align_bytes=64)
+            xsc[b] = work.tile([P, G, S], U8, name="xsc", align_bytes=64)
+            for g in range(G):
                 nc.vector.quantize_mx(
-                    out=xc[u][:, g, :].bitcast(FP8X4),
-                    scales=xsc[u][:, g, :],
-                    in_=xi[u][:, g].rearrange("p n h -> p (n h)").bitcast(BF16),
+                    out=xc[b][:, g, :].bitcast(FP8X4),
+                    scales=xsc[b][:, g, :],
+                    in_=xi[b][:, g].rearrange("p n h -> p (n h)").bitcast(BF16),
                 )
 
-        def kpose(b, half):
-            if half == 0:
-                kt[b] = work.tile([P, S, 2], F32, name="kt", align_bytes=64)
-            tp = psum.tile([P, 2, 2, P], F32, name="tp")
+        def turn_k(b, half):
+            ktp[b, half] = psum.tile([P, 2, 2, P], F32, name="tp", bufs=4)
             for j in range(2):
                 words = k_tiles[b][:, 2 * half + j, :].bitcast(F32)
                 for h in range(2):
-                    nc.tensor.transpose(tp[:, j, h, :], words[:, h:256:2], ident[:])
+                    nc.tensor.transpose(ktp[b, half][:, j, h, :], words[:, h:256:2], ident[:])
+
+        def empty_k(b, half):
+            if half == 0:
+                kt[b] = work.tile([P, S, 2], F32, name="kt", bufs=3, align_bytes=64)
             dst = kt[b][:, 256 * half : 256 * (half + 1), :].rearrange("p (j r) h -> p j r h", j=2)
-            nc.scalar.copy(out=dst, in_=tp[:].rearrange("p j h r -> p j r h"))
+            nc.scalar.copy(out=dst, in_=ktp[b, half][:].rearrange("p j h r -> p j r h"))
 
         def quant_k(b):
-            kc[b] = work.tile([P, S], U32, name="kc", bufs=3, align_bytes=64)
-            ksc[b] = work.tile([P, S], U8, name="ksc", bufs=3, align_bytes=64)
-            nc.vector.quantize_mx(
-                out=kc[b][:].bitcast(FP8X4),
-                scales=ksc[b][:],
-                in_=kt[b][:].rearrange("p n h -> p (n h)").bitcast(BF16),
-            )
+            rows = kt[b][:].rearrange("p n h -> p (n h)").bitcast(BF16)
+            nc.vector.quantize_mx(out=kc[:, S * b : S * (b + 1)].bitcast(FP8X4), scales=ksc[:, S * b : S * (b + 1)], in_=rows)
+            if b == 0:
+                nc.vector.quantize_mx(out=kc[:, B * S :].bitcast(FP8X4), scales=ksc[:, B * S :], in_=rows[:, 0 : 4 * Q])
 
-        def project(u, t):
-            if t == 0:
-                qp[u] = work.tile([P, 2, S], F32, name="qp", align_bytes=64)
-            acc = psum.tile([P, S], F32, name="acc")
-            for g in range(2):
+        def project(b, t):
+            acc[b, t] = psum.tile([P, S], F32, name="acc", bufs=3)
+            for g in range(G):
                 nc.tensor.matmul_mx(
-                    out=acc[:],
+                    out=acc[b, t][:],
                     lhsT=w_perm[:, g, 256 * t : 256 * (t + 1)].bitcast(FP4X4),
                     lhsT_scale=ws_perm[:, g, P * t : P * (t + 1)],
-                    rhs=xc[u][:, g, :].bitcast(FP8X4),
-                    rhs_scale=xsc[u][:, g, :],
+                    rhs=xc[b][:, g, :].bitcast(FP8X4),
+                    rhs_scale=xsc[b][:, g, :],
                     start=(g == 0),
-                    stop=(g == 1),
+                    stop=(g == G - 1),
                 )
-            pair = qp[u][:, t // 2, :].bitcast(BF16)
-            nc.scalar.activation(out=pair[:, t % 2 :: 2], in_=acc[:], func=ACT.Identity, bias=bias[:, t : t + 1])
 
-        def interleave(u):
-            qi[u] = work.tile([P, S, 2], F32, name="qi", align_bytes=64)
-            nc.vector.tensor_copy(out=qi[u][:], in_=qp[u][:].rearrange("p h n -> p n h"))
+        def empty_q(b, t):
+            if t == 0:
+                qp[b] = work.tile([P, 2, S], F32, name="qp", align_bytes=64)
+            pair = qp[b][:, t // 2, :].bitcast(BF16)
+            nc.scalar.activation(out=pair[:, t % 2 :: 2], in_=acc[b, t][:], func=ACT.Identity, bias=bias[:, t : t + 1])
 
-        def quant_q(u):
-            qc[u] = work.tile([P, S], U32, name="qc", align_bytes=64)
-            qsc[u] = work.tile([P, S], U8, name="qsc", align_bytes=64)
-            nc.vector.quantize_mx(
-                out=qc[u][:].bitcast(FP8X4),
-                scales=qsc[u][:],
-                in_=qi[u][:].rearrange("p n h -> p (n h)").bitcast(BF16),
+        def weave_q(b, cut=0):
+            qi[b] = work.tile([P, S, 2], F32, name="qi", align_bytes=64)
+            pairs = qp[b][:].rearrange("p h n -> p n h")
+            if cut > 0:
+                nc.scalar.copy(out=qi[b][:, 0:cut], in_=pairs[:, 0:cut])
+            if cut < S:
+                nc.vector.tensor_copy(out=qi[b][:, cut:S], in_=pairs[:, cut:S])
+
+        def quant_q(b):
+            rows = qi[b][:].rearrange("p n h -> p (n h)").bitcast(BF16)
+            cuts = [0] + list(range(Q, S, P)) + [S]
+            for lo, hi in zip(cuts[:-1], cuts[1:]):
+                at = lo + Q * ((lo // Q + 1) // 2)
+                cols = slice(at, at + hi - lo)
+                nc.vector.quantize_mx(out=qc[b % 2][:, cols].bitcast(FP8X4), scales=qsc[b % 2][:, cols], in_=rows[:, 4 * lo : 4 * hi])
+
+        def scores(b, i0=0, n=NT, tag="sc", bufs=1):
+            sc[b, i0] = psum.tile([P, n, P], F32, name=tag, bufs=bufs)
+            for i in range(i0, i0 + n):
+                for s in range(2):
+                    qcols = slice(Q * (3 * i + s), Q * (3 * i + s) + P)
+                    kcols = slice(S * b + P * i + Q * s, S * b + P * i + Q * s + P)
+                    nc.tensor.matmul_mx(
+                        out=sc[b, i0][:, i - i0, :],
+                        lhsT=qc[b % 2][:, qcols].bitcast(FP8X4),
+                        lhsT_scale=qsc[b % 2][:, qcols],
+                        rhs=kc[:, kcols].bitcast(FP8X4),
+                        rhs_scale=ksc[:, kcols],
+                        start=(s == 0),
+                        stop=(s == 1),
+                    )
+
+        def mask_scores(b, i0=0, n=NT):
+            sm[b, i0] = work.tile([P, n, STRIP], F32, name="sm", bufs=4)
+            window = sc[b, i0][:, :, SHIFT - MARGIN : SHIFT - MARGIN + STRIP]
+            nc.vector.scalar_tensor_tensor(
+                out=sm[b, i0][:], in0=window, scalar=SCALE, in1=mask[:, i0 : i0 + n, :], op0=ALU.mult, op1=ALU.add
             )
 
-        PAIRS = (((1, 64), (2, 192)), ((3, 256), (0, 0)))
+        def row_max(b, i0=0, n=NT):
+            nm[b, i0] = work.tile([P, n], F32, name="nm", bufs=4)
+            nc.vector.tensor_reduce(out=nm[b, i0][:], in_=sm[b, i0][:], axis=AX.X, op=ALU.max, negate=True)
 
-        def scores(u, pair):
-            sc = psum.tile([P, 2, KEYS], F32, name="sc", bufs=2)
-            for h in range(2):
-                i, j0 = PAIRS[pair][h]
-                nc.tensor.matmul_mx(
-                    out=sc[:, h, :],
-                    lhsT=qc[u][:, P * i : P * (i + 1)].bitcast(FP8X4),
-                    lhsT_scale=qsc[u][:, P * i : P * (i + 1)],
-                    rhs=kc[u][:, j0 : j0 + KEYS].bitcast(FP8X4),
-                    rhs_scale=ksc[u][:, j0 : j0 + KEYS],
-                    start=True,
-                    stop=True,
+        def exps(b, i0=0, n=NT):
+            ss[b, i0] = work.tile([P, n], F32, name="ss", bufs=4)
+            for i in range(n):
+                row = sm[b, i0][:, i, :]
+                nc.scalar.activation(out=row, in_=row, func=ACT.Exp, bias=nm[b, i0][:, i : i + 1], accum_out=ss[b, i0][:, i : i + 1])
+
+        def recip(b, i0=0, n=NT):
+            rs[b, i0] = work.tile([P, n], F32, name="rs", bufs=4)
+            nc.vector.reciprocal(out=rs[b, i0][:], in_=ss[b, i0][:])
+
+        def strip_rows(b, i0, n, s):
+            diag = P * S + P
+            back = 2 * S
+            lo = diag * i0 + (Q * S + Q) * s - MARGIN - back
+            view = oflat[b][lo : lo + n * diag].rearrange("(i y) -> i y", i=n)[:, back : back + Q * S]
+            return view.rearrange("i (r j) -> r i j", r=Q)[:, :, 0:STRIP]
+
+        def store(b, strip, i0, n):
+            first, last = i0 == 0, i0 + n == NT
+            if first:
+                nc.sync.dma_start(out=out[b, 0:Q, 0 : STRIP - MARGIN], in_=strip[0:Q, 0, MARGIN:STRIP])
+            if n > first:
+                nc.sync.dma_start(out=strip_rows(b, i0 + first, n - first, 0), in_=strip[0:Q, first:n, :])
+            if n > last:
+                nc.sync.dma_start(out=strip_rows(b, i0, n - last, 1), in_=strip[Q:P, 0 : n - last, :])
+            if last:
+                nc.sync.dma_start(out=out[b, S - Q : S, S - STRIP + MARGIN : S], in_=strip[Q:P, n - 1, 0 : STRIP - MARGIN])
+
+        def finish(b, i0=0, n=NT):
+            strip = work.tile([P, n, STRIP], F32, name="strip", bufs=4)
+            for i in range(n):
+                nc.scalar.activation(out=strip[:, i, :], in_=sm[b, i0][:, i, :], func=ACT.Copy, scale=rs[b, i0][:, i : i + 1])
+            store(b, strip, i0, n)
+
+        L = B - 1
+        tx, tc_, ts, tacc, tq = {}, {}, {}, {}, {}
+
+        def t_empty_x(i):
+            tx[i] = work.tile([P, G, P, 2], F32, name="t_xi", bufs=4, align_bytes=64)
+            nc.scalar.copy(out=tx[i][:], in_=xt[L, i][:].rearrange("p g h r -> p g r h"))
+
+        def t_quant_x(i):
+            tc_[i] = work.tile([P, G * P], U32, name="t_xc", bufs=4, align_bytes=64)
+            ts[i] = work.tile([P, G * P], U8, name="t_xsc", bufs=4, align_bytes=64)
+            nc.vector.quantize_mx(
+                out=tc_[i][:].bitcast(FP8X4), scales=ts[i][:], in_=tx[i][:].rearrange("p g n h -> p (g n h)").bitcast(BF16)
+            )
+
+        def t_project(i):
+            tacc[i] = psum.tile([P, 4, P], F32, name="acc", bufs=3)
+            for t in range(4):
+                for g in range(G):
+                    nc.tensor.matmul_mx(
+                        out=tacc[i][:, t, :],
+                        lhsT=w_perm[:, g, 256 * t : 256 * (t + 1)].bitcast(FP4X4),
+                        lhsT_scale=ws_perm[:, g, P * t : P * (t + 1)],
+                        rhs=tc_[i][:, P * g : P * (g + 1)].bitcast(FP8X4),
+                        rhs_scale=ts[i][:, P * g : P * (g + 1)],
+                        start=(g == 0),
+                        stop=(g == G - 1),
+                    )
+
+        def t_empty_q(i):
+            tq[i] = work.tile([P, P, 4], BF16, name="t_qi", bufs=4, align_bytes=64)
+            nc.vector.tensor_tensor(
+                out=tq[i][:], in0=tacc[i][:].rearrange("p t n -> p n t"), in1=bias[:].unsqueeze(1).to_broadcast([P, P, 4]), op=ALU.add
+            )
+
+        def t_quant_q(i):
+            rows = tq[i][:].rearrange("p n t -> p (n t)")
+            for s in range(2):
+                cols = slice(Q * (3 * i + 2 * s), Q * (3 * i + 2 * s + 1))
+                nc.vector.quantize_mx(
+                    out=qc[L % 2][:, cols].bitcast(FP8X4), scales=qsc[L % 2][:, cols], in_=rows[:, 4 * Q * s : 4 * Q * (s + 1)]
                 )
-            if pair == 0:
-                width = BAND
-                m = work.tile([P, 2, BAND], F32, name="m0", bufs=3)
-                src, dst, msk = sc[:, :, 59 : 59 + BAND], m[:], mask_in[:]
-            else:
-                width = EDGE
-                m = work.tile([P, 2, EDGE], F32, name="m1", bufs=3)
-                src = sc[:].rearrange("p h j -> p (h j)")[:, 256 - EDGE : 256 + EDGE]
-                dst, msk = m[:].rearrange("p h j -> p (h j)"), mask_edge[:].rearrange("p h j -> p (h j)")
-            nc.vector.scalar_tensor_tensor(out=dst, in0=src, scalar=SCALE, in1=msk, op0=ALU.mult, op1=ALU.add)
-            nm = work.tile([P, 2], F32, name="nm", bufs=4)
-            sm[u, pair] = (m, nm)
 
-        def rowmax(u, pair):
-            m, nm = sm[u, pair]
-            nc.vector.tensor_reduce(out=nm[:], in_=m[:], axis=AX.X, op=ALU.max, negate=True)
+        def step(fn, b, *args):
+            if 0 <= b < B:
+                fn(b, *args)
 
-        def exps(u, pair):
-            m, nm = sm[u, pair]
-            ss = work.tile([P, 2], F32, name="ss", bufs=4)
-            for h in range(2):
-                nc.scalar.activation(out=m[:, h, :], in_=m[:, h, :], func=ACT.Exp, bias=nm[:, h : h + 1], accum_out=ss[:, h : h + 1])
-            st[u, pair] = ss
-
-        def finish(u, pair):
-            m, nm = sm[u, pair]
-            rs = work.tile([P, 2], F32, name="rs", bufs=4)
-            nc.vector.reciprocal(out=rs[:], in_=st[u, pair][:])
-            stage = stages[u % 3]
-            for h in range(2):
-                i = PAIRS[pair][h][0]
-                lo = max(0, P * i - HALF)
-                hi = min(S, P * (i + 1) + HALF)
-                nc.scalar.activation(out=stage[:, i, lo:hi], in_=m[:, h, :], func=ACT.Copy, scale=rs[:, h : h + 1])
-            tiles = slice(1, 3) if pair == 0 else slice(0, 4, 3)
-            nc.sync.dma_start(out=ov[u][:, tiles, :], in_=stage[:, tiles, :])
-
-        for s in range(B + 2):
-            new, mid, old = s < B, 0 <= s - 1 < B, 0 <= s - 2 < B
-            if new:
-                widen(s, 0)
-                xpose(s, 0)
-            if mid:
-                quant_x(s - 1)
-                project(s - 1, 0)
-                project(s - 1, 1)
-            if old:
-                scores(s - 2, 0)
-            if new:
-                widen(s, 1)
-                xpose(s, 1)
-            if old:
-                rowmax(s - 2, 0)
-                exps(s - 2, 0)
-                scores(s - 2, 1)
-            if mid:
-                project(s - 1, 2)
-                project(s - 1, 3)
-            if new:
-                kpose(s, 0)
-                widen(s, 2)
-                xpose(s, 2)
-            if s == 0:
-                for g in range(2):
-                    nc.vector.tensor_copy(
-                        out=w_perm[:, g, :].rearrange("p (t m c) -> p m t c", t=4, c=2),
-                        in_=w_raw[:, g, :].rearrange("p (m t c) -> p m t c", t=4, c=2),
-                    )
-                    nc.vector.tensor_copy(
-                        out=ws_perm[:, g, :].rearrange("p (t m) -> p m t", t=4),
-                        in_=ws_raw[:, g, :].rearrange("p (m t) -> p m t", t=4),
-                    )
-            if old:
-                rowmax(s - 2, 1)
-                finish(s - 2, 0)
-                exps(s - 2, 1)
-            if new:
-                kpose(s, 1)
-            if mid:
-                interleave(s - 1)
-            if new:
-                widen(s, 3)
-                xpose(s, 3)
-                quant_k(s)
-            if old:
-                finish(s - 2, 1)
-            if mid:
-                quant_q(s - 1)
+        spread_scale(0)
+        spread_scale(1)
+        permute_codes()
+        build_mask()
+        widen(0, 0)
+        turn_x(0, 0)
+        widen(0, 1)
+        empty_x(0, 0)
+        turn_k(0, 0)
+        turn_x(0, 1)
+        empty_k(0, 0)
+        widen(0, 2)
+        empty_x(0, 1)
+        turn_k(0, 1)
+        turn_x(0, 2)
+        empty_k(0, 1)
+        widen(0, 3)
+        empty_x(0, 2)
+        turn_x(0, 3)
+        permute_scales()
+        quant_k(0)
+        empty_x(0, 3)
+        turn_k(1, 0)
+        turn_k(1, 1)
+        empty_k(1, 0)
+        empty_k(1, 1)
+        for n in range(1, L):
+            c = n + 1
+            step(widen, n, 0)
+            if n > 1:
+                step(empty_x, n - 1, 3)
+            step(project, n - 2, 3)
+            step(empty_q, n - 2, 3)
+            step(row_max, n - 3)
+            step(quant_k, n)
+            step(turn_x, n, 0)
+            step(turn_k, c, 0)
+            step(quant_x, n - 1)
+            step(empty_x, n, 0)
+            step(exps, n - 3)
+            step(widen, n, 1)
+            step(project, n - 1, 0)
+            step(empty_k, c, 0)
+            step(turn_k, c, 1)
+            step(turn_x, n, 1)
+            step(empty_q, n - 1, 0)
+            step(weave_q, n - 2)
+            step(recip, n - 3)
+            step(widen, n, 2)
+            step(empty_x, n, 1)
+            step(project, n - 1, 1)
+            step(empty_k, c, 1)
+            step(quant_q, n - 2)
+            step(turn_x, n, 2)
+            step(finish, n - 3)
+            step(empty_q, n - 1, 1)
+            step(scores, n - 2)
+            step(project, n - 1, 2)
+            step(widen, n, 3)
+            step(empty_x, n, 2)
+            step(empty_q, n - 1, 2)
+            step(mask_scores, n - 2)
+            step(turn_x, n, 3)
+        widen(L, 0)
+        empty_x(L - 1, 3)
+        project(L - 2, 3)
+        empty_q(L - 2, 3)
+        row_max(L - 3)
+        quant_k(L)
+        turn_x(L, 0)
+        quant_x(L - 1)
+        t_empty_x(0)
+        exps(L - 3)
+        widen(L, 1)
+        project(L - 1, 0)
+        turn_x(L, 1)
+        empty_q(L - 1, 0)
+        weave_q(L - 2)
+        recip(L - 3)
+        project(L - 1, 1)
+        widen(L, 2)
+        t_empty_x(1)
+        empty_q(L - 1, 1)
+        project(L - 1, 2)
+        turn_x(L, 2)
+        quant_q(L - 2)
+        widen(L, 3)
+        scores(L - 2)
+        project(L - 1, 3)
+        empty_q(L - 1, 2)
+        t_empty_x(2)
+        turn_x(L, 3)
+        mask_scores(L - 2)
+        t_quant_x(0)
+        t_quant_x(1)
+        empty_q(L - 1, 3)
+        t_empty_x(3)
+        t_project(0)
+        row_max(L - 2)
+        t_quant_x(2)
+        t_project(1)
+        weave_q(L - 1)
+        t_empty_q(0)
+        finish(L - 3)
+        exps(L - 2)
+        t_project(2)
+        t_quant_x(3)
+        quant_q(L - 1)
+        t_project(3)
+        scores(L - 1)
+        recip(L - 2)
+        t_empty_q(1)
+        finish(L - 2)
+        t_quant_q(0)
+        mask_scores(L - 1)
+        t_quant_q(1)
+        scores(L, 0, 2, "tp", 4)
+        t_empty_q(2)
+        row_max(L - 1)
+        exps(L - 1)
+        t_empty_q(3)
+        t_quant_q(2)
+        mask_scores(L, 0, 2)
+        t_quant_q(3)
+        scores(L, 2, 2, "tp", 4)
+        recip(L - 1)
+        row_max(L, 0, 2)
+        finish(L - 1)
+        exps(L, 0, 2)
+        mask_scores(L, 2, 2)
+        row_max(L, 2, 2)
+        exps(L, 2, 2)
+        recip(L, 0, 2)
+        finish(L, 0, 2)
+        recip(L, 2, 2)
+        finish(L, 2, 2)

@@ -41,7 +41,10 @@ def tile_localattention_pa_t_w4_kernel(tc, x_bytes, x_scale, Wq_words, Wq_scales
 
         ident = keep.tile([P, P], F32, name="ident")
         scale_p = keep.tile([P, G, 4], F32, name="scale_p")
-        scale_b = keep.tile([P, D], F32, name="scale_b", align_bytes=64)
+        xi = [keep.tile([P, G * S * 4], BF16, name=f"xi{j}", align_bytes=64) for j in range(2)]
+        qi = [keep.tile([P, S * 4], BF16, name=f"qi{j}", align_bytes=64) for j in range(2)]
+        kt = [keep.tile([P, S * 4], BF16, name=f"kt{j}", align_bytes=64) for j in range(3)]
+        x_head = [keep.tile([P, 2 * D], BF16, name=f"x_head{j}", align_bytes=64) for j in range(2)]
         w_raw = keep.tile([P, G, 2 * E], U8, name="w_raw", align_bytes=64)
         w_perm = keep.tile([P, G, 2 * E], U8, name="w_perm", align_bytes=64)
         ws_raw = keep.tile([P, G, E], U8, name="ws_raw", align_bytes=64)
@@ -68,28 +71,26 @@ def tile_localattention_pa_t_w4_kernel(tc, x_bytes, x_scale, Wq_words, Wq_scales
             nc.sync.dma_start(out=k_tiles[b][:], in_=rows.rearrange("(i p) e -> p i e", p=P))
 
         nc.vector.memset(ws_raw[:].rearrange("p g n -> p (g n)").bitcast(I32), 0)
-        nc.sync.dma_start(out=scale_p[:], in_=x_scale.rearrange("a b (g p c) -> p (a b g) c", p=P, c=4))
         nc.sync.dma_start(out=w_raw[:].bitcast(I32), in_=Wq_words.rearrange("g p n -> p g n").bitcast(I32))
         nc.sync.dma_start(out=x_first[:], in_=xv[0][:, 0, :])
-        nc.sync.dma_start(out=x_tiles[0][:, 1:NT, :], in_=xv[0][:, 1:NT, :])
         for q in range(4):
             nc.sync.dma_start(
                 out=ws_raw[32 * q : 32 * q + 4].bitcast(I32),
                 in_=Wq_scales[:, 4 * q : 4 * q + 4, :].rearrange("g r n -> r g n").bitcast(I32),
             )
+        nc.sync.dma_start(out=x_tiles[0][:, 1:NT, :], in_=xv[0][:, 1:NT, :])
+        nc.sync.dma_start(out=scale_p[:], in_=x_scale.rearrange("a b (g p c) -> p (a b g) c", p=P, c=4))
+        nc.sync.dma_start(out=x_tiles[1][:], in_=xv[1])
         nc.sync.dma_start(out=k_tiles[0][0:SHIFT, 0, :], in_=kflat[B * S - SHIFT : B * S, :])
         nc.sync.dma_start(out=k_tiles[0][SHIFT:P, 0, :], in_=kflat[0 : P - SHIFT, :])
         nc.sync.dma_start(
             out=k_tiles[0][:, 1:NT, :], in_=kflat[P - SHIFT : S - SHIFT, :].rearrange("(i p) e -> p i e", p=P)
         )
-        load_k(1)
-        nc.sync.dma_start(out=x_tiles[1][:], in_=xv[1])
         nc.sync.dma_start(out=bias[:], in_=bq.rearrange("(p t) -> p t", t=4))
-        load_k(2)
+        load_k(1)
         for b in range(2, B):
             nc.sync.dma_start(out=x_tiles[b][:], in_=xv[b])
-            if b + 1 < B:
-                load_k(b + 1)
+            load_k(b)
 
         make_identity(nc, ident[:])
         for j in range(2):
@@ -118,7 +119,7 @@ def tile_localattention_pa_t_w4_kernel(tc, x_bytes, x_scale, Wq_words, Wq_scales
             nc.scalar.copy(out=mask[0:Q, 0, 0:MARGIN], in_=band[0:Q, Q + STRIP - MARGIN : Q + STRIP])
             nc.scalar.copy(out=mask[Q:P, NT - 1, STRIP - MARGIN : STRIP], in_=band[Q:P, 0:MARGIN])
 
-        xw, xt, xi, xc, xsc, kt, ktp, acc, qp, qi = {}, {}, {}, {}, {}, {}, {}, {}, {}, {}
+        xw, xt, xc, xsc, ktp, acc, qp = {}, {}, {}, {}, {}, {}, {}
         sc, sm, nm, ss, rs = {}, {}, {}, {}, {}
 
         def permute_codes():
@@ -133,41 +134,43 @@ def tile_localattention_pa_t_w4_kernel(tc, x_bytes, x_scale, Wq_words, Wq_scales
                 in_=ws_raw[:].rearrange("p g (m t) -> p g t m", t=4),
             )
 
-        def spread_scale(g):
-            bank = psum.tile([P, 4, P], F32, name="tp", bufs=4)
-            for c in range(4):
-                nc.tensor.transpose(bank[:, c, :], scale_p[:, g, c : c + 1].to_broadcast([P, P]), ident[:])
-            dst = scale_b[:, 512 * g : 512 * (g + 1)].rearrange("m (p c) -> m p c", c=4)
-            nc.scalar.activation(out=dst, in_=bank[:].rearrange("m c p -> m p c"), func=ACT.Copy)
+        def widen_head(i):
+            xw[0, i] = x_head[i // 2][:, D * (i % 2) : D * (i % 2 + 1)]
+            codes = x_first[:] if i == 0 else x_tiles[0][:, i, :]
+            nc.scalar.activation(out=xw[0, i], in_=codes.bitcast(FP8), func=ACT.Copy)
 
-        def widen(b, i):
-            xw[b, i] = work.tile([P, D], BF16, name="xw", bufs=4, align_bytes=64)
-            codes = x_first[:] if (b, i) == (0, 0) else x_tiles[b][:, i, :]
-            parts = G if (b, i) == (0, 0) else 1
-            for h in range(parts):
-                cols = slice(D // parts * h, D // parts * (h + 1))
-                nc.vector.tensor_tensor(out=xw[b, i][:, cols], in0=codes[:, cols].bitcast(FP8), in1=scale_b[:, cols], op=ALU.mult)
+        def widen(b, pair):
+            if pair == 1:
+                room = xi[(b - 1) % 2][:, 0 : 2 * D]
+            else:
+                room = (x_head[0], kt[1])[b - 1][:] if b < 3 else qi[(b - 3) % 2][:]
+            for j in range(2):
+                xw[b, 2 * pair + j] = room[:, D * j : D * (j + 1)]
+            codes = x_tiles[b][:, 2 * pair : 2 * pair + 2, :].rearrange("p i k -> p (i k)")
+            nc.gpsimd.tensor_copy(out=room, in_=codes.bitcast(FP8))
 
         def turn_x(b, i):
-            words = xw[b, i][:].bitcast(F32)
-            xt[b, i] = psum.tile([P, G, 2, P], F32, name="tp", bufs=4)
+            words = xw[b, i].bitcast(F32)
+            xt[b, i] = psum.tile([P, 2, G, P], F32, name="tp", bufs=4)
             for g in range(G):
                 for h in range(2):
-                    nc.tensor.transpose(xt[b, i][:, g, h, :], words[:, 256 * g + h : 256 * (g + 1) : 2], ident[:])
+                    nc.tensor.transpose(xt[b, i][:, h, g, :], words[:, 256 * g + h : 256 * (g + 1) : 2], ident[:])
+
+        def scale_x(b, i, dst):
+            values = xt[b, i][:].bitcast(BF16).rearrange("p h g (r e) -> p g r h e", e=2)
+            scales = scale_p[:].rearrange("p g (h e) -> p g h e", e=2).unsqueeze(2).to_broadcast([P, G, P, 2, 2])
+            nc.vector.tensor_tensor(out=dst, in0=values, in1=scales, op=ALU.mult)
 
         def empty_x(b, i):
-            if i == 0:
-                xi[b] = work.tile([P, G, S, 2], F32, name="xi", align_bytes=64)
-            nc.scalar.copy(out=xi[b][:, :, P * i : P * (i + 1), :], in_=xt[b, i][:].rearrange("p g h r -> p g r h"))
+            rows = xi[b % 2][:].rearrange("p (g n h e) -> p g n h e", g=G, h=2, e=2)
+            scale_x(b, i, rows[:, :, P * i : P * (i + 1)])
 
         def quant_x(b):
             xc[b] = work.tile([P, G, S], U32, name="xc", align_bytes=64)
             xsc[b] = work.tile([P, G, S], U8, name="xsc", align_bytes=64)
             for g in range(G):
                 nc.vector.quantize_mx(
-                    out=xc[b][:, g, :].bitcast(FP8X4),
-                    scales=xsc[b][:, g, :],
-                    in_=xi[b][:, g].rearrange("p n h -> p (n h)").bitcast(BF16),
+                    out=xc[b][:, g, :].bitcast(FP8X4), scales=xsc[b][:, g, :], in_=xi[b % 2][:, 4 * S * g : 4 * S * (g + 1)]
                 )
 
         def turn_k(b, half):
@@ -178,16 +181,14 @@ def tile_localattention_pa_t_w4_kernel(tc, x_bytes, x_scale, Wq_words, Wq_scales
                     nc.tensor.transpose(ktp[b, half][:, j, h, :], words[:, h:256:2], ident[:])
 
         def empty_k(b, half):
-            if half == 0:
-                kt[b] = work.tile([P, S, 2], F32, name="kt", bufs=3, align_bytes=64)
-            dst = kt[b][:, 256 * half : 256 * (half + 1), :].rearrange("p (j r) h -> p j r h", j=2)
+            dst = kt[b % 3][:, 2 * S * half : 2 * S * (half + 1)].bitcast(F32).rearrange("p (j r h) -> p j r h", j=2, h=2)
             nc.scalar.copy(out=dst, in_=ktp[b, half][:].rearrange("p j h r -> p j r h"))
 
         def quant_k(b):
-            rows = kt[b][:].rearrange("p n h -> p (n h)").bitcast(BF16)
-            nc.vector.quantize_mx(out=kc[:, S * b : S * (b + 1)].bitcast(FP8X4), scales=ksc[:, S * b : S * (b + 1)], in_=rows)
+            rows = kt[b % 3][:]
             if b == 0:
                 nc.vector.quantize_mx(out=kc[:, B * S :].bitcast(FP8X4), scales=ksc[:, B * S :], in_=rows[:, 0 : 4 * Q])
+            nc.vector.quantize_mx(out=kc[:, S * b : S * (b + 1)].bitcast(FP8X4), scales=ksc[:, S * b : S * (b + 1)], in_=rows)
 
         def project(b, t):
             acc[b, t] = psum.tile([P, S], F32, name="acc", bufs=3)
@@ -208,16 +209,12 @@ def tile_localattention_pa_t_w4_kernel(tc, x_bytes, x_scale, Wq_words, Wq_scales
             pair = qp[b][:, t // 2, :].bitcast(BF16)
             nc.scalar.activation(out=pair[:, t % 2 :: 2], in_=acc[b, t][:], func=ACT.Identity, bias=bias[:, t : t + 1])
 
-        def weave_q(b, cut=0):
-            qi[b] = work.tile([P, S, 2], F32, name="qi", align_bytes=64)
-            pairs = qp[b][:].rearrange("p h n -> p n h")
-            if cut > 0:
-                nc.scalar.copy(out=qi[b][:, 0:cut], in_=pairs[:, 0:cut])
-            if cut < S:
-                nc.vector.tensor_copy(out=qi[b][:, cut:S], in_=pairs[:, cut:S])
+        def weave_q(b):
+            dst = qi[b % 2][:].bitcast(F32).rearrange("p (n h) -> p n h", h=2)
+            nc.scalar.copy(out=dst, in_=qp[b][:].rearrange("p h n -> p n h"))
 
         def quant_q(b):
-            rows = qi[b][:].rearrange("p n h -> p (n h)").bitcast(BF16)
+            rows = qi[b % 2][:]
             cuts = [0] + list(range(Q, S, P)) + [S]
             for lo, hi in zip(cuts[:-1], cuts[1:]):
                 at = lo + Q * ((lo // Q + 1) // 2)
@@ -289,14 +286,14 @@ def tile_localattention_pa_t_w4_kernel(tc, x_bytes, x_scale, Wq_words, Wq_scales
         tx, tc_, ts, tacc, tq = {}, {}, {}, {}, {}
 
         def t_empty_x(i):
-            tx[i] = work.tile([P, G, P, 2], F32, name="t_xi", bufs=4, align_bytes=64)
-            nc.scalar.copy(out=tx[i][:], in_=xt[L, i][:].rearrange("p g h r -> p g r h"))
+            tx[i] = work.tile([P, G, P, 2, 2], BF16, name="t_xi", bufs=4, align_bytes=64)
+            scale_x(L, i, tx[i][:])
 
         def t_quant_x(i):
             tc_[i] = work.tile([P, G * P], U32, name="t_xc", bufs=4, align_bytes=64)
             ts[i] = work.tile([P, G * P], U8, name="t_xsc", bufs=4, align_bytes=64)
             nc.vector.quantize_mx(
-                out=tc_[i][:].bitcast(FP8X4), scales=ts[i][:], in_=tx[i][:].rearrange("p g n h -> p (g n h)").bitcast(BF16)
+                out=tc_[i][:].bitcast(FP8X4), scales=ts[i][:], in_=tx[i][:].rearrange("p g n h e -> p (g n h e)")
             )
 
         def t_project(i):
@@ -331,133 +328,115 @@ def tile_localattention_pa_t_w4_kernel(tc, x_bytes, x_scale, Wq_words, Wq_scales
             if 0 <= b < B:
                 fn(b, *args)
 
-        spread_scale(0)
-        spread_scale(1)
         permute_codes()
-        build_mask()
-        widen(0, 0)
-        turn_x(0, 0)
-        widen(0, 1)
-        empty_x(0, 0)
-        turn_k(0, 0)
-        turn_x(0, 1)
-        empty_k(0, 0)
-        widen(0, 2)
-        empty_x(0, 1)
-        turn_k(0, 1)
-        turn_x(0, 2)
-        empty_k(0, 1)
-        widen(0, 3)
-        empty_x(0, 2)
-        turn_x(0, 3)
         permute_scales()
-        quant_k(0)
-        empty_x(0, 3)
-        turn_k(1, 0)
-        turn_k(1, 1)
-        empty_k(1, 0)
-        empty_k(1, 1)
+        for i in range(NT):
+            widen_head(i)
+            turn_x(0, i)
+            if i == 1:
+                widen(1, 0)
+        for i in range(NT):
+            empty_x(0, i)
+        build_mask()
+        for c in range(2):
+            for half in range(2):
+                turn_k(c, half)
+                empty_k(c, half)
         for n in range(1, L):
-            c = n + 1
-            step(widen, n, 0)
-            if n > 1:
-                step(empty_x, n - 1, 3)
+            quant_x(n - 1)
+            widen(n, 1)
+            turn_x(n, 0)
             step(project, n - 2, 3)
+            turn_x(n, 1)
             step(empty_q, n - 2, 3)
-            step(row_max, n - 3)
-            step(quant_k, n)
-            step(turn_x, n, 0)
-            step(turn_k, c, 0)
-            step(quant_x, n - 1)
-            step(empty_x, n, 0)
-            step(exps, n - 3)
-            step(widen, n, 1)
-            step(project, n - 1, 0)
-            step(empty_k, c, 0)
-            step(turn_k, c, 1)
-            step(turn_x, n, 1)
-            step(empty_q, n - 1, 0)
+            empty_x(n, 0)
             step(weave_q, n - 2)
-            step(recip, n - 3)
-            step(widen, n, 2)
-            step(empty_x, n, 1)
-            step(project, n - 1, 1)
-            step(empty_k, c, 1)
+            project(n - 1, 0)
+            turn_k(n + 1, 0)
+            step(row_max, n - 3)
+            empty_q(n - 1, 0)
+            empty_x(n, 1)
+            project(n - 1, 1)
+            step(exps, n - 3)
+            turn_x(n, 2)
             step(quant_q, n - 2)
-            step(turn_x, n, 2)
-            step(finish, n - 3)
-            step(empty_q, n - 1, 1)
+            if n == 1:
+                quant_k(0)
+            quant_k(n)
+            widen(n + 1, 0)
+            empty_k(n + 1, 0)
+            empty_q(n - 1, 1)
             step(scores, n - 2)
-            step(project, n - 1, 2)
-            step(widen, n, 3)
-            step(empty_x, n, 2)
-            step(empty_q, n - 1, 2)
+            step(recip, n - 3)
+            empty_x(n, 2)
+            turn_x(n, 3)
+            step(finish, n - 3)
+            project(n - 1, 2)
+            empty_x(n, 3)
+            turn_k(n + 1, 1)
+            empty_q(n - 1, 2)
             step(mask_scores, n - 2)
-            step(turn_x, n, 3)
-        widen(L, 0)
-        empty_x(L - 1, 3)
-        project(L - 2, 3)
-        empty_q(L - 2, 3)
-        row_max(L - 3)
-        quant_k(L)
-        turn_x(L, 0)
+            empty_k(n + 1, 1)
         quant_x(L - 1)
-        t_empty_x(0)
-        exps(L - 3)
         widen(L, 1)
-        project(L - 1, 0)
+        turn_x(L, 0)
+        project(L - 2, 3)
         turn_x(L, 1)
-        empty_q(L - 1, 0)
+        empty_q(L - 2, 3)
+        t_empty_x(0)
         weave_q(L - 2)
-        recip(L - 3)
-        project(L - 1, 1)
-        widen(L, 2)
+        project(L - 1, 0)
+        row_max(L - 3)
+        empty_q(L - 1, 0)
         t_empty_x(1)
-        empty_q(L - 1, 1)
-        project(L - 1, 2)
+        project(L - 1, 1)
+        exps(L - 3)
         turn_x(L, 2)
+        project(L - 1, 2)
         quant_q(L - 2)
-        widen(L, 3)
+        quant_k(L)
+        empty_q(L - 1, 1)
         scores(L - 2)
-        project(L - 1, 3)
-        empty_q(L - 1, 2)
-        t_empty_x(2)
         turn_x(L, 3)
-        mask_scores(L - 2)
+        project(L - 1, 3)
+        recip(L - 3)
+        t_empty_x(2)
+        empty_q(L - 1, 2)
         t_quant_x(0)
         t_quant_x(1)
-        empty_q(L - 1, 3)
         t_empty_x(3)
+        empty_q(L - 1, 3)
         t_project(0)
-        row_max(L - 2)
+        mask_scores(L - 2)
         t_quant_x(2)
         t_project(1)
         weave_q(L - 1)
         t_empty_q(0)
+        t_quant_x(3)
+        row_max(L - 2)
         finish(L - 3)
         exps(L - 2)
         t_project(2)
-        t_quant_x(3)
-        quant_q(L - 1)
+        t_empty_q(1)
         t_project(3)
+        quant_q(L - 1)
         scores(L - 1)
         recip(L - 2)
-        t_empty_q(1)
         finish(L - 2)
         t_quant_q(0)
-        mask_scores(L - 1)
         t_quant_q(1)
-        scores(L, 0, 2, "tp", 4)
         t_empty_q(2)
+        scores(L, 0, 2, "tp", 4)
+        mask_scores(L - 1)
+        t_empty_q(3)
         row_max(L - 1)
         exps(L - 1)
-        t_empty_q(3)
         t_quant_q(2)
         mask_scores(L, 0, 2)
         t_quant_q(3)
         scores(L, 2, 2, "tp", 4)
-        recip(L - 1)
         row_max(L, 0, 2)
+        recip(L - 1)
         finish(L - 1)
         exps(L, 0, 2)
         mask_scores(L, 2, 2)

@@ -71,8 +71,8 @@ def tile_localattention_pa_t_w4_kernel(tc, x_bytes, x_scale, Wq_words, Wq_scales
             nc.sync.dma_start(out=k_tiles[b][:], in_=rows.rearrange("(i p) e -> p i e", p=P))
 
         nc.vector.memset(ws_raw[:].rearrange("p g n -> p (g n)").bitcast(I32), 0)
-        nc.sync.dma_start(out=w_raw[:].bitcast(I32), in_=Wq_words.rearrange("g p n -> p g n").bitcast(I32))
         nc.sync.dma_start(out=x_first[:], in_=xv[0][:, 0, :])
+        nc.sync.dma_start(out=w_raw[:].bitcast(I32), in_=Wq_words.rearrange("g p n -> p g n").bitcast(I32))
         for q in range(4):
             nc.sync.dma_start(
                 out=ws_raw[32 * q : 32 * q + 4].bitcast(I32),
@@ -134,16 +134,16 @@ def tile_localattention_pa_t_w4_kernel(tc, x_bytes, x_scale, Wq_words, Wq_scales
                 in_=ws_raw[:].rearrange("p g (m t) -> p g t m", t=4),
             )
 
-        def widen_head(i):
-            xw[0, i] = x_head[i // 2][:, D * (i % 2) : D * (i % 2 + 1)]
-            codes = x_first[:] if i == 0 else x_tiles[0][:, i, :]
-            nc.scalar.activation(out=xw[0, i], in_=codes.bitcast(FP8), func=ACT.Copy)
+        def widen_head(b, i):
+            xw[b, i] = x_head[i // 2][:, D * (i % 2) : D * (i % 2 + 1)]
+            codes = x_first[:] if (b, i) == (0, 0) else x_tiles[b][:, i, :]
+            nc.scalar.activation(out=xw[b, i], in_=codes.bitcast(FP8), func=ACT.Copy)
 
         def widen(b, pair):
             if pair == 1:
                 room = xi[(b - 1) % 2][:, 0 : 2 * D]
             else:
-                room = (x_head[0], kt[1])[b - 1][:] if b < 3 else qi[(b - 3) % 2][:]
+                room = (x_head[0][:], xi[0][:, 0 : 2 * D])[b - 1] if b < 3 else qi[(b - 3) % 2][:]
             for j in range(2):
                 xw[b, 2 * pair + j] = room[:, D * j : D * (j + 1)]
             codes = x_tiles[b][:, 2 * pair : 2 * pair + 2, :].rearrange("p i k -> p (i k)")
@@ -164,6 +164,21 @@ def tile_localattention_pa_t_w4_kernel(tc, x_bytes, x_scale, Wq_words, Wq_scales
         def empty_x(b, i):
             rows = xi[b % 2][:].rearrange("p (g n h e) -> p g n h e", g=G, h=2, e=2)
             scale_x(b, i, rows[:, :, P * i : P * (i + 1)])
+
+        def empty_x_scalar(b, i, dst=None):
+            if dst is None:
+                dst = xi[b % 2][:].bitcast(F32).rearrange("p (g n h) -> p g n h", g=G, h=2)[:, :, P * i : P * (i + 1)]
+            planes = work.tile([P, 2, G, P], F32, name="x_planes", align_bytes=64)
+            for e in range(2):
+                for h in range(2):
+                    for g in range(G):
+                        nc.scalar.activation(
+                            out=planes[:, h, g, :].bitcast(BF16)[:, e::2],
+                            in_=xt[b, i][:, h, g, :].bitcast(BF16)[:, e::2],
+                            func=ACT.Copy,
+                            scale=scale_p[:, g, 2 * h + e : 2 * h + e + 1],
+                        )
+            nc.scalar.copy(out=dst, in_=planes[:].rearrange("p h g r -> p g r h"))
 
         def quant_x(b):
             xc[b] = work.tile([P, G, S], U32, name="xc", align_bytes=64)
@@ -276,10 +291,19 @@ def tile_localattention_pa_t_w4_kernel(tc, x_bytes, x_scale, Wq_words, Wq_scales
             if last:
                 nc.sync.dma_start(out=out[b, S - Q : S, S - STRIP + MARGIN : S], in_=strip[Q:P, n - 1, 0 : STRIP - MARGIN])
 
-        def finish(b, i0=0, n=NT):
+        def finish(b, i0=0, n=NT, eng="s"):
             strip = work.tile([P, n, STRIP], F32, name="strip", bufs=4)
+            if eng == "v":
+                nc.vector.tensor_tensor(
+                    out=strip[:], in0=sm[b, i0][:], in1=rs[b, i0][:].unsqueeze(2).to_broadcast([P, n, STRIP]), op=ALU.mult
+                )
             for i in range(n):
-                nc.scalar.activation(out=strip[:, i, :], in_=sm[b, i0][:, i, :], func=ACT.Copy, scale=rs[b, i0][:, i : i + 1])
+                if eng == "s":
+                    nc.scalar.activation(out=strip[:, i, :], in_=sm[b, i0][:, i, :], func=ACT.Copy, scale=rs[b, i0][:, i : i + 1])
+                if eng == "g":
+                    nc.gpsimd.tensor_scalar(
+                        out=strip[:, i, :], in0=sm[b, i0][:, i, :], scalar1=rs[b, i0][:, i : i + 1], scalar2=0.0, op0=ALU.mult, op1=ALU.add
+                    )
             store(b, strip, i0, n)
 
         L = B - 1
@@ -297,7 +321,7 @@ def tile_localattention_pa_t_w4_kernel(tc, x_bytes, x_scale, Wq_words, Wq_scales
             )
 
         def t_project(i):
-            tacc[i] = psum.tile([P, 4, P], F32, name="acc", bufs=3)
+            tacc[i] = psum.tile([P, 4, P], F32, name="tp", bufs=4)
             for t in range(4):
                 for g in range(G):
                     nc.tensor.matmul_mx(
@@ -324,6 +348,58 @@ def tile_localattention_pa_t_w4_kernel(tc, x_bytes, x_scale, Wq_words, Wq_scales
                     out=qc[L % 2][:, cols].bitcast(FP8X4), scales=qsc[L % 2][:, cols], in_=rows[:, 4 * Q * s : 4 * Q * (s + 1)]
                 )
 
+        half = {}
+
+        def h_empty_x(i):
+            if i == 0:
+                half["x"] = work.tile([P, G, 2 * P, 2, 2], BF16, name="h_xi", bufs=1, align_bytes=64)
+            scale_x(L, i, half["x"][:, :, P * i : P * (i + 1)])
+
+        def h_quant_x():
+            half["c"] = work.tile([P, G * 2 * P], U32, name="h_xc", bufs=1, align_bytes=64)
+            half["s"] = work.tile([P, G * 2 * P], U8, name="h_xsc", bufs=1, align_bytes=64)
+            nc.vector.quantize_mx(
+                out=half["c"][:].bitcast(FP8X4), scales=half["s"][:], in_=half["x"][:].rearrange("p g n h e -> p (g n h e)")
+            )
+
+        def h_project(h):
+            half[h] = psum.tile([P, 2, 2, P], F32, name="acc", bufs=3)
+            for e in range(2):
+                t = 2 * h + e
+                for i in range(2):
+                    for g in range(G):
+                        cols = slice(2 * P * g + P * i, 2 * P * g + P * (i + 1))
+                        nc.tensor.matmul_mx(
+                            out=half[h][:, e, i, :],
+                            lhsT=w_perm[:, g, 256 * t : 256 * (t + 1)].bitcast(FP4X4),
+                            lhsT_scale=ws_perm[:, g, P * t : P * (t + 1)],
+                            rhs=half["c"][:, cols].bitcast(FP8X4),
+                            rhs_scale=half["s"][:, cols],
+                            start=(g == 0),
+                            stop=(g == G - 1),
+                        )
+
+        def h_empty_q():
+            half["p"] = work.tile([P, 2, 2 * P], F32, name="h_qp", bufs=1, align_bytes=64)
+            for e, h in ((0, 0), (0, 1), (1, 0), (1, 1)):
+                t = 2 * h + e
+                nc.scalar.activation(
+                    out=half["p"][:, h, :].bitcast(BF16)[:, e::2],
+                    in_=half[h][:, e].rearrange("p i n -> p (i n)"),
+                    func=ACT.Identity,
+                    bias=bias[:, t : t + 1],
+                )
+
+        def h_weave_q():
+            half["q"] = work.tile([P, 2 * P, 2], F32, name="h_qi", bufs=1, align_bytes=64)
+            nc.scalar.copy(out=half["q"][:], in_=half["p"][:].rearrange("p h n -> p n h"))
+
+        def h_quant_q():
+            rows = half["q"][:].rearrange("p n h -> p (n h)").bitcast(BF16)
+            for lo, hi, at in ((0, Q, 0), (Q, 3 * Q, 2 * Q), (3 * Q, 4 * Q, 5 * Q)):
+                cols = slice(at, at + hi - lo)
+                nc.vector.quantize_mx(out=qc[L % 2][:, cols].bitcast(FP8X4), scales=qsc[L % 2][:, cols], in_=rows[:, 4 * lo : 4 * hi])
+
         def step(fn, b, *args):
             if 0 <= b < B:
                 fn(b, *args)
@@ -331,118 +407,151 @@ def tile_localattention_pa_t_w4_kernel(tc, x_bytes, x_scale, Wq_words, Wq_scales
         permute_codes()
         permute_scales()
         for i in range(NT):
-            widen_head(i)
+            widen_head(0, i)
             turn_x(0, i)
             if i == 1:
                 widen(1, 0)
-        for i in range(NT):
-            empty_x(0, i)
+        widen_head(1, 2)
+        widen_head(1, 3)
+        empty_x(0, 0)
+        empty_x(0, 1)
+        turn_k(0, 0)
+        turn_k(0, 1)
+        empty_k(0, 0)
+        empty_k(0, 1)
         build_mask()
-        for c in range(2):
-            for half in range(2):
-                turn_k(c, half)
-                empty_k(c, half)
-        for n in range(1, L):
+        turn_x(1, 0)
+        empty_x(0, 2)
+        turn_x(1, 1)
+        empty_x(0, 3)
+        quant_x(0)
+        widen(2, 0)
+        project(0, 0)
+        turn_x(1, 2)
+        empty_x(1, 0)
+        empty_q(0, 0)
+        project(0, 1)
+        turn_x(1, 3)
+        empty_x(1, 1)
+        empty_q(0, 1)
+        project(0, 2)
+        turn_x(2, 0)
+        empty_x(1, 2)
+        empty_q(0, 2)
+        project(0, 3)
+        turn_k(1, 0)
+        turn_x(2, 1)
+        empty_x(1, 3)
+        empty_q(0, 3)
+        empty_k(1, 0)
+        turn_k(1, 1)
+        quant_k(0)
+        weave_q(0)
+        empty_k(1, 1)
+        halves = {2: (4, 5), 3: (6, 7, 8), 4: (9, 10, 11), 5: (12, 13), 6: (14, 15)}
+        for n in range(2, L):
+            keys = [divmod(j, 2) for j in halves[n]]
+            if n == 5:
+                quant_k(4)
             quant_x(n - 1)
             widen(n, 1)
-            turn_x(n, 0)
-            step(project, n - 2, 3)
-            turn_x(n, 1)
-            step(empty_q, n - 2, 3)
+            step(exps, n - 3)
+            if n > 2:
+                turn_x(n, 0)
+                project(n - 2, 3)
+                turn_x(n, 1)
+                empty_q(n - 2, 3)
             empty_x(n, 0)
-            step(weave_q, n - 2)
+            if n > 2:
+                weave_q(n - 2)
             project(n - 1, 0)
-            turn_k(n + 1, 0)
-            step(row_max, n - 3)
+            turn_k(*keys[0])
             empty_q(n - 1, 0)
             empty_x(n, 1)
-            project(n - 1, 1)
-            step(exps, n - 3)
-            turn_x(n, 2)
-            step(quant_q, n - 2)
-            if n == 1:
-                quant_k(0)
-            quant_k(n)
-            widen(n + 1, 0)
-            empty_k(n + 1, 0)
-            empty_q(n - 1, 1)
-            step(scores, n - 2)
             step(recip, n - 3)
+            project(n - 1, 1)
+            step(finish, n - 3)
+            turn_x(n, 2)
+            quant_q(n - 2)
+            quant_k(n - 1 if n < 5 else n)
+            widen(n + 1, 0)
+            empty_k(*keys[0])
+            empty_q(n - 1, 1)
+            scores(n - 2)
             empty_x(n, 2)
             turn_x(n, 3)
-            step(finish, n - 3)
             project(n - 1, 2)
+            mask_scores(n - 2)
             empty_x(n, 3)
-            turn_k(n + 1, 1)
+            for key in keys[1:]:
+                turn_k(*key)
             empty_q(n - 1, 2)
-            step(mask_scores, n - 2)
-            empty_k(n + 1, 1)
+            row_max(n - 2)
+            for key in keys[1:]:
+                empty_k(*key)
         quant_x(L - 1)
         widen(L, 1)
+        exps(L - 3)
         turn_x(L, 0)
         project(L - 2, 3)
         turn_x(L, 1)
         empty_q(L - 2, 3)
-        t_empty_x(0)
+        h_empty_x(0)
         weave_q(L - 2)
         project(L - 1, 0)
-        row_max(L - 3)
         empty_q(L - 1, 0)
-        t_empty_x(1)
-        project(L - 1, 1)
-        exps(L - 3)
-        turn_x(L, 2)
+        h_empty_x(1)
+        recip(L - 3)
         project(L - 1, 2)
+        empty_q(L - 1, 2)
+        project(L - 1, 1)
+        turn_x(L, 2)
         quant_q(L - 2)
-        quant_k(L)
-        empty_q(L - 1, 1)
-        scores(L - 2)
+        h_quant_x()
         turn_x(L, 3)
         project(L - 1, 3)
-        recip(L - 3)
+        scores(L - 2)
         t_empty_x(2)
-        empty_q(L - 1, 2)
-        t_quant_x(0)
-        t_quant_x(1)
+        empty_q(L - 1, 1)
+        h_project(0)
         t_empty_x(3)
         empty_q(L - 1, 3)
-        t_project(0)
-        mask_scores(L - 2)
+        h_project(1)
         t_quant_x(2)
-        t_project(1)
-        weave_q(L - 1)
-        t_empty_q(0)
         t_quant_x(3)
-        row_max(L - 2)
-        finish(L - 3)
-        exps(L - 2)
         t_project(2)
-        t_empty_q(1)
+        mask_scores(L - 2)
+        finish(L - 3)
+        weave_q(L - 1)
+        quant_k(L)
+        row_max(L - 2)
+        h_empty_q()
+        exps(L - 2)
         t_project(3)
         quant_q(L - 1)
         scores(L - 1)
-        recip(L - 2)
-        finish(L - 2)
-        t_quant_q(0)
-        t_quant_q(1)
         t_empty_q(2)
-        scores(L, 0, 2, "tp", 4)
+        h_weave_q()
         mask_scores(L - 1)
         t_empty_q(3)
         row_max(L - 1)
+        recip(L - 2)
+        finish(L - 2)
         exps(L - 1)
         t_quant_q(2)
-        mask_scores(L, 0, 2)
         t_quant_q(3)
         scores(L, 2, 2, "tp", 4)
-        row_max(L, 0, 2)
+        h_quant_q()
+        scores(L, 0, 2, "tp", 4)
+        mask_scores(L, 2, 2)
         recip(L - 1)
         finish(L - 1)
-        exps(L, 0, 2)
-        mask_scores(L, 2, 2)
         row_max(L, 2, 2)
         exps(L, 2, 2)
-        recip(L, 0, 2)
-        finish(L, 0, 2)
+        mask_scores(L, 0, 2)
+        row_max(L, 0, 2)
+        exps(L, 0, 2)
         recip(L, 2, 2)
-        finish(L, 2, 2)
+        finish(L, 2, 2, "v")
+        recip(L, 0, 2)
+        finish(L, 0, 2, "v")

@@ -400,6 +400,10 @@ def tile_localattention_pa_t_w4_kernel(tc, x_bytes, x_scale, Wq_words, Wq_scales
                 cols = slice(at, at + hi - lo)
                 nc.vector.quantize_mx(out=qc[L % 2][:, cols].bitcast(FP8X4), scales=qsc[L % 2][:, cols], in_=rows[:, 4 * lo : 4 * hi])
 
+        def warm_up():
+            idle = psum.tile([P, 2 * P], F32, name="sc", bufs=1)
+            nc.tensor.matmul(out=idle[:], lhsT=ident[:], rhs=zeros[:, 0 : 2 * P], start=True, stop=True)
+
         def step(fn, b, *args):
             if 0 <= b < B:
                 fn(b, *args)
@@ -408,6 +412,7 @@ def tile_localattention_pa_t_w4_kernel(tc, x_bytes, x_scale, Wq_words, Wq_scales
         permute_scales()
         for i in range(NT):
             widen_head(0, i)
+            warm_up()
             turn_x(0, i)
             if i == 1:
                 widen(1, 0)
@@ -415,11 +420,13 @@ def tile_localattention_pa_t_w4_kernel(tc, x_bytes, x_scale, Wq_words, Wq_scales
         widen_head(1, 3)
         empty_x(0, 0)
         empty_x(0, 1)
+        warm_up()
         turn_k(0, 0)
         turn_k(0, 1)
         empty_k(0, 0)
         empty_k(0, 1)
         build_mask()
+        warm_up()
         turn_x(1, 0)
         empty_x(0, 2)
         turn_x(1, 1)

@@ -27,6 +27,8 @@ Q = 64
 SHIFT = 32
 MARGIN = 8
 STRIP = Q + 2 * MARGIN
+LIVE = slice(MARGIN - HALF, STRIP - MARGIN + HALF)
+WIDTH = Q + 2 * HALF
 MASKED = -1e9
 SCALE = 1.0 / math.sqrt(E)
 
@@ -44,6 +46,7 @@ def tile_localattention_pa_t_w4_kernel(tc, x_bytes, x_scale, Wq_words, Wq_scales
         xi = [keep.tile([P, G * S * 4], BF16, name=f"xi{j}", align_bytes=64) for j in range(2)]
         qi = [keep.tile([P, S * 4], BF16, name=f"qi{j}", align_bytes=64) for j in range(2)]
         kt = [keep.tile([P, S * 4], BF16, name=f"kt{j}", align_bytes=64) for j in range(3)]
+        strips = [keep.tile([P, NT, STRIP], F32, name=f"strip{j}") for j in range(3)]
         x_head = [keep.tile([P, 2 * D], BF16, name=f"x_head{j}", align_bytes=64) for j in range(2)]
         w_raw = keep.tile([P, G, 2 * E], U8, name="w_raw", align_bytes=64)
         w_perm = keep.tile([P, G, 2 * E], U8, name="w_perm", align_bytes=64)
@@ -58,7 +61,7 @@ def tile_localattention_pa_t_w4_kernel(tc, x_bytes, x_scale, Wq_words, Wq_scales
         qc = [keep.tile([P, NT * 3 * Q], U32, name=f"qc{j}", align_bytes=64) for j in range(2)]
         qsc = [keep.tile([P, NT * 3 * Q], U8, name=f"qsc{j}", align_bytes=64) for j in range(2)]
 
-        x_first = keep.tile([P, D], U8, name="x_codes_first", align_bytes=64)
+        x_first = [keep.tile([P, D], U8, name=f"x_codes_first{i}", align_bytes=64) for i in range(2)]
         x_tiles = [keep.tile([P, NT, D], U8, name=f"x_codes{b}", align_bytes=64) for b in range(B)]
         k_tiles = [keep.tile([P, NT, E], BF16, name=f"k_rows{b}", align_bytes=64) for b in range(B)]
 
@@ -71,15 +74,16 @@ def tile_localattention_pa_t_w4_kernel(tc, x_bytes, x_scale, Wq_words, Wq_scales
             nc.sync.dma_start(out=k_tiles[b][:], in_=rows.rearrange("(i p) e -> p i e", p=P))
 
         nc.vector.memset(ws_raw[:].rearrange("p g n -> p (g n)").bitcast(I32), 0)
-        nc.sync.dma_start(out=x_first[:], in_=xv[0][:, 0, :])
+        nc.sync.dma_start(out=x_first[0][:], in_=xv[0][:, 0, :])
+        nc.sync.dma_start(out=scale_p[:], in_=x_scale.rearrange("a b (g p c) -> p (a b g) c", p=P, c=4))
         nc.sync.dma_start(out=w_raw[:].bitcast(I32), in_=Wq_words.rearrange("g p n -> p g n").bitcast(I32))
+        nc.sync.dma_start(out=x_first[1][:], in_=xv[0][:, 1, :])
         for q in range(4):
             nc.sync.dma_start(
                 out=ws_raw[32 * q : 32 * q + 4].bitcast(I32),
                 in_=Wq_scales[:, 4 * q : 4 * q + 4, :].rearrange("g r n -> r g n").bitcast(I32),
             )
-        nc.sync.dma_start(out=x_tiles[0][:, 1:NT, :], in_=xv[0][:, 1:NT, :])
-        nc.sync.dma_start(out=scale_p[:], in_=x_scale.rearrange("a b (g p c) -> p (a b g) c", p=P, c=4))
+        nc.sync.dma_start(out=x_tiles[0][:, 2:NT, :], in_=xv[0][:, 2:NT, :])
         nc.sync.dma_start(out=x_tiles[1][:], in_=xv[1])
         nc.sync.dma_start(out=k_tiles[0][0:SHIFT, 0, :], in_=kflat[B * S - SHIFT : B * S, :])
         nc.sync.dma_start(out=k_tiles[0][SHIFT:P, 0, :], in_=kflat[0 : P - SHIFT, :])
@@ -87,12 +91,14 @@ def tile_localattention_pa_t_w4_kernel(tc, x_bytes, x_scale, Wq_words, Wq_scales
             out=k_tiles[0][:, 1:NT, :], in_=kflat[P - SHIFT : S - SHIFT, :].rearrange("(i p) e -> p i e", p=P)
         )
         nc.sync.dma_start(out=bias[:], in_=bq.rearrange("(p t) -> p t", t=4))
-        load_k(1)
         for b in range(2, B):
             nc.sync.dma_start(out=x_tiles[b][:], in_=xv[b])
-            load_k(b)
+            load_k(b - 1)
+        load_k(B - 1)
 
-        make_identity(nc, ident[:])
+        nc.vector.memset(ident[:], 0.0)
+        nc.vector.memset(band[:], 0.0)
+        make_identity(nc, ident[:], nomemset=True)
         for j in range(2):
             nc.vector.memset(qc[j][:].bitcast(I32).rearrange("p (i u n) -> p i u n", i=NT, u=3)[:, :, 1, :], 0)
             nc.vector.memset(qsc[j][:].bitcast(I32).rearrange("p (i u n) -> p i u n", i=NT, u=3)[:, :, 1, :], 0)
@@ -102,7 +108,6 @@ def tile_localattention_pa_t_w4_kernel(tc, x_bytes, x_scale, Wq_words, Wq_scales
                 out=oflat[b].rearrange("(p r n) -> p r n", p=P, r=2), in_=zeros[:].unsqueeze(1).to_broadcast([P, 2, 2 * S])
             )
 
-        nc.gpsimd.memset(band[:], 0.0)
         nc.gpsimd.affine_select(
             out=band[:], in_=band[:], pattern=[[1, Q + STRIP]], compare_op=ALU.is_ge, fill=MASKED,
             base=HALF - MARGIN, channel_multiplier=-1,
@@ -111,6 +116,9 @@ def tile_localattention_pa_t_w4_kernel(tc, x_bytes, x_scale, Wq_words, Wq_scales
             out=band[:], in_=band[:], pattern=[[-1, Q + STRIP]], compare_op=ALU.is_ge, fill=MASKED,
             base=HALF + MARGIN, channel_multiplier=1,
         )
+
+        for strip in strips:
+            nc.gpsimd.memset(strip[:], 0.0)
 
         def build_mask():
             for s in range(2):
@@ -129,24 +137,24 @@ def tile_localattention_pa_t_w4_kernel(tc, x_bytes, x_scale, Wq_words, Wq_scales
             )
 
         def permute_scales():
-            nc.vector.tensor_copy(
+            nc.gpsimd.tensor_copy(
                 out=ws_perm[:].rearrange("p g (t m) -> p g t m", t=4),
                 in_=ws_raw[:].rearrange("p g (m t) -> p g t m", t=4),
             )
 
         def widen_head(b, i):
             xw[b, i] = x_head[i // 2][:, D * (i % 2) : D * (i % 2 + 1)]
-            codes = x_first[:] if (b, i) == (0, 0) else x_tiles[b][:, i, :]
+            codes = x_first[i][:] if b == 0 and i < 2 else x_tiles[b][:, i, :]
             nc.scalar.activation(out=xw[b, i], in_=codes.bitcast(FP8), func=ACT.Copy)
 
-        def widen(b, pair):
-            if pair == 1:
-                room = xi[(b - 1) % 2][:, 0 : 2 * D]
+        def widen(b, pair, n=2):
+            if pair == 0:
+                room = xi[b % 2][:, 0 : 2 * D] if b > 1 else x_head[0][:]
             else:
-                room = (x_head[0][:], xi[0][:, 0 : 2 * D])[b - 1] if b < 3 else qi[(b - 3) % 2][:]
-            for j in range(2):
+                room = qi[(b - 3) % 2][:] if b > 2 else kt[0][:, 0 : n * D]
+            for j in range(n):
                 xw[b, 2 * pair + j] = room[:, D * j : D * (j + 1)]
-            codes = x_tiles[b][:, 2 * pair : 2 * pair + 2, :].rearrange("p i k -> p (i k)")
+            codes = x_tiles[b][:, 2 * pair : 2 * pair + n, :].rearrange("p i k -> p (i k)")
             nc.gpsimd.tensor_copy(out=room, in_=codes.bitcast(FP8))
 
         def turn_x(b, i):
@@ -156,24 +164,23 @@ def tile_localattention_pa_t_w4_kernel(tc, x_bytes, x_scale, Wq_words, Wq_scales
                 for h in range(2):
                     nc.tensor.transpose(xt[b, i][:, h, g, :], words[:, 256 * g + h : 256 * (g + 1) : 2], ident[:])
 
-        def scale_x(b, i, dst):
-            values = xt[b, i][:].bitcast(BF16).rearrange("p h g (r e) -> p g r h e", e=2)
-            scales = scale_p[:].rearrange("p g (h e) -> p g h e", e=2).unsqueeze(2).to_broadcast([P, G, P, 2, 2])
+        def scale_x(b, i, dst, passes=G):
+            values = xt[b, i][:].bitcast(BF16).rearrange("p h g (r e) -> p g r h e", e=2)[:, 0:passes]
+            scales = scale_p[:, 0:passes].rearrange("p g (h e) -> p g h e", e=2).unsqueeze(2).to_broadcast([P, passes, P, 2, 2])
             nc.vector.tensor_tensor(out=dst, in0=values, in1=scales, op=ALU.mult)
 
-        def empty_x(b, i):
+        def empty_x(b, i, passes=G):
             rows = xi[b % 2][:].rearrange("p (g n h e) -> p g n h e", g=G, h=2, e=2)
-            scale_x(b, i, rows[:, :, P * i : P * (i + 1)])
+            scale_x(b, i, rows[:, 0:passes, P * i : P * (i + 1)], passes)
 
-        def empty_x_scalar(b, i, dst=None):
-            if dst is None:
-                dst = xi[b % 2][:].bitcast(F32).rearrange("p (g n h) -> p g n h", g=G, h=2)[:, :, P * i : P * (i + 1)]
-            planes = work.tile([P, 2, G, P], F32, name="x_planes", align_bytes=64)
+        def empty_x_scalar(b, i, first):
+            dst = xi[b % 2][:].bitcast(F32).rearrange("p (g n h) -> p g n h", g=G, h=2)[:, first:G, P * i : P * (i + 1)]
+            planes = work.tile([P, 2, G - first, P], F32, name="x_planes", align_bytes=64)
             for e in range(2):
                 for h in range(2):
-                    for g in range(G):
+                    for g in range(first, G):
                         nc.scalar.activation(
-                            out=planes[:, h, g, :].bitcast(BF16)[:, e::2],
+                            out=planes[:, h, g - first, :].bitcast(BF16)[:, e::2],
                             in_=xt[b, i][:, h, g, :].bitcast(BF16)[:, e::2],
                             func=ACT.Copy,
                             scale=scale_p[:, g, 2 * h + e : 2 * h + e + 1],
@@ -253,10 +260,10 @@ def tile_localattention_pa_t_w4_kernel(tc, x_bytes, x_scale, Wq_words, Wq_scales
                     )
 
         def mask_scores(b, i0=0, n=NT):
-            sm[b, i0] = work.tile([P, n, STRIP], F32, name="sm", bufs=4)
-            window = sc[b, i0][:, :, SHIFT - MARGIN : SHIFT - MARGIN + STRIP]
+            sm[b, i0] = work.tile([P, n, WIDTH], F32, name="sm", bufs=4)
+            window = sc[b, i0][:, :, SHIFT - HALF : SHIFT - HALF + WIDTH]
             nc.vector.scalar_tensor_tensor(
-                out=sm[b, i0][:], in0=window, scalar=SCALE, in1=mask[:, i0 : i0 + n, :], op0=ALU.mult, op1=ALU.add
+                out=sm[b, i0][:], in0=window, scalar=SCALE, in1=mask[:, i0 : i0 + n, LIVE], op0=ALU.mult, op1=ALU.add
             )
 
         def row_max(b, i0=0, n=NT):
@@ -291,11 +298,11 @@ def tile_localattention_pa_t_w4_kernel(tc, x_bytes, x_scale, Wq_words, Wq_scales
             if last:
                 nc.sync.dma_start(out=out[b, S - Q : S, S - STRIP + MARGIN : S], in_=strip[Q:P, n - 1, 0 : STRIP - MARGIN])
 
-        def finish(b, i0=0, n=NT, eng="s"):
-            strip = work.tile([P, n, STRIP], F32, name="strip", bufs=4)
+        def finish(b, i0=0, n=NT, eng="s", last=True):
+            strip = strips[b % 3][:, i0 : i0 + n, LIVE]
             if eng == "v":
                 nc.vector.tensor_tensor(
-                    out=strip[:], in0=sm[b, i0][:], in1=rs[b, i0][:].unsqueeze(2).to_broadcast([P, n, STRIP]), op=ALU.mult
+                    out=strip, in0=sm[b, i0][:], in1=rs[b, i0][:].unsqueeze(2).to_broadcast([P, n, WIDTH]), op=ALU.mult
                 )
             for i in range(n):
                 if eng == "s":
@@ -304,7 +311,8 @@ def tile_localattention_pa_t_w4_kernel(tc, x_bytes, x_scale, Wq_words, Wq_scales
                     nc.gpsimd.tensor_scalar(
                         out=strip[:, i, :], in0=sm[b, i0][:, i, :], scalar1=rs[b, i0][:, i : i + 1], scalar2=0.0, op0=ALU.mult, op1=ALU.add
                     )
-            store(b, strip, i0, n)
+            if last:
+                store(b, strips[b % 3], 0, NT)
 
         L = B - 1
         tx, tc_, ts, tacc, tq = {}, {}, {}, {}, {}
@@ -437,22 +445,24 @@ def tile_localattention_pa_t_w4_kernel(tc, x_bytes, x_scale, Wq_words, Wq_scales
         turn_x(1, 2)
         empty_x(1, 0)
         empty_q(0, 0)
-        project(0, 1)
         turn_x(1, 3)
+        project(0, 1)
         empty_x(1, 1)
+        quant_k(0)
+        widen(2, 1, 1)
+        widen_head(2, 3)
         empty_q(0, 1)
         project(0, 2)
-        turn_x(2, 0)
+        turn_k(1, 0)
         empty_x(1, 2)
         empty_q(0, 2)
         project(0, 3)
-        turn_k(1, 0)
-        turn_x(2, 1)
+        turn_x(2, 0)
         empty_x(1, 3)
         empty_q(0, 3)
         empty_k(1, 0)
         turn_k(1, 1)
-        quant_k(0)
+        turn_x(2, 1)
         weave_q(0)
         empty_k(1, 1)
         halves = {2: (4, 5), 3: (6, 7, 8), 4: (9, 10, 11), 5: (12, 13), 6: (14, 15)}
@@ -461,48 +471,46 @@ def tile_localattention_pa_t_w4_kernel(tc, x_bytes, x_scale, Wq_words, Wq_scales
             if n == 5:
                 quant_k(4)
             quant_x(n - 1)
-            widen(n, 1)
-            step(exps, n - 3)
+            widen(n + 1, 0)
             if n > 2:
-                turn_x(n, 0)
-                project(n - 2, 3)
-                turn_x(n, 1)
                 empty_q(n - 2, 3)
+            step(exps, n - 3)
+            project(n - 1, 0)
             empty_x(n, 0)
             if n > 2:
                 weave_q(n - 2)
-            project(n - 1, 0)
-            turn_k(*keys[0])
+            turn_x(n, 2)
             empty_q(n - 1, 0)
+            project(n - 1, 1)
             empty_x(n, 1)
             step(recip, n - 3)
-            project(n - 1, 1)
+            turn_x(n, 3)
             step(finish, n - 3)
-            turn_x(n, 2)
             quant_q(n - 2)
             quant_k(n - 1 if n < 5 else n)
-            widen(n + 1, 0)
-            empty_k(*keys[0])
+            widen(n + 1, 1)
             empty_q(n - 1, 1)
+            project(n - 1, 2)
             scores(n - 2)
             empty_x(n, 2)
-            turn_x(n, 3)
-            project(n - 1, 2)
-            mask_scores(n - 2)
-            empty_x(n, 3)
-            for key in keys[1:]:
+            for key in keys[:2]:
                 turn_k(*key)
+            mask_scores(n - 2)
             empty_q(n - 1, 2)
-            row_max(n - 2)
-            for key in keys[1:]:
+            for key in keys[:2]:
                 empty_k(*key)
+            empty_x(n, 3)
+            for key in keys[2:]:
+                turn_k(*key)
+            project(n - 1, 3)
+            for key in keys[2:]:
+                empty_k(*key)
+            turn_x(n + 1, 0)
+            turn_x(n + 1, 1)
+            row_max(n - 2)
         quant_x(L - 1)
-        widen(L, 1)
-        exps(L - 3)
-        turn_x(L, 0)
-        project(L - 2, 3)
-        turn_x(L, 1)
         empty_q(L - 2, 3)
+        exps(L - 3)
         h_empty_x(0)
         weave_q(L - 2)
         project(L - 1, 0)
@@ -535,30 +543,30 @@ def tile_localattention_pa_t_w4_kernel(tc, x_bytes, x_scale, Wq_words, Wq_scales
         h_empty_q()
         exps(L - 2)
         t_project(3)
+        t_empty_q(2)
         quant_q(L - 1)
         scores(L - 1)
-        t_empty_q(2)
         h_weave_q()
-        mask_scores(L - 1)
         t_empty_q(3)
-        row_max(L - 1)
         recip(L - 2)
         finish(L - 2)
-        exps(L - 1)
         t_quant_q(2)
         t_quant_q(3)
         scores(L, 2, 2, "tp", 4)
         h_quant_q()
         scores(L, 0, 2, "tp", 4)
+        mask_scores(L - 1)
         mask_scores(L, 2, 2)
-        recip(L - 1)
-        finish(L - 1)
-        row_max(L, 2, 2)
-        exps(L, 2, 2)
+        row_max(L - 1)
+        exps(L - 1)
         mask_scores(L, 0, 2)
+        row_max(L, 2, 2)
         row_max(L, 0, 2)
+        exps(L, 2, 2)
         exps(L, 0, 2)
+        recip(L - 1)
+        finish(L - 1, 0, NT, "v")
         recip(L, 2, 2)
-        finish(L, 2, 2, "v")
+        finish(L, 2, 2, "s", False)
         recip(L, 0, 2)
         finish(L, 0, 2, "v")

@@ -55,7 +55,7 @@ def tile_localattention_pa_t_w4_kernel(tc, x_bytes, x_scale, Wq_words, Wq_scales
         bias = keep.tile([P, 4], BF16, name="bias")
         band = keep.tile([P, Q + STRIP], F32, name="band")
         mask = keep.tile([P, NT, STRIP], F32, name="mask")
-        zeros = keep.tile([P, 2 * S], F32, name="zeros")
+        zeros = keep.tile([P, S], F32, name="zeros")
         kc = keep.tile([P, B * S + Q], U32, name="kc", align_bytes=64)
         ksc = keep.tile([P, B * S + Q], U8, name="ksc", align_bytes=64)
         qc = [keep.tile([P, NT * 3 * Q], U32, name=f"qc{j}", align_bytes=64) for j in range(2)]
@@ -78,12 +78,12 @@ def tile_localattention_pa_t_w4_kernel(tc, x_bytes, x_scale, Wq_words, Wq_scales
         nc.sync.dma_start(out=scale_p[:], in_=x_scale.rearrange("a b (g p c) -> p (a b g) c", p=P, c=4))
         nc.sync.dma_start(out=w_raw[:].bitcast(I32), in_=Wq_words.rearrange("g p n -> p g n").bitcast(I32))
         nc.sync.dma_start(out=x_first[1][:], in_=xv[0][:, 1, :])
+        nc.sync.dma_start(out=x_tiles[0][:, 2:NT, :], in_=xv[0][:, 2:NT, :])
         for q in range(4):
             nc.sync.dma_start(
                 out=ws_raw[32 * q : 32 * q + 4].bitcast(I32),
                 in_=Wq_scales[:, 4 * q : 4 * q + 4, :].rearrange("g r n -> r g n").bitcast(I32),
             )
-        nc.sync.dma_start(out=x_tiles[0][:, 2:NT, :], in_=xv[0][:, 2:NT, :])
         nc.sync.dma_start(out=x_tiles[1][:], in_=xv[1])
         nc.sync.dma_start(out=k_tiles[0][0:SHIFT, 0, :], in_=kflat[B * S - SHIFT : B * S, :])
         nc.sync.dma_start(out=k_tiles[0][SHIFT:P, 0, :], in_=kflat[0 : P - SHIFT, :])
@@ -103,9 +103,11 @@ def tile_localattention_pa_t_w4_kernel(tc, x_bytes, x_scale, Wq_words, Wq_scales
             nc.vector.memset(qc[j][:].bitcast(I32).rearrange("p (i u n) -> p i u n", i=NT, u=3)[:, :, 1, :], 0)
             nc.vector.memset(qsc[j][:].bitcast(I32).rearrange("p (i u n) -> p i u n", i=NT, u=3)[:, :, 1, :], 0)
         nc.vector.memset(zeros[:], 0.0)
+        for strip in strips:
+            nc.vector.memset(strip[:], 0.0)
         for b in range(B):
             nc.sync.dma_start(
-                out=oflat[b].rearrange("(p r n) -> p r n", p=P, r=2), in_=zeros[:].unsqueeze(1).to_broadcast([P, 2, 2 * S])
+                out=oflat[b].rearrange("(p r n) -> p r n", p=P, r=NT), in_=zeros[:].unsqueeze(1).to_broadcast([P, NT, S])
             )
 
         nc.gpsimd.affine_select(
@@ -116,9 +118,6 @@ def tile_localattention_pa_t_w4_kernel(tc, x_bytes, x_scale, Wq_words, Wq_scales
             out=band[:], in_=band[:], pattern=[[-1, Q + STRIP]], compare_op=ALU.is_ge, fill=MASKED,
             base=HALF + MARGIN, channel_multiplier=1,
         )
-
-        for strip in strips:
-            nc.gpsimd.memset(strip[:], 0.0)
 
         def build_mask():
             for s in range(2):
@@ -454,6 +453,7 @@ def tile_localattention_pa_t_w4_kernel(tc, x_bytes, x_scale, Wq_words, Wq_scales
         empty_q(0, 1)
         project(0, 2)
         turn_k(1, 0)
+        turn_k(1, 1)
         empty_x(1, 2)
         empty_q(0, 2)
         project(0, 3)
@@ -461,33 +461,30 @@ def tile_localattention_pa_t_w4_kernel(tc, x_bytes, x_scale, Wq_words, Wq_scales
         empty_x(1, 3)
         empty_q(0, 3)
         empty_k(1, 0)
-        turn_k(1, 1)
         turn_x(2, 1)
         weave_q(0)
         empty_k(1, 1)
-        halves = {2: (4, 5), 3: (6, 7, 8), 4: (9, 10, 11), 5: (12, 13), 6: (14, 15)}
+        halves = {n: (2 * n, 2 * n + 1) for n in range(2, L)}
         for n in range(2, L):
             keys = [divmod(j, 2) for j in halves[n]]
-            if n == 5:
-                quant_k(4)
             quant_x(n - 1)
             widen(n + 1, 0)
             if n > 2:
                 empty_q(n - 2, 3)
             step(exps, n - 3)
             project(n - 1, 0)
+            project(n - 1, 1)
             empty_x(n, 0)
             if n > 2:
                 weave_q(n - 2)
             turn_x(n, 2)
+            turn_x(n, 3)
             empty_q(n - 1, 0)
-            project(n - 1, 1)
             empty_x(n, 1)
             step(recip, n - 3)
-            turn_x(n, 3)
             step(finish, n - 3)
             quant_q(n - 2)
-            quant_k(n - 1 if n < 5 else n)
+            quant_k(n - 1)
             widen(n + 1, 1)
             empty_q(n - 1, 1)
             project(n - 1, 2)
@@ -522,10 +519,13 @@ def tile_localattention_pa_t_w4_kernel(tc, x_bytes, x_scale, Wq_words, Wq_scales
         project(L - 1, 1)
         turn_x(L, 2)
         quant_q(L - 2)
+        quant_k(L - 1)
         h_quant_x()
         turn_x(L, 3)
         project(L - 1, 3)
         scores(L - 2)
+        turn_k(L, 0)
+        turn_k(L, 1)
         t_empty_x(2)
         empty_q(L - 1, 1)
         h_project(0)
@@ -537,6 +537,8 @@ def tile_localattention_pa_t_w4_kernel(tc, x_bytes, x_scale, Wq_words, Wq_scales
         t_project(2)
         mask_scores(L - 2)
         finish(L - 3)
+        empty_k(L, 0)
+        empty_k(L, 1)
         weave_q(L - 1)
         quant_k(L)
         row_max(L - 2)

@@ -288,14 +288,15 @@ def tile_localattention_pa_t_w4_kernel(tc, x_bytes, x_scale, Wq_words, Wq_scales
 
         def store(b, strip, i0, n):
             first, last = i0 == 0, i0 + n == NT
-            if first:
-                nc.sync.dma_start(out=out[b, 0:Q, 0 : STRIP - MARGIN], in_=strip[0:Q, 0, MARGIN:STRIP])
+            other = nc.scalar if b == B - 1 else nc.sync
             if n > first:
                 nc.sync.dma_start(out=strip_rows(b, i0 + first, n - first, 0), in_=strip[0:Q, first:n, :])
             if n > last:
-                nc.sync.dma_start(out=strip_rows(b, i0, n - last, 1), in_=strip[Q:P, 0 : n - last, :])
+                other.dma_start(out=strip_rows(b, i0, n - last, 1), in_=strip[Q:P, 0 : n - last, :])
+            if first:
+                nc.sync.dma_start(out=out[b, 0:Q, 0 : STRIP - MARGIN], in_=strip[0:Q, 0, MARGIN:STRIP])
             if last:
-                nc.sync.dma_start(out=out[b, S - Q : S, S - STRIP + MARGIN : S], in_=strip[Q:P, n - 1, 0 : STRIP - MARGIN])
+                other.dma_start(out=out[b, S - Q : S, S - STRIP + MARGIN : S], in_=strip[Q:P, n - 1, 0 : STRIP - MARGIN])
 
         def finish(b, i0=0, n=NT, eng="s", last=True):
             strip = strips[b % 3][:, i0 : i0 + n, LIVE]
@@ -427,7 +428,6 @@ def tile_localattention_pa_t_w4_kernel(tc, x_bytes, x_scale, Wq_words, Wq_scales
         widen_head(1, 3)
         empty_x(0, 0)
         empty_x(0, 1)
-        warm_up()
         turn_k(0, 0)
         turn_k(0, 1)
         empty_k(0, 0)
@@ -457,16 +457,14 @@ def tile_localattention_pa_t_w4_kernel(tc, x_bytes, x_scale, Wq_words, Wq_scales
         empty_x(1, 2)
         empty_q(0, 2)
         project(0, 3)
+        empty_k(1, 0)
+        empty_k(1, 1)
         turn_x(2, 0)
         empty_x(1, 3)
         empty_q(0, 3)
-        empty_k(1, 0)
         turn_x(2, 1)
         weave_q(0)
-        empty_k(1, 1)
-        halves = {n: (2 * n, 2 * n + 1) for n in range(2, L)}
         for n in range(2, L):
-            keys = [divmod(j, 2) for j in halves[n]]
             quant_x(n - 1)
             widen(n + 1, 0)
             if n > 2:
@@ -483,25 +481,21 @@ def tile_localattention_pa_t_w4_kernel(tc, x_bytes, x_scale, Wq_words, Wq_scales
             empty_x(n, 1)
             step(recip, n - 3)
             step(finish, n - 3)
-            quant_q(n - 2)
             quant_k(n - 1)
+            quant_q(n - 2)
             widen(n + 1, 1)
             empty_q(n - 1, 1)
             project(n - 1, 2)
             scores(n - 2)
             empty_x(n, 2)
-            for key in keys[:2]:
-                turn_k(*key)
+            turn_k(n, 0)
+            turn_k(n, 1)
             mask_scores(n - 2)
             empty_q(n - 1, 2)
-            for key in keys[:2]:
-                empty_k(*key)
+            empty_k(n, 0)
+            empty_k(n, 1)
             empty_x(n, 3)
-            for key in keys[2:]:
-                turn_k(*key)
             project(n - 1, 3)
-            for key in keys[2:]:
-                empty_k(*key)
             turn_x(n + 1, 0)
             turn_x(n + 1, 1)
             row_max(n - 2)
@@ -518,8 +512,8 @@ def tile_localattention_pa_t_w4_kernel(tc, x_bytes, x_scale, Wq_words, Wq_scales
         empty_q(L - 1, 2)
         project(L - 1, 1)
         turn_x(L, 2)
-        quant_q(L - 2)
         quant_k(L - 1)
+        quant_q(L - 2)
         h_quant_x()
         turn_x(L, 3)
         project(L - 1, 3)

@@ -31,6 +31,7 @@ LIVE = slice(MARGIN - HALF, STRIP - MARGIN + HALF)
 WIDTH = Q + 2 * HALF
 MASKED = -1e9
 SCALE = 1.0 / math.sqrt(E)
+L = B - 1
 
 
 def tile_localattention_pa_t_w4_kernel(tc, x_bytes, x_scale, Wq_words, Wq_scales, bq, k, out):
@@ -43,12 +44,11 @@ def tile_localattention_pa_t_w4_kernel(tc, x_bytes, x_scale, Wq_words, Wq_scales
 
         ident = keep.tile([P, P], F32, name="ident")
         scale_p = keep.tile([P, G, 4], F32, name="scale_p")
-        xi = [keep.tile([P, G * S * 4], BF16, name=f"xi{j}", align_bytes=64) for j in range(2)]
+        ring = [keep.tile([P, NT * D], BF16, name=f"ring{j}", align_bytes=64) for j in range(3)]
         qi = [keep.tile([P, S * 4], BF16, name=f"qi{j}", align_bytes=64) for j in range(2)]
         kt = [keep.tile([P, S * 4], BF16, name=f"kt{j}", align_bytes=64) for j in range(3)]
-        strips = [keep.tile([P, NT, STRIP], F32, name=f"strip{j}") for j in range(3)]
-        x_head = [keep.tile([P, 2 * D], BF16, name=f"x_head{j}", align_bytes=64) for j in range(2)]
-        w_raw = keep.tile([P, G, 2 * E], U8, name="w_raw", align_bytes=64)
+        strips = keep.tile([P, B, NT, STRIP], F32, name="strips")
+        w_raw = [keep.tile([P, 2 * E], U8, name=f"w_raw{g}", align_bytes=64) for g in range(G)]
         w_perm = keep.tile([P, G, 2 * E], U8, name="w_perm", align_bytes=64)
         ws_raw = keep.tile([P, G, E], U8, name="ws_raw", align_bytes=64)
         ws_perm = keep.tile([P, G, E], U8, name="ws_perm", align_bytes=64)
@@ -75,9 +75,10 @@ def tile_localattention_pa_t_w4_kernel(tc, x_bytes, x_scale, Wq_words, Wq_scales
 
         nc.vector.memset(ws_raw[:].rearrange("p g n -> p (g n)").bitcast(I32), 0)
         nc.sync.dma_start(out=x_first[0][:], in_=xv[0][:, 0, :])
-        nc.sync.dma_start(out=scale_p[:], in_=x_scale.rearrange("a b (g p c) -> p (a b g) c", p=P, c=4))
-        nc.sync.dma_start(out=w_raw[:].bitcast(I32), in_=Wq_words.rearrange("g p n -> p g n").bitcast(I32))
         nc.sync.dma_start(out=x_first[1][:], in_=xv[0][:, 1, :])
+        for g in range(G):
+            nc.sync.dma_start(out=w_raw[g][:].bitcast(I32), in_=Wq_words[g].bitcast(I32))
+        nc.sync.dma_start(out=scale_p[:], in_=x_scale.rearrange("a b (g p c) -> p (a b g) c", p=P, c=4))
         nc.sync.dma_start(out=x_tiles[0][:, 2:NT, :], in_=xv[0][:, 2:NT, :])
         for q in range(4):
             nc.sync.dma_start(
@@ -86,7 +87,8 @@ def tile_localattention_pa_t_w4_kernel(tc, x_bytes, x_scale, Wq_words, Wq_scales
             )
         nc.sync.dma_start(out=x_tiles[1][:], in_=xv[1])
         nc.sync.dma_start(out=k_tiles[0][0:SHIFT, 0, :], in_=kflat[B * S - SHIFT : B * S, :])
-        nc.sync.dma_start(out=k_tiles[0][SHIFT:P, 0, :], in_=kflat[0 : P - SHIFT, :])
+        nc.sync.dma_start(out=k_tiles[0][SHIFT:Q, 0, :], in_=kflat[0:SHIFT, :])
+        nc.sync.dma_start(out=k_tiles[0][Q:P, 0, :], in_=kflat[SHIFT : P - SHIFT, :])
         nc.sync.dma_start(
             out=k_tiles[0][:, 1:NT, :], in_=kflat[P - SHIFT : S - SHIFT, :].rearrange("(i p) e -> p i e", p=P)
         )
@@ -94,30 +96,27 @@ def tile_localattention_pa_t_w4_kernel(tc, x_bytes, x_scale, Wq_words, Wq_scales
         for b in range(2, B):
             nc.sync.dma_start(out=x_tiles[b][:], in_=xv[b])
             load_k(b - 1)
-        load_k(B - 1)
+        load_k(L)
 
         nc.vector.memset(ident[:], 0.0)
-        nc.vector.memset(band[:], 0.0)
+        nc.vector.memset(zeros[:], 0.0)
         make_identity(nc, ident[:], nomemset=True)
+        nc.vector.memset(band[:], 0.0)
         for j in range(2):
             nc.vector.memset(qc[j][:].bitcast(I32).rearrange("p (i u n) -> p i u n", i=NT, u=3)[:, :, 1, :], 0)
             nc.vector.memset(qsc[j][:].bitcast(I32).rearrange("p (i u n) -> p i u n", i=NT, u=3)[:, :, 1, :], 0)
-        nc.vector.memset(zeros[:], 0.0)
-        for strip in strips:
-            nc.vector.memset(strip[:], 0.0)
+        for margin in (slice(0, LIVE.start), slice(LIVE.stop, STRIP)):
+            nc.vector.memset(strips[:].rearrange("p j i c -> p (j i) c")[:, :, margin], 0.0)
         for b in range(B):
             nc.sync.dma_start(
                 out=oflat[b].rearrange("(p r n) -> p r n", p=P, r=NT), in_=zeros[:].unsqueeze(1).to_broadcast([P, NT, S])
             )
 
-        nc.gpsimd.affine_select(
-            out=band[:], in_=band[:], pattern=[[1, Q + STRIP]], compare_op=ALU.is_ge, fill=MASKED,
-            base=HALF - MARGIN, channel_multiplier=-1,
-        )
-        nc.gpsimd.affine_select(
-            out=band[:], in_=band[:], pattern=[[-1, Q + STRIP]], compare_op=ALU.is_ge, fill=MASKED,
-            base=HALF + MARGIN, channel_multiplier=1,
-        )
+        def cut_band(side):
+            nc.gpsimd.affine_select(
+                out=band[:], in_=band[:], pattern=[[side, Q + STRIP]], compare_op=ALU.is_ge, fill=MASKED,
+                base=HALF - side * MARGIN, channel_multiplier=-side,
+            )
 
         def build_mask():
             for s in range(2):
@@ -126,14 +125,15 @@ def tile_localattention_pa_t_w4_kernel(tc, x_bytes, x_scale, Wq_words, Wq_scales
             nc.scalar.copy(out=mask[0:Q, 0, 0:MARGIN], in_=band[0:Q, Q + STRIP - MARGIN : Q + STRIP])
             nc.scalar.copy(out=mask[Q:P, NT - 1, STRIP - MARGIN : STRIP], in_=band[Q:P, 0:MARGIN])
 
-        xw, xt, xc, xsc, ktp, acc, qp = {}, {}, {}, {}, {}, {}, {}
+        xt, xc, xsc, ktp, acc, qp = {}, {}, {}, {}, {}, {}
         sc, sm, nm, ss, rs = {}, {}, {}, {}, {}
 
         def permute_codes():
-            nc.vector.tensor_copy(
-                out=w_perm[:].rearrange("p g (t m c) -> p g t m c", t=4, c=2),
-                in_=w_raw[:].rearrange("p g (m t c) -> p g t m c", t=4, c=2),
-            )
+            for g in range(G):
+                nc.vector.tensor_copy(
+                    out=w_perm[:, g, :].rearrange("p (t m c) -> p t m c", t=4, c=2),
+                    in_=w_raw[g][:].rearrange("p (m t c) -> p t m c", t=4, c=2),
+                )
 
         def permute_scales():
             nc.gpsimd.tensor_copy(
@@ -141,57 +141,63 @@ def tile_localattention_pa_t_w4_kernel(tc, x_bytes, x_scale, Wq_words, Wq_scales
                 in_=ws_raw[:].rearrange("p g (m t) -> p g t m", t=4),
             )
 
-        def widen_head(b, i):
-            xw[b, i] = x_head[i // 2][:, D * (i % 2) : D * (i % 2 + 1)]
+        def wide(b, i, n=1):
+            return ring[(b + 1) % 3][:, D * i : D * (i + n)]
+
+        def widen_s(b, i):
             codes = x_first[i][:] if b == 0 and i < 2 else x_tiles[b][:, i, :]
-            nc.scalar.activation(out=xw[b, i], in_=codes.bitcast(FP8), func=ACT.Copy)
+            nc.scalar.activation(out=wide(b, i), in_=codes.bitcast(FP8), func=ACT.Copy)
 
-        def widen(b, pair, n=2):
-            if pair == 0:
-                room = xi[b % 2][:, 0 : 2 * D] if b > 1 else x_head[0][:]
-            else:
-                room = qi[(b - 3) % 2][:] if b > 2 else kt[0][:, 0 : n * D]
-            for j in range(n):
-                xw[b, 2 * pair + j] = room[:, D * j : D * (j + 1)]
-            codes = x_tiles[b][:, 2 * pair : 2 * pair + n, :].rearrange("p i k -> p (i k)")
-            nc.gpsimd.tensor_copy(out=room, in_=codes.bitcast(FP8))
+        def widen_v(b, i):
+            nc.vector.tensor_copy(out=wide(b, i), in_=x_first[i][:].bitcast(FP8))
 
-        def turn_x(b, i):
-            words = xw[b, i].bitcast(F32)
-            xt[b, i] = psum.tile([P, 2, G, P], F32, name="tp", bufs=4)
-            for g in range(G):
+        def widen(b, i0=0, n=NT):
+            codes = x_tiles[b][:, i0 : i0 + n, :].rearrange("p i k -> p (i k)")
+            nc.gpsimd.tensor_copy(out=wide(b, i0, n), in_=codes.bitcast(FP8))
+
+        def turn_x(b, i, passes=range(G)):
+            words = wide(b, i).bitcast(F32)
+            if (b, i) not in xt:
+                xt[b, i] = psum.tile([P, 2, G, P], F32, name="tp", bufs=4)
+            for g in passes:
                 for h in range(2):
                     nc.tensor.transpose(xt[b, i][:, h, g, :], words[:, 256 * g + h : 256 * (g + 1) : 2], ident[:])
 
-        def scale_x(b, i, dst, passes=G):
-            values = xt[b, i][:].bitcast(BF16).rearrange("p h g (r e) -> p g r h e", e=2)[:, 0:passes]
-            scales = scale_p[:, 0:passes].rearrange("p g (h e) -> p g h e", e=2).unsqueeze(2).to_broadcast([P, passes, P, 2, 2])
+        def woven_x(b):
+            return ring[b % 3][:]
+
+        def rows_x(b, i0, n):
+            room = woven_x(b)[:, G * 4 * P * i0 : G * 4 * P * (i0 + n)]
+            return room.rearrange("p (g n h e) -> p g n h e", g=G, h=2, e=2)
+
+        def empty_x(b, i, i0=0, n=NT, g0=0, g1=G):
+            dst = rows_x(b, i0, n)[:, g0:g1, P * (i - i0) : P * (i - i0 + 1)]
+            values = xt[b, i][:].bitcast(BF16).rearrange("p h g (r e) -> p g r h e", e=2)[:, g0:g1]
+            scales = scale_p[:, g0:g1].rearrange("p g (h e) -> p g h e", e=2).unsqueeze(2).to_broadcast([P, g1 - g0, P, 2, 2])
             nc.vector.tensor_tensor(out=dst, in0=values, in1=scales, op=ALU.mult)
 
-        def empty_x(b, i, passes=G):
-            rows = xi[b % 2][:].rearrange("p (g n h e) -> p g n h e", g=G, h=2, e=2)
-            scale_x(b, i, rows[:, 0:passes, P * i : P * (i + 1)], passes)
-
-        def empty_x_scalar(b, i, first):
-            dst = xi[b % 2][:].bitcast(F32).rearrange("p (g n h) -> p g n h", g=G, h=2)[:, first:G, P * i : P * (i + 1)]
-            planes = work.tile([P, 2, G - first, P], F32, name="x_planes", align_bytes=64)
+        def empty_x_s(b, i, g, i0=0, n=NT):
+            dst = rows_x(b, i0, n)[:, g, P * (i - i0) : P * (i - i0 + 1)].rearrange("p n h e -> p (n h e)")
+            planes = work.tile([P, 2, P], F32, name="x_planes", align_bytes=64)
             for e in range(2):
                 for h in range(2):
-                    for g in range(first, G):
-                        nc.scalar.activation(
-                            out=planes[:, h, g - first, :].bitcast(BF16)[:, e::2],
-                            in_=xt[b, i][:, h, g, :].bitcast(BF16)[:, e::2],
-                            func=ACT.Copy,
-                            scale=scale_p[:, g, 2 * h + e : 2 * h + e + 1],
-                        )
-            nc.scalar.copy(out=dst, in_=planes[:].rearrange("p h g r -> p g r h"))
+                    nc.scalar.activation(
+                        out=planes[:, h, :].bitcast(BF16)[:, e::2],
+                        in_=xt[b, i][:, h, g, :].bitcast(BF16)[:, e::2],
+                        func=ACT.Copy,
+                        scale=scale_p[:, g, 2 * h + e : 2 * h + e + 1],
+                    )
+            nc.scalar.copy(out=dst.bitcast(F32).rearrange("p (r h) -> p r h", h=2), in_=planes[:].rearrange("p h r -> p r h"))
 
-        def quant_x(b):
-            xc[b] = work.tile([P, G, S], U32, name="xc", align_bytes=64)
-            xsc[b] = work.tile([P, G, S], U8, name="xsc", align_bytes=64)
-            for g in range(G):
+        def quant_x(b, i0=0, n=NT, cuts=G):
+            if (b, 0) not in xc:
+                xc[b, 0] = work.tile([P, G * S], U32, name="xc", align_bytes=64)
+                xsc[b, 0] = work.tile([P, G * S], U8, name="xsc", align_bytes=64)
+            w = G * P * n // cuts
+            for g in range(cuts):
+                cols = slice(G * P * i0 + w * g, G * P * i0 + w * (g + 1))
                 nc.vector.quantize_mx(
-                    out=xc[b][:, g, :].bitcast(FP8X4), scales=xsc[b][:, g, :], in_=xi[b % 2][:, 4 * S * g : 4 * S * (g + 1)]
+                    out=xc[b, 0][:, cols].bitcast(FP8X4), scales=xsc[b, 0][:, cols], in_=woven_x(b)[:, 4 * cols.start : 4 * cols.stop]
                 )
 
         def turn_k(b, half):
@@ -211,36 +217,52 @@ def tile_localattention_pa_t_w4_kernel(tc, x_bytes, x_scale, Wq_words, Wq_scales
                 nc.vector.quantize_mx(out=kc[:, B * S :].bitcast(FP8X4), scales=ksc[:, B * S :], in_=rows[:, 0 : 4 * Q])
             nc.vector.quantize_mx(out=kc[:, S * b : S * (b + 1)].bitcast(FP8X4), scales=ksc[:, S * b : S * (b + 1)], in_=rows)
 
-        def project(b, t):
-            acc[b, t] = psum.tile([P, S], F32, name="acc", bufs=3)
-            for g in range(G):
+        def project(b, t, passes=range(G), i0=0, n=NT, tag="acc", bufs=3):
+            per = NT // n
+            if (b, i0, t // per) not in acc:
+                acc[b, i0, t // per] = psum.tile([P, per, n * P], F32, name=tag, bufs=bufs)
+            for g in passes:
+                cols = slice(G * P * i0 + n * P * g, G * P * i0 + n * P * (g + 1))
                 nc.tensor.matmul_mx(
-                    out=acc[b, t][:],
+                    out=acc[b, i0, t // per][:, t % per, :],
                     lhsT=w_perm[:, g, 256 * t : 256 * (t + 1)].bitcast(FP4X4),
                     lhsT_scale=ws_perm[:, g, P * t : P * (t + 1)],
-                    rhs=xc[b][:, g, :].bitcast(FP8X4),
-                    rhs_scale=xsc[b][:, g, :],
+                    rhs=xc[b, 0][:, cols].bitcast(FP8X4),
+                    rhs_scale=xsc[b, 0][:, cols],
                     start=(g == 0),
                     stop=(g == G - 1),
                 )
 
-        def empty_q(b, t):
-            if t == 0:
+        def empty_q(b, t, i0=0, n=NT):
+            if b not in qp:
                 qp[b] = work.tile([P, 2, S], F32, name="qp", align_bytes=64)
-            pair = qp[b][:, t // 2, :].bitcast(BF16)
-            nc.scalar.activation(out=pair[:, t % 2 :: 2], in_=acc[b, t][:], func=ACT.Identity, bias=bias[:, t : t + 1])
+            per = NT // n
+            pair = qp[b][:, t // 2, P * i0 : P * (i0 + n)].bitcast(BF16)
+            nc.scalar.activation(out=pair[:, t % 2 :: 2], in_=acc[b, i0, t // per][:, t % per, :], func=ACT.Identity, bias=bias[:, t : t + 1])
 
-        def weave_q(b):
-            dst = qi[b % 2][:].bitcast(F32).rearrange("p (n h) -> p n h", h=2)
-            nc.scalar.copy(out=dst, in_=qp[b][:].rearrange("p h n -> p n h"))
+        def rows_q(b):
+            return qi[b % 2][:]
 
-        def quant_q(b):
-            rows = qi[b % 2][:]
-            cuts = [0] + list(range(Q, S, P)) + [S]
+        def weave_q(b, i0=0, n=NT):
+            dst = rows_q(b)[:, 4 * P * i0 : 4 * P * (i0 + n)].bitcast(F32).rearrange("p (n h) -> p n h", h=2)
+            nc.scalar.copy(out=dst, in_=qp[b][:, :, P * i0 : P * (i0 + n)].rearrange("p h n -> p n h"))
+
+        def empty_q_v(b, i):
+            nc.vector.tensor_tensor(
+                out=rows_q(b)[:, 4 * P * i : 4 * P * (i + 1)].rearrange("p (n t) -> p n t", t=4),
+                in0=acc[b, i, 0][:].rearrange("p t n -> p n t"),
+                in1=bias[:].unsqueeze(1).to_broadcast([P, P, 4]),
+                op=ALU.add,
+            )
+
+        def quant_q(b, i0=0, n=NT):
+            cuts = [P * i0] + list(range(P * i0 + Q, P * (i0 + n), P)) + [P * (i0 + n)]
             for lo, hi in zip(cuts[:-1], cuts[1:]):
                 at = lo + Q * ((lo // Q + 1) // 2)
                 cols = slice(at, at + hi - lo)
-                nc.vector.quantize_mx(out=qc[b % 2][:, cols].bitcast(FP8X4), scales=qsc[b % 2][:, cols], in_=rows[:, 4 * lo : 4 * hi])
+                nc.vector.quantize_mx(
+                    out=qc[b % 2][:, cols].bitcast(FP8X4), scales=qsc[b % 2][:, cols], in_=rows_q(b)[:, 4 * lo : 4 * hi]
+                )
 
         def scores(b, i0=0, n=NT, tag="sc", bufs=1):
             sc[b, i0] = psum.tile([P, n, P], F32, name=tag, bufs=bufs)
@@ -259,24 +281,24 @@ def tile_localattention_pa_t_w4_kernel(tc, x_bytes, x_scale, Wq_words, Wq_scales
                     )
 
         def mask_scores(b, i0=0, n=NT):
-            sm[b, i0] = work.tile([P, n, WIDTH], F32, name="sm", bufs=4)
+            sm[b, i0] = work.tile([P, n, WIDTH], F32, name="sm", bufs=6)
             window = sc[b, i0][:, :, SHIFT - HALF : SHIFT - HALF + WIDTH]
             nc.vector.scalar_tensor_tensor(
                 out=sm[b, i0][:], in0=window, scalar=SCALE, in1=mask[:, i0 : i0 + n, LIVE], op0=ALU.mult, op1=ALU.add
             )
 
         def row_max(b, i0=0, n=NT):
-            nm[b, i0] = work.tile([P, n], F32, name="nm", bufs=4)
+            nm[b, i0] = work.tile([P, n], F32, name="nm", bufs=6)
             nc.vector.tensor_reduce(out=nm[b, i0][:], in_=sm[b, i0][:], axis=AX.X, op=ALU.max, negate=True)
 
         def exps(b, i0=0, n=NT):
-            ss[b, i0] = work.tile([P, n], F32, name="ss", bufs=4)
+            ss[b, i0] = work.tile([P, n], F32, name="ss", bufs=6)
             for i in range(n):
                 row = sm[b, i0][:, i, :]
                 nc.scalar.activation(out=row, in_=row, func=ACT.Exp, bias=nm[b, i0][:, i : i + 1], accum_out=ss[b, i0][:, i : i + 1])
 
         def recip(b, i0=0, n=NT):
-            rs[b, i0] = work.tile([P, n], F32, name="rs", bufs=4)
+            rs[b, i0] = work.tile([P, n], F32, name="rs", bufs=6)
             nc.vector.reciprocal(out=rs[b, i0][:], in_=ss[b, i0][:])
 
         def strip_rows(b, i0, n, s):
@@ -286,283 +308,199 @@ def tile_localattention_pa_t_w4_kernel(tc, x_bytes, x_scale, Wq_words, Wq_scales
             view = oflat[b][lo : lo + n * diag].rearrange("(i y) -> i y", i=n)[:, back : back + Q * S]
             return view.rearrange("i (r j) -> r i j", r=Q)[:, :, 0:STRIP]
 
-        def store(b, strip, i0, n):
-            first, last = i0 == 0, i0 + n == NT
-            other = nc.scalar if b == B - 1 else nc.sync
-            if n > first:
-                nc.sync.dma_start(out=strip_rows(b, i0 + first, n - first, 0), in_=strip[0:Q, first:n, :])
-            if n > last:
-                other.dma_start(out=strip_rows(b, i0, n - last, 1), in_=strip[Q:P, 0 : n - last, :])
-            if first:
-                nc.sync.dma_start(out=out[b, 0:Q, 0 : STRIP - MARGIN], in_=strip[0:Q, 0, MARGIN:STRIP])
-            if last:
-                other.dma_start(out=out[b, S - Q : S, S - STRIP + MARGIN : S], in_=strip[Q:P, n - 1, 0 : STRIP - MARGIN])
+        def store_inner(b, other=nc.sync):
+            nc.sync.dma_start(out=strip_rows(b, 1, NT - 1, 0), in_=strips[0:Q, b, 1:NT, :])
+            other.dma_start(out=strip_rows(b, 0, NT - 1, 1), in_=strips[Q:P, b, 0 : NT - 1, :])
 
-        def finish(b, i0=0, n=NT, eng="s", last=True):
-            strip = strips[b % 3][:, i0 : i0 + n, LIVE]
-            if eng == "v":
-                nc.vector.tensor_tensor(
-                    out=strip, in0=sm[b, i0][:], in1=rs[b, i0][:].unsqueeze(2).to_broadcast([P, n, WIDTH]), op=ALU.mult
-                )
+        def store_edges(b, n=1, other=nc.sync):
+            first = out[b : b + n, 0:Q, 0 : STRIP - MARGIN].rearrange("b r j -> r b j")
+            last = out[b : b + n, S - Q : S, S - STRIP + MARGIN : S].rearrange("b r j -> r b j")
+            nc.sync.dma_start(out=first, in_=strips[0:Q, b : b + n, 0, MARGIN:STRIP])
+            other.dma_start(out=last, in_=strips[Q:P, b : b + n, NT - 1, 0 : STRIP - MARGIN])
+
+        def store(b):
+            store_inner(b)
+            store_edges(b)
+
+        def finish(b, i0=0, n=NT):
+            strip = strips[:, b, i0 : i0 + n, LIVE]
             for i in range(n):
-                if eng == "s":
-                    nc.scalar.activation(out=strip[:, i, :], in_=sm[b, i0][:, i, :], func=ACT.Copy, scale=rs[b, i0][:, i : i + 1])
-                if eng == "g":
-                    nc.gpsimd.tensor_scalar(
-                        out=strip[:, i, :], in0=sm[b, i0][:, i, :], scalar1=rs[b, i0][:, i : i + 1], scalar2=0.0, op0=ALU.mult, op1=ALU.add
-                    )
-            if last:
-                store(b, strips[b % 3], 0, NT)
+                nc.scalar.activation(out=strip[:, i, :], in_=sm[b, i0][:, i, :], func=ACT.Copy, scale=rs[b, i0][:, i : i + 1])
 
-        L = B - 1
-        tx, tc_, ts, tacc, tq = {}, {}, {}, {}, {}
-
-        def t_empty_x(i):
-            tx[i] = work.tile([P, G, P, 2, 2], BF16, name="t_xi", bufs=4, align_bytes=64)
-            scale_x(L, i, tx[i][:])
-
-        def t_quant_x(i):
-            tc_[i] = work.tile([P, G * P], U32, name="t_xc", bufs=4, align_bytes=64)
-            ts[i] = work.tile([P, G * P], U8, name="t_xsc", bufs=4, align_bytes=64)
-            nc.vector.quantize_mx(
-                out=tc_[i][:].bitcast(FP8X4), scales=ts[i][:], in_=tx[i][:].rearrange("p g n h e -> p (g n h e)")
-            )
-
-        def t_project(i):
-            tacc[i] = psum.tile([P, 4, P], F32, name="tp", bufs=4)
-            for t in range(4):
-                for g in range(G):
-                    nc.tensor.matmul_mx(
-                        out=tacc[i][:, t, :],
-                        lhsT=w_perm[:, g, 256 * t : 256 * (t + 1)].bitcast(FP4X4),
-                        lhsT_scale=ws_perm[:, g, P * t : P * (t + 1)],
-                        rhs=tc_[i][:, P * g : P * (g + 1)].bitcast(FP8X4),
-                        rhs_scale=ts[i][:, P * g : P * (g + 1)],
-                        start=(g == 0),
-                        stop=(g == G - 1),
-                    )
-
-        def t_empty_q(i):
-            tq[i] = work.tile([P, P, 4], BF16, name="t_qi", bufs=4, align_bytes=64)
+        def finish_v(b, i0=0, n=NT):
             nc.vector.tensor_tensor(
-                out=tq[i][:], in0=tacc[i][:].rearrange("p t n -> p n t"), in1=bias[:].unsqueeze(1).to_broadcast([P, P, 4]), op=ALU.add
+                out=strips[:, b, i0 : i0 + n, LIVE],
+                in0=sm[b, i0][:],
+                in1=rs[b, i0][:].unsqueeze(2).to_broadcast([P, n, WIDTH]),
+                op=ALU.mult,
             )
-
-        def t_quant_q(i):
-            rows = tq[i][:].rearrange("p n t -> p (n t)")
-            for s in range(2):
-                cols = slice(Q * (3 * i + 2 * s), Q * (3 * i + 2 * s + 1))
-                nc.vector.quantize_mx(
-                    out=qc[L % 2][:, cols].bitcast(FP8X4), scales=qsc[L % 2][:, cols], in_=rows[:, 4 * Q * s : 4 * Q * (s + 1)]
-                )
-
-        half = {}
-
-        def h_empty_x(i):
-            if i == 0:
-                half["x"] = work.tile([P, G, 2 * P, 2, 2], BF16, name="h_xi", bufs=1, align_bytes=64)
-            scale_x(L, i, half["x"][:, :, P * i : P * (i + 1)])
-
-        def h_quant_x():
-            half["c"] = work.tile([P, G * 2 * P], U32, name="h_xc", bufs=1, align_bytes=64)
-            half["s"] = work.tile([P, G * 2 * P], U8, name="h_xsc", bufs=1, align_bytes=64)
-            nc.vector.quantize_mx(
-                out=half["c"][:].bitcast(FP8X4), scales=half["s"][:], in_=half["x"][:].rearrange("p g n h e -> p (g n h e)")
-            )
-
-        def h_project(h):
-            half[h] = psum.tile([P, 2, 2, P], F32, name="acc", bufs=3)
-            for e in range(2):
-                t = 2 * h + e
-                for i in range(2):
-                    for g in range(G):
-                        cols = slice(2 * P * g + P * i, 2 * P * g + P * (i + 1))
-                        nc.tensor.matmul_mx(
-                            out=half[h][:, e, i, :],
-                            lhsT=w_perm[:, g, 256 * t : 256 * (t + 1)].bitcast(FP4X4),
-                            lhsT_scale=ws_perm[:, g, P * t : P * (t + 1)],
-                            rhs=half["c"][:, cols].bitcast(FP8X4),
-                            rhs_scale=half["s"][:, cols],
-                            start=(g == 0),
-                            stop=(g == G - 1),
-                        )
-
-        def h_empty_q():
-            half["p"] = work.tile([P, 2, 2 * P], F32, name="h_qp", bufs=1, align_bytes=64)
-            for e, h in ((0, 0), (0, 1), (1, 0), (1, 1)):
-                t = 2 * h + e
-                nc.scalar.activation(
-                    out=half["p"][:, h, :].bitcast(BF16)[:, e::2],
-                    in_=half[h][:, e].rearrange("p i n -> p (i n)"),
-                    func=ACT.Identity,
-                    bias=bias[:, t : t + 1],
-                )
-
-        def h_weave_q():
-            half["q"] = work.tile([P, 2 * P, 2], F32, name="h_qi", bufs=1, align_bytes=64)
-            nc.scalar.copy(out=half["q"][:], in_=half["p"][:].rearrange("p h n -> p n h"))
-
-        def h_quant_q():
-            rows = half["q"][:].rearrange("p n h -> p (n h)").bitcast(BF16)
-            for lo, hi, at in ((0, Q, 0), (Q, 3 * Q, 2 * Q), (3 * Q, 4 * Q, 5 * Q)):
-                cols = slice(at, at + hi - lo)
-                nc.vector.quantize_mx(out=qc[L % 2][:, cols].bitcast(FP8X4), scales=qsc[L % 2][:, cols], in_=rows[:, 4 * lo : 4 * hi])
 
         def warm_up():
             idle = psum.tile([P, 2 * P], F32, name="sc", bufs=1)
-            nc.tensor.matmul(out=idle[:], lhsT=ident[:], rhs=zeros[:, 0 : 2 * P], start=True, stop=True)
+            nc.tensor.matmul(out=idle[:], lhsT=zeros[:, 0:P], rhs=zeros[:, 0 : 2 * P], start=True, stop=True)
 
         def step(fn, b, *args):
             if 0 <= b < B:
                 fn(b, *args)
 
+        warm_up()
+        warm_up()
+        widen_v(0, 0)
         permute_codes()
         permute_scales()
-        for i in range(NT):
-            widen_head(0, i)
-            warm_up()
-            turn_x(0, i)
-            if i == 1:
-                widen(1, 0)
-        widen_head(1, 2)
-        widen_head(1, 3)
+        turn_x(0, 0)
+        widen_s(0, 1)
         empty_x(0, 0)
-        empty_x(0, 1)
-        turn_k(0, 0)
-        turn_k(0, 1)
-        empty_k(0, 0)
-        empty_k(0, 1)
-        build_mask()
+        turn_x(0, 1)
         warm_up()
-        turn_x(1, 0)
+        widen_s(0, 2)
+        empty_x(0, 1)
+        turn_x(0, 2)
+        widen_s(0, 3)
+        widen(1, 2, 2)
+        turn_x(0, 3)
+        widen_s(1, 0)
+        widen_s(1, 1)
+        turn_k(0, 0)
         empty_x(0, 2)
+        turn_k(0, 1)
+        warm_up()
+        empty_k(0, 0)
+        empty_x(0, 3, 0, NT, 0, 1)
+        empty_x(0, 3, 0, NT, 1, 2)
+        turn_x(1, 0)
+        empty_k(0, 1)
         turn_x(1, 1)
-        empty_x(0, 3)
-        quant_x(0)
-        widen(2, 0)
-        project(0, 0)
-        turn_x(1, 2)
-        empty_x(1, 0)
-        empty_q(0, 0)
-        turn_x(1, 3)
-        project(0, 1)
-        empty_x(1, 1)
-        quant_k(0)
-        widen(2, 1, 1)
-        widen_head(2, 3)
-        empty_q(0, 1)
-        project(0, 2)
-        turn_k(1, 0)
-        turn_k(1, 1)
-        empty_x(1, 2)
-        empty_q(0, 2)
-        project(0, 3)
-        empty_k(1, 0)
-        empty_k(1, 1)
-        turn_x(2, 0)
-        empty_x(1, 3)
-        empty_q(0, 3)
-        turn_x(2, 1)
-        weave_q(0)
-        for n in range(2, L):
-            quant_x(n - 1)
-            widen(n + 1, 0)
-            if n > 2:
-                empty_q(n - 2, 3)
+        for n in range(L - 1):
+            step(quant_q, n - 2)
+            step(quant_k, n - 1)
+            quant_x(n)
+            widen(n + 2, 0, 2)
+            if n == 0:
+                cut_band(1)
+            widen(n + 2, 2, 2 - (n < 2))
+            if n == 0:
+                cut_band(-1)
+            if n < 2:
+                widen_s(n + 2, 3)
+            step(scores, n - 2)
+            project(n, 0, [0])
+            project(n, 1, [0])
+            project(n, 0, [1])
             step(exps, n - 3)
-            project(n - 1, 0)
-            project(n - 1, 1)
-            empty_x(n, 0)
-            if n > 2:
-                weave_q(n - 2)
-            turn_x(n, 2)
-            turn_x(n, 3)
-            empty_q(n - 1, 0)
-            empty_x(n, 1)
+            empty_x(n + 1, 0)
+            turn_x(n + 1, 2)
+            turn_x(n + 1, 3)
+            step(mask_scores, n - 2)
+            empty_q(n, 0)
+            project(n, 1, [1])
+            project(n, 2)
+            empty_x(n + 1, 1)
             step(recip, n - 3)
             step(finish, n - 3)
-            quant_k(n - 1)
-            quant_q(n - 2)
-            widen(n + 1, 1)
-            empty_q(n - 1, 1)
-            project(n - 1, 2)
-            scores(n - 2)
-            empty_x(n, 2)
-            turn_k(n, 0)
-            turn_k(n, 1)
-            mask_scores(n - 2)
-            empty_q(n - 1, 2)
-            empty_k(n, 0)
-            empty_k(n, 1)
-            empty_x(n, 3)
-            project(n - 1, 3)
-            turn_x(n + 1, 0)
-            turn_x(n + 1, 1)
-            row_max(n - 2)
+            step(store, n - 3)
+            empty_q(n, 1)
+            turn_k(n + 1, 0)
+            turn_k(n + 1, 1)
+            empty_x(n + 1, 2)
+            empty_q(n, 2)
+            project(n, 3)
+            if n == 1:
+                build_mask()
+            step(turn_x, n + 2, 0)
+            empty_k(n + 1, 0)
+            empty_q(n, 3)
+            empty_k(n + 1, 1)
+            if n < 1:
+                empty_x(n + 1, 3, 0, NT, 0, 1)
+                empty_x(n + 1, 3, 0, NT, 1, 2)
+            else:
+                empty_x(n + 1, 3)
+            step(turn_x, n + 2, 1)
+            step(row_max, n - 2)
+            weave_q(n)
+        quant_q(L - 3)
+        quant_k(L - 2)
         quant_x(L - 1)
-        empty_q(L - 2, 3)
-        exps(L - 3)
-        h_empty_x(0)
-        weave_q(L - 2)
-        project(L - 1, 0)
-        empty_q(L - 1, 0)
-        h_empty_x(1)
-        recip(L - 3)
-        project(L - 1, 2)
-        empty_q(L - 1, 2)
-        project(L - 1, 1)
+        scores(L - 3)
+        project(L - 1, 0, [0])
+        project(L - 1, 1, [0])
+        project(L - 1, 0, [1])
+        exps(L - 4)
+        empty_x(L, 0, 0, 2)
         turn_x(L, 2)
-        quant_k(L - 1)
-        quant_q(L - 2)
-        h_quant_x()
         turn_x(L, 3)
-        project(L - 1, 3)
-        scores(L - 2)
+        empty_q(L - 1, 0)
+        project(L - 1, 1, [1])
+        project(L - 1, 2)
+        recip(L - 4)
+        mask_scores(L - 3)
+        finish(L - 4)
+        store(L - 4)
+        empty_x(L, 1, 0, 2)
+        row_max(L - 3)
+        quant_x(L, 0, 2, 1)
+        empty_q(L - 1, 1)
         turn_k(L, 0)
         turn_k(L, 1)
-        t_empty_x(2)
-        empty_q(L - 1, 1)
-        h_project(0)
-        t_empty_x(3)
-        empty_q(L - 1, 3)
-        h_project(1)
-        t_quant_x(2)
-        t_quant_x(3)
-        t_project(2)
-        mask_scores(L - 2)
-        finish(L - 3)
+        empty_x(L, 2, 2, 1)
+        empty_q(L - 1, 2)
+        exps(L - 3)
+        project(L - 1, 3)
+        project(L, 0, range(G), 0, 2)
+        project(L, 1, range(G), 0, 2)
+        quant_q(L - 2)
+        quant_x(L, 2, 1, 1)
         empty_k(L, 0)
+        empty_x(L, 3, 3, 1)
+        empty_q(L - 1, 3)
+        project(L, 2, range(G), 0, 2)
+        project(L, 3, range(G), 0, 2)
         empty_k(L, 1)
+        quant_k(L - 1)
+        quant_x(L, 3, 1, 1)
+        for t in range(4):
+            project(L, t, range(G), 2, 1, "tp", 4)
         weave_q(L - 1)
+        recip(L - 3)
+        scores(L - 2)
+        for t in range(4):
+            project(L, t, range(G), 3, 1, "tp", 4)
+        for t in range(4):
+            empty_q(L, t, 0, 2)
+        finish(L - 3)
+        store(L - 3)
+        weave_q(L, 0, 2)
         quant_k(L)
-        row_max(L - 2)
-        h_empty_q()
-        exps(L - 2)
-        t_project(3)
-        t_empty_q(2)
+        empty_q_v(L, 2)
+        mask_scores(L - 2)
         quant_q(L - 1)
+        empty_q_v(L, 3)
         scores(L - 1)
-        h_weave_q()
-        t_empty_q(3)
-        recip(L - 2)
-        finish(L - 2)
-        t_quant_q(2)
-        t_quant_q(3)
+        row_max(L - 2)
+        quant_q(L, 2, 2)
         scores(L, 2, 2, "tp", 4)
-        h_quant_q()
-        scores(L, 0, 2, "tp", 4)
+        exps(L - 2)
         mask_scores(L - 1)
-        mask_scores(L, 2, 2)
+        quant_q(L, 0, 2)
+        scores(L, 0, 2, "tp", 4)
+        recip(L - 2)
         row_max(L - 1)
+        finish(L - 2)
+        store_inner(L - 2)
+        mask_scores(L, 2, 2)
         exps(L - 1)
         mask_scores(L, 0, 2)
         row_max(L, 2, 2)
         row_max(L, 0, 2)
+        recip(L - 1)
         exps(L, 2, 2)
         exps(L, 0, 2)
-        recip(L - 1)
-        finish(L - 1, 0, NT, "v")
+        finish(L - 1)
+        store_inner(L - 1)
         recip(L, 2, 2)
-        finish(L, 2, 2, "s", False)
         recip(L, 0, 2)
-        finish(L, 0, 2, "v")
+        finish_v(L, 2, 2)
+        finish_v(L, 0, 2)
+        store_inner(L, nc.scalar)
+        store_edges(L - 2, 3, nc.scalar)

@@ -388,27 +388,27 @@ def tile_localattention_pa_t_w4_kernel(tc, x_bytes, x_scale, Wq_words, Wq_scales
             project(n, 1, [0])
             project(n, 0, [1])
             step(exps, n - 3)
-            empty_x(n + 1, 0)
             turn_x(n + 1, 2)
+            empty_x(n + 1, 0)
             turn_x(n + 1, 3)
             step(mask_scores, n - 2)
             empty_q(n, 0)
-            project(n, 1, [1])
-            project(n, 2)
+            turn_k(n + 1, 0)
             empty_x(n + 1, 1)
             step(recip, n - 3)
             step(finish, n - 3)
             step(store, n - 3)
+            project(n, 1, [1])
+            project(n, 2)
+            empty_k(n + 1, 0)
             empty_q(n, 1)
-            turn_k(n + 1, 0)
-            turn_k(n + 1, 1)
+            project(n, 3)
             empty_x(n + 1, 2)
             empty_q(n, 2)
-            project(n, 3)
             if n == 1:
                 build_mask()
-            step(turn_x, n + 2, 0)
-            empty_k(n + 1, 0)
+            turn_k(n + 1, 1)
+            turn_x(n + 2, 0)
             empty_q(n, 3)
             empty_k(n + 1, 1)
             if n < 1:
@@ -416,7 +416,7 @@ def tile_localattention_pa_t_w4_kernel(tc, x_bytes, x_scale, Wq_words, Wq_scales
                 empty_x(n + 1, 3, 0, NT, 1, 2)
             else:
                 empty_x(n + 1, 3)
-            step(turn_x, n + 2, 1)
+            turn_x(n + 2, 1)
             step(row_max, n - 2)
             weave_q(n)
         quant_q(L - 3)

@@ -73,6 +73,8 @@ def tile_localattention_pa_t_w4_kernel(tc, x_bytes, x_scale, Wq_words, Wq_scales
             rows = kflat[S * b - SHIFT : S * (b + 1) - SHIFT, :]
             nc.sync.dma_start(out=k_tiles[b][:], in_=rows.rearrange("(i p) e -> p i e", p=P))
 
+        nc.vector.memset(zeros[:], 0.0)
+        nc.vector.memset(ident[:], 0.0)
         nc.vector.memset(ws_raw[:].rearrange("p g n -> p (g n)").bitcast(I32), 0)
         nc.sync.dma_start(out=x_first[0][:], in_=xv[0][:, 0, :])
         nc.sync.dma_start(out=x_first[1][:], in_=xv[0][:, 1, :])
@@ -98,8 +100,6 @@ def tile_localattention_pa_t_w4_kernel(tc, x_bytes, x_scale, Wq_words, Wq_scales
             load_k(b - 1)
         load_k(L)
 
-        nc.vector.memset(ident[:], 0.0)
-        nc.vector.memset(zeros[:], 0.0)
         make_identity(nc, ident[:], nomemset=True)
         nc.vector.memset(band[:], 0.0)
         for j in range(2):
@@ -336,7 +336,7 @@ def tile_localattention_pa_t_w4_kernel(tc, x_bytes, x_scale, Wq_words, Wq_scales
             )
 
         def warm_up():
-            idle = psum.tile([P, 2 * P], F32, name="sc", bufs=1)
+            idle = psum.tile([P, 2 * P], F32, name="acc", bufs=3)
             nc.tensor.matmul(out=idle[:], lhsT=zeros[:, 0:P], rhs=zeros[:, 0 : 2 * P], start=True, stop=True)
 
         def step(fn, b, *args):
@@ -433,14 +433,14 @@ def tile_localattention_pa_t_w4_kernel(tc, x_bytes, x_scale, Wq_words, Wq_scales
         empty_q(L - 1, 0)
         project(L - 1, 1, [1])
         project(L - 1, 2)
-        recip(L - 4)
         mask_scores(L - 3)
-        finish(L - 4)
-        store(L - 4)
         empty_x(L, 1, 0, 2)
+        recip(L - 4)
         row_max(L - 3)
         quant_x(L, 0, 2, 1)
         empty_q(L - 1, 1)
+        finish(L - 4)
+        store(L - 4)
         turn_k(L, 0)
         turn_k(L, 1)
         empty_x(L, 2, 2, 1)
@@ -496,11 +496,11 @@ def tile_localattention_pa_t_w4_kernel(tc, x_bytes, x_scale, Wq_words, Wq_scales
         recip(L - 1)
         exps(L, 2, 2)
         exps(L, 0, 2)
-        finish(L - 1)
+        finish_v(L - 1)
         store_inner(L - 1)
         recip(L, 2, 2)
         recip(L, 0, 2)
-        finish_v(L, 2, 2)
+        finish(L, 2, 2)
         finish_v(L, 0, 2)
-        store_inner(L, nc.scalar)
         store_edges(L - 2, 3, nc.scalar)
+        store_inner(L, nc.scalar)

@@ -32,6 +32,13 @@ WIDTH = Q + 2 * HALF
 MASKED = -1e9
 SCALE = 1.0 / math.sqrt(E)
 L = B - 1
+PARKED = 4
+BAND = 2 * HALF + 1
+ROWS = 8
+PITCH = 16
+BOX = 3 * MARGIN
+ROOM = S * (STRIP + 1)
+SHARE = 512
 
 
 def tile_localattention_pa_t_w4_kernel(tc, x_bytes, x_scale, Wq_words, Wq_scales, bq, k, out):
@@ -47,7 +54,7 @@ def tile_localattention_pa_t_w4_kernel(tc, x_bytes, x_scale, Wq_words, Wq_scales
         ring = [keep.tile([P, NT * D], BF16, name=f"ring{j}", align_bytes=64) for j in range(3)]
         qi = [keep.tile([P, S * 4], BF16, name=f"qi{j}", align_bytes=64) for j in range(2)]
         kt = [keep.tile([P, S * 4], BF16, name=f"kt{j}", align_bytes=64) for j in range(3)]
-        strips = keep.tile([P, B, NT, STRIP], F32, name="strips")
+        strips = keep.tile([P, B - PARKED, NT, STRIP], F32, name="strips")
         w_raw = [keep.tile([P, 2 * E], U8, name=f"w_raw{g}", align_bytes=64) for g in range(G)]
         w_perm = keep.tile([P, G, 2 * E], U8, name="w_perm", align_bytes=64)
         ws_raw = keep.tile([P, G, E], U8, name="ws_raw", align_bytes=64)
@@ -61,6 +68,9 @@ def tile_localattention_pa_t_w4_kernel(tc, x_bytes, x_scale, Wq_words, Wq_scales
         qc = [keep.tile([P, NT * 3 * Q], U32, name=f"qc{j}", align_bytes=64) for j in range(2)]
         qsc = [keep.tile([P, NT * 3 * Q], U8, name=f"qsc{j}", align_bytes=64) for j in range(2)]
 
+        diag = [keep.tile([P, ROWS, PITCH], F32, name=f"diag{j}", align_bytes=64) for j in range(PARKED // 2)]
+        boxes = [keep.tile([P, ROWS * BOX + ROWS], F32, name=f"boxes{j}", align_bytes=64) for j in range(PARKED // 2)]
+
         x_first = [keep.tile([P, D], U8, name=f"x_codes_first{i}", align_bytes=64) for i in range(2)]
         x_tiles = [keep.tile([P, NT, D], U8, name=f"x_codes{b}", align_bytes=64) for b in range(B)]
         k_tiles = [keep.tile([P, NT, E], BF16, name=f"k_rows{b}", align_bytes=64) for b in range(B)]
@@ -68,6 +78,7 @@ def tile_localattention_pa_t_w4_kernel(tc, x_bytes, x_scale, Wq_words, Wq_scales
         xv = x_bytes.rearrange("b (i p) k -> b p i k", p=P)
         kflat = k.rearrange("b s e -> (b s) e")
         oflat = out.rearrange("b s j -> b (s j)")
+        flat = out.rearrange("b s j -> (b s j)")
 
         def load_k(b):
             rows = kflat[S * b - SHIFT : S * (b + 1) - SHIFT, :]
@@ -107,10 +118,17 @@ def tile_localattention_pa_t_w4_kernel(tc, x_bytes, x_scale, Wq_words, Wq_scales
             nc.vector.memset(qsc[j][:].bitcast(I32).rearrange("p (i u n) -> p i u n", i=NT, u=3)[:, :, 1, :], 0)
         for margin in (slice(0, LIVE.start), slice(LIVE.stop, STRIP)):
             nc.vector.memset(strips[:].rearrange("p j i c -> p (j i) c")[:, :, margin], 0.0)
-        for b in range(B):
+        for j in range(PARKED // 2):
+            nc.vector.memset(boxes[j][:], 0.0)
+
+        def clear(b):
             nc.sync.dma_start(
                 out=oflat[b].rearrange("(p r n) -> p r n", p=P, r=NT), in_=zeros[:].unsqueeze(1).to_broadcast([P, NT, S])
             )
+
+        for b in range(B):
+            if b != L - 1:
+                clear(b)
 
         def cut_band(side):
             nc.gpsimd.affine_select(
@@ -127,6 +145,7 @@ def tile_localattention_pa_t_w4_kernel(tc, x_bytes, x_scale, Wq_words, Wq_scales
 
         xt, xc, xsc, ktp, acc, qp = {}, {}, {}, {}, {}, {}
         sc, sm, nm, ss, rs = {}, {}, {}, {}, {}
+        raw, top, total, inverse = {}, {}, {}, {}
 
         def permute_codes():
             for g in range(G):
@@ -154,6 +173,14 @@ def tile_localattention_pa_t_w4_kernel(tc, x_bytes, x_scale, Wq_words, Wq_scales
         def widen(b, i0=0, n=NT):
             codes = x_tiles[b][:, i0 : i0 + n, :].rearrange("p i k -> p (i k)")
             nc.gpsimd.tensor_copy(out=wide(b, i0, n), in_=codes.bitcast(FP8))
+
+        def widen_most(b):
+            codes = x_tiles[b][:].rearrange("p i k -> p (i k)")[:, 2 * D : NT * D - SHARE]
+            nc.gpsimd.tensor_copy(out=wide(b, 0, NT)[:, 2 * D : NT * D - SHARE], in_=codes.bitcast(FP8))
+
+        def widen_rest(b):
+            codes = x_tiles[b][:].rearrange("p i k -> p (i k)")[:, NT * D - SHARE :]
+            nc.scalar.copy(out=wide(b, 0, NT)[:, NT * D - SHARE :], in_=codes.bitcast(FP8))
 
         def turn_x(b, i, passes=range(G)):
             words = wide(b, i).bitcast(F32)
@@ -280,6 +307,88 @@ def tile_localattention_pa_t_w4_kernel(tc, x_bytes, x_scale, Wq_words, Wq_scales
                         stop=(s == 1),
                     )
 
+        def parked(b):
+            return (L - 1) * S * S + b * ROOM
+
+        def park_edges():
+            for s in range(2):
+                lo = parked(0) + s * (ROOM - Q * (STRIP + 1) + STRIP - MARGIN)
+                view = flat[lo : lo + PARKED * ROOM].rearrange("(b y) -> b y", b=PARKED)[:, 0 : Q * STRIP]
+                cells = view.rearrange("b (r j) -> r b j", r=Q)[:, :, 0:MARGIN]
+                at = (1 - s) * (Q + STRIP - MARGIN)
+                nc.sync.dma_start(out=cells, in_=band[Q * s : Q * (s + 1), at : at + MARGIN].unsqueeze(1).to_broadcast([Q, PARKED, MARGIN]))
+
+        def empty_scores(b):
+            raw[b] = work.tile([P, NT, STRIP], F32, name="raw", bufs=PARKED, align_bytes=64)
+            window = sc[b, 0][:, :, SHIFT - MARGIN : SHIFT - MARGIN + STRIP]
+            nc.scalar.activation(out=raw[b][:], in_=window, func=ACT.Copy, scale=SCALE)
+
+        def park(b):
+            for s in range(2):
+                lo = parked(b) + (STRIP + 1) * Q * s
+                view = flat[lo : lo + ROOM].rearrange("(i y) -> i y", i=NT)[:, 0 : Q * STRIP].rearrange("i (r j) -> r i j", r=Q)
+                rows = raw[b][Q * s : Q * (s + 1)]
+                inner = slice(1 - s, NT - s)
+                nc.sync.dma_start(out=view[:, inner, :], in_=rows[:, inner, :])
+                outer = (s * (NT - 1), slice(MARGIN * (1 - s), STRIP - MARGIN * s))
+                nc.sync.dma_start(out=view[:, outer[0], outer[1]], in_=rows[:, outer[0], outer[1]])
+
+        def fetch(b):
+            lo = parked(b) + MARGIN - HALF
+            view = flat[lo : lo + ROOM].rearrange("(p r y) -> p r y", r=ROWS, y=STRIP + 1)[:, :, 0:BAND]
+            nc.sync.dma_start(out=diag[b // 2][Q * (b % 2) : Q * (b % 2 + 1), :, 0:BAND], in_=view)
+
+        def pair_max(j):
+            top[j] = work.tile([P, ROWS], F32, name="top")
+            nc.vector.tensor_reduce(out=top[j][:], in_=diag[j][:, :, 0:BAND], axis=AX.X, op=ALU.max, negate=True)
+
+        def pair_shift(j):
+            live = diag[j][:, :, 0:BAND]
+            nc.vector.tensor_tensor(out=live, in0=live, in1=top[j][:].unsqueeze(2).to_broadcast([P, ROWS, BAND]), op=ALU.add)
+
+        def pair_exp(j):
+            live = diag[j][:, :, 0:BAND]
+            nc.scalar.activation(out=live, in_=live, func=ACT.Exp)
+
+        def pair_sum(j):
+            total[j] = work.tile([P, ROWS], F32, name="total")
+            nc.vector.tensor_reduce(out=total[j][:], in_=diag[j][:, :, 0:BAND], axis=AX.X, op=ALU.add)
+
+        def pair_recip(j):
+            inverse[j] = work.tile([P, ROWS], F32, name="inverse")
+            nc.vector.reciprocal(out=inverse[j][:], in_=total[j][:])
+
+        def pair_finish(j):
+            first = MARGIN - HALF
+            skew = boxes[j][:].rearrange("p (r c) -> p r c", r=ROWS)[:, :, first : first + BAND]
+            nc.vector.tensor_tensor(
+                out=skew, in0=diag[j][:, :, 0:BAND], in1=inverse[j][:].unsqueeze(2).to_broadcast([P, ROWS, BAND]), op=ALU.mult
+            )
+
+        def box_rows(b, at, n, r):
+            lo = b * S * S - MARGIN + at
+            return flat[lo : lo + n * ROWS * (S + 1)].rearrange("(p y) -> p y", p=n)[:, 0 : r * S].rearrange("p (r j) -> p r j", r=r)
+
+        def box_view(j):
+            return boxes[j][:, 0 : ROWS * BOX].rearrange("p (r c) -> p r c", r=ROWS)
+
+        def store_later_rows(j):
+            for u in range(2):
+                nc.sync.dma_start(out=box_rows(2 * j + u, S, Q, ROWS - 1)[:, :, 0:BOX], in_=box_view(j)[Q * u : Q * (u + 1), 1:ROWS, :])
+
+        def store_first_left(j):
+            for u in range(2):
+                nc.sync.dma_start(out=box_rows(2 * j + u, ROWS * (S + 1), Q - 1, 1)[:, 0, 0:MARGIN], in_=box_view(j)[Q * u + 1 : Q * (u + 1), 0, 0:MARGIN])
+
+        def store_first_right(j):
+            for u in range(2):
+                nc.sync.dma_start(out=box_rows(2 * j + u, MARGIN, Q, 1)[:, 0, 0 : BOX - MARGIN], in_=box_view(j)[Q * u : Q * (u + 1), 0, MARGIN:BOX])
+
+        def store_boxes(j):
+            store_later_rows(j)
+            store_first_left(j)
+            store_first_right(j)
+
         def mask_scores(b, i0=0, n=NT):
             sm[b, i0] = work.tile([P, n, WIDTH], F32, name="sm", bufs=6)
             window = sc[b, i0][:, :, SHIFT - HALF : SHIFT - HALF + WIDTH]
@@ -309,27 +418,27 @@ def tile_localattention_pa_t_w4_kernel(tc, x_bytes, x_scale, Wq_words, Wq_scales
             return view.rearrange("i (r j) -> r i j", r=Q)[:, :, 0:STRIP]
 
         def store_inner(b, other=nc.sync):
-            nc.sync.dma_start(out=strip_rows(b, 1, NT - 1, 0), in_=strips[0:Q, b, 1:NT, :])
-            other.dma_start(out=strip_rows(b, 0, NT - 1, 1), in_=strips[Q:P, b, 0 : NT - 1, :])
+            nc.sync.dma_start(out=strip_rows(b, 1, NT - 1, 0), in_=strips[0:Q, b - PARKED, 1:NT, :])
+            other.dma_start(out=strip_rows(b, 0, NT - 1, 1), in_=strips[Q:P, b - PARKED, 0 : NT - 1, :])
 
         def store_edges(b, n=1, other=nc.sync):
             first = out[b : b + n, 0:Q, 0 : STRIP - MARGIN].rearrange("b r j -> r b j")
             last = out[b : b + n, S - Q : S, S - STRIP + MARGIN : S].rearrange("b r j -> r b j")
-            nc.sync.dma_start(out=first, in_=strips[0:Q, b : b + n, 0, MARGIN:STRIP])
-            other.dma_start(out=last, in_=strips[Q:P, b : b + n, NT - 1, 0 : STRIP - MARGIN])
+            nc.sync.dma_start(out=first, in_=strips[0:Q, b - PARKED : b - PARKED + n, 0, MARGIN:STRIP])
+            other.dma_start(out=last, in_=strips[Q:P, b - PARKED : b - PARKED + n, NT - 1, 0 : STRIP - MARGIN])
 
         def store(b):
             store_inner(b)
             store_edges(b)
 
         def finish(b, i0=0, n=NT):
-            strip = strips[:, b, i0 : i0 + n, LIVE]
+            strip = strips[:, b - PARKED, i0 : i0 + n, LIVE]
             for i in range(n):
                 nc.scalar.activation(out=strip[:, i, :], in_=sm[b, i0][:, i, :], func=ACT.Copy, scale=rs[b, i0][:, i : i + 1])
 
         def finish_v(b, i0=0, n=NT):
             nc.vector.tensor_tensor(
-                out=strips[:, b, i0 : i0 + n, LIVE],
+                out=strips[:, b - PARKED, i0 : i0 + n, LIVE],
                 in0=sm[b, i0][:],
                 in1=rs[b, i0][:].unsqueeze(2).to_broadcast([P, n, WIDTH]),
                 op=ALU.mult,
@@ -378,26 +487,30 @@ def tile_localattention_pa_t_w4_kernel(tc, x_bytes, x_scale, Wq_words, Wq_scales
             widen(n + 2, 0, 2)
             if n == 0:
                 cut_band(1)
-            widen(n + 2, 2, 2 - (n < 2))
+            if n < 2:
+                widen(n + 2, 2, 1)
+            else:
+                widen_most(n + 2)
             if n == 0:
                 cut_band(-1)
+                park_edges()
             if n < 2:
                 widen_s(n + 2, 3)
             step(scores, n - 2)
             project(n, 0, [0])
             project(n, 1, [0])
             project(n, 0, [1])
-            step(exps, n - 3)
             turn_x(n + 1, 2)
             empty_x(n + 1, 0)
             turn_x(n + 1, 3)
-            step(mask_scores, n - 2)
+            step(empty_scores, n - 2)
+            step(park, n - 2)
+            if n % 2 and n > 2:
+                fetch(n - 3)
+                fetch(n - 2)
             empty_q(n, 0)
             turn_k(n + 1, 0)
             empty_x(n + 1, 1)
-            step(recip, n - 3)
-            step(finish, n - 3)
-            step(store, n - 3)
             project(n, 1, [1])
             project(n, 2)
             empty_k(n + 1, 0)
@@ -417,16 +530,21 @@ def tile_localattention_pa_t_w4_kernel(tc, x_bytes, x_scale, Wq_words, Wq_scales
             else:
                 empty_x(n + 1, 3)
             turn_x(n + 2, 1)
-            step(row_max, n - 2)
+            if n == 5:
+                pair_max(0)
             weave_q(n)
+            if n >= 2:
+                widen_rest(n + 2)
         quant_q(L - 3)
+        pair_shift(0)
+        pair_exp(0)
+        clear(L - 1)
         quant_k(L - 2)
         quant_x(L - 1)
         scores(L - 3)
         project(L - 1, 0, [0])
         project(L - 1, 1, [0])
         project(L - 1, 0, [1])
-        exps(L - 4)
         empty_x(L, 0, 0, 2)
         turn_x(L, 2)
         turn_x(L, 3)
@@ -435,22 +553,30 @@ def tile_localattention_pa_t_w4_kernel(tc, x_bytes, x_scale, Wq_words, Wq_scales
         project(L - 1, 2)
         mask_scores(L - 3)
         empty_x(L, 1, 0, 2)
-        recip(L - 4)
+        pair_sum(0)
+        pair_max(1)
         row_max(L - 3)
+        pair_recip(0)
+        pair_shift(1)
         quant_x(L, 0, 2, 1)
+        pair_finish(0)
+        store_boxes(0)
         empty_q(L - 1, 1)
-        finish(L - 4)
-        store(L - 4)
+        pair_exp(1)
         turn_k(L, 0)
         turn_k(L, 1)
         empty_x(L, 2, 2, 1)
+        pair_sum(1)
         empty_q(L - 1, 2)
         exps(L - 3)
         project(L - 1, 3)
         project(L, 0, range(G), 0, 2)
         project(L, 1, range(G), 0, 2)
         quant_q(L - 2)
+        pair_recip(1)
         quant_x(L, 2, 1, 1)
+        pair_finish(1)
+        store_boxes(1)
         empty_k(L, 0)
         empty_x(L, 3, 3, 1)
         empty_q(L - 1, 3)

@@ -38,6 +38,7 @@ ROWS = 8
 PITCH = 16
 BOX = 3 * MARGIN
 ROOM = S * (STRIP + 1)
+STENCIL = Q + STRIP + 2 * MARGIN
 SHARE = 512
 
 
@@ -54,13 +55,14 @@ def tile_localattention_pa_t_w4_kernel(tc, x_bytes, x_scale, Wq_words, Wq_scales
         ring = [keep.tile([P, NT * D], BF16, name=f"ring{j}", align_bytes=64) for j in range(3)]
         qi = [keep.tile([P, S * 4], BF16, name=f"qi{j}", align_bytes=64) for j in range(2)]
         kt = [keep.tile([P, S * 4], BF16, name=f"kt{j}", align_bytes=64) for j in range(3)]
+        k_last = keep.tile([P, S * 4], BF16, name="k_last", align_bytes=64)
         strips = keep.tile([P, B - PARKED, NT, STRIP], F32, name="strips")
         w_raw = [keep.tile([P, 2 * E], U8, name=f"w_raw{g}", align_bytes=64) for g in range(G)]
         w_perm = keep.tile([P, G, 2 * E], U8, name="w_perm", align_bytes=64)
         ws_raw = keep.tile([P, G, E], U8, name="ws_raw", align_bytes=64)
         ws_perm = keep.tile([P, G, E], U8, name="ws_perm", align_bytes=64)
         bias = keep.tile([P, 4], BF16, name="bias")
-        band = keep.tile([P, Q + STRIP], F32, name="band")
+        stencil = keep.tile([P, STENCIL], F32, name="stencil")
         mask = keep.tile([P, NT, STRIP], F32, name="mask")
         zeros = keep.tile([P, S], F32, name="zeros")
         kc = keep.tile([P, B * S + Q], U32, name="kc", align_bytes=64)
@@ -72,6 +74,7 @@ def tile_localattention_pa_t_w4_kernel(tc, x_bytes, x_scale, Wq_words, Wq_scales
         boxes = [keep.tile([P, ROWS * BOX + ROWS], F32, name=f"boxes{j}", align_bytes=64) for j in range(PARKED // 2)]
 
         x_first = [keep.tile([P, D], U8, name=f"x_codes_first{i}", align_bytes=64) for i in range(2)]
+        x_second = keep.tile([P, 2, D], U8, name="x_codes_second", align_bytes=64)
         x_tiles = [keep.tile([P, NT, D], U8, name=f"x_codes{b}", align_bytes=64) for b in range(B)]
         k_tiles = [keep.tile([P, NT, E], BF16, name=f"k_rows{b}", align_bytes=64) for b in range(B)]
 
@@ -81,8 +84,9 @@ def tile_localattention_pa_t_w4_kernel(tc, x_bytes, x_scale, Wq_words, Wq_scales
         flat = out.rearrange("b s j -> (b s j)")
 
         def load_k(b):
-            rows = kflat[S * b - SHIFT : S * (b + 1) - SHIFT, :]
-            nc.sync.dma_start(out=k_tiles[b][:], in_=rows.rearrange("(i p) e -> p i e", p=P))
+            n = NT - (b == L)
+            rows = kflat[S * b + SHIFT : S * b + SHIFT + P * n, :]
+            nc.sync.dma_start(out=k_tiles[b][:, 0:n, :], in_=rows.rearrange("(i p) e -> p i e", p=P))
 
         nc.vector.memset(zeros[:], 0.0)
         nc.vector.memset(ident[:], 0.0)
@@ -93,55 +97,73 @@ def tile_localattention_pa_t_w4_kernel(tc, x_bytes, x_scale, Wq_words, Wq_scales
             nc.sync.dma_start(out=w_raw[g][:].bitcast(I32), in_=Wq_words[g].bitcast(I32))
         nc.sync.dma_start(out=scale_p[:], in_=x_scale.rearrange("a b (g p c) -> p (a b g) c", p=P, c=4))
         nc.sync.dma_start(out=x_tiles[0][:, 2:NT, :], in_=xv[0][:, 2:NT, :])
+        nc.sync.dma_start(out=x_second[:], in_=xv[1][:, 0:2, :])
         for q in range(4):
             nc.sync.dma_start(
                 out=ws_raw[32 * q : 32 * q + 4].bitcast(I32),
                 in_=Wq_scales[:, 4 * q : 4 * q + 4, :].rearrange("g r n -> r g n").bitcast(I32),
             )
-        nc.sync.dma_start(out=x_tiles[1][:], in_=xv[1])
-        nc.sync.dma_start(out=k_tiles[0][0:SHIFT, 0, :], in_=kflat[B * S - SHIFT : B * S, :])
-        nc.sync.dma_start(out=k_tiles[0][SHIFT:Q, 0, :], in_=kflat[0:SHIFT, :])
-        nc.sync.dma_start(out=k_tiles[0][Q:P, 0, :], in_=kflat[SHIFT : P - SHIFT, :])
-        nc.sync.dma_start(
-            out=k_tiles[0][:, 1:NT, :], in_=kflat[P - SHIFT : S - SHIFT, :].rearrange("(i p) e -> p i e", p=P)
-        )
+        nc.sync.dma_start(out=x_tiles[1][:, 2:NT, :], in_=xv[1][:, 2:NT, :])
+        nc.sync.dma_start(out=x_tiles[2][:], in_=xv[2])
         nc.sync.dma_start(out=bias[:], in_=bq.rearrange("(p t) -> p t", t=4))
-        for b in range(2, B):
+        load_k(0)
+        seam = B * S - (P - SHIFT)
+        nc.sync.dma_start(out=k_tiles[L][0:Q, NT - 1, :], in_=kflat[seam : seam + Q, :])
+        nc.sync.dma_start(out=k_tiles[L][Q : P - SHIFT, NT - 1, :], in_=kflat[seam + Q : B * S, :])
+        nc.sync.dma_start(out=k_tiles[L][P - SHIFT : P, NT - 1, :], in_=kflat[0:SHIFT, :])
+        for b in range(3, B):
             nc.sync.dma_start(out=x_tiles[b][:], in_=xv[b])
-            load_k(b - 1)
+            load_k(b - 2)
+        load_k(L - 1)
         load_k(L)
 
         make_identity(nc, ident[:], nomemset=True)
-        nc.vector.memset(band[:], 0.0)
+        nc.vector.memset(stencil[:], MASKED)
+        nc.vector.memset(stencil[:, Q + MARGIN - HALF : Q + MARGIN + HALF + 1], 0.0)
         for j in range(2):
             nc.vector.memset(qc[j][:].bitcast(I32).rearrange("p (i u n) -> p i u n", i=NT, u=3)[:, :, 1, :], 0)
             nc.vector.memset(qsc[j][:].bitcast(I32).rearrange("p (i u n) -> p i u n", i=NT, u=3)[:, :, 1, :], 0)
         for margin in (slice(0, LIVE.start), slice(LIVE.stop, STRIP)):
             nc.vector.memset(strips[:].rearrange("p j i c -> p (j i) c")[:, :, margin], 0.0)
         for j in range(PARKED // 2):
-            nc.vector.memset(boxes[j][:], 0.0)
+            nc.scalar.activation(out=boxes[j][:], in_=zeros[:, 0 : ROWS * (BOX + 1)], func=ACT.Copy)
 
         def clear(b):
             nc.sync.dma_start(
                 out=oflat[b].rearrange("(p r n) -> p r n", p=P, r=NT), in_=zeros[:].unsqueeze(1).to_broadcast([P, NT, S])
             )
 
+        def parked(b):
+            return (L - 1) * S * S + b * ROOM
+
+        def lay_stencil():
+            lo = parked(PARKED)
+            nc.sync.dma_start(out=flat[lo : lo + P * STENCIL].rearrange("(p c) -> p c", p=P), in_=stencil[:])
+
+        def load_mask():
+            lo = parked(PARKED)
+            for s in range(2):
+                at = lo + Q * STENCIL * s + Q
+                rows = flat[at : at + Q * (STENCIL - 1)].rearrange("(r c) -> r c", r=Q)[:, 0:STRIP]
+                nc.sync.dma_start(out=mask[Q * s : Q * (s + 1)], in_=rows.unsqueeze(1).to_broadcast([Q, NT, STRIP]))
+
+        def mask_edges():
+            nc.vector.memset(mask[0:Q, 0, 0:MARGIN], MASKED)
+            nc.vector.memset(mask[Q:P, NT - 1, STRIP - MARGIN : STRIP], MASKED)
+
+        def park_edges():
+            for s in range(2):
+                lo = parked(0) + s * (ROOM - Q * (STRIP + 1) + STRIP - MARGIN)
+                view = flat[lo : lo + PARKED * ROOM].rearrange("(b y) -> b y", b=PARKED)[:, 0 : Q * STRIP]
+                cells = view.rearrange("b (r j) -> r b j", r=Q)[:, :, 0:MARGIN]
+                nc.sync.dma_start(out=cells, in_=stencil[Q * s : Q * (s + 1), 0 : PARKED * MARGIN].rearrange("p (b j) -> p b j", b=PARKED))
+
+        park_edges()
+        lay_stencil()
         for b in range(B):
             if b != L - 1:
                 clear(b)
-
-        def cut_band(side):
-            nc.gpsimd.affine_select(
-                out=band[:], in_=band[:], pattern=[[side, Q + STRIP]], compare_op=ALU.is_ge, fill=MASKED,
-                base=HALF - side * MARGIN, channel_multiplier=-side,
-            )
-
-        def build_mask():
-            for s in range(2):
-                rows = slice(Q * s, Q * (s + 1))
-                nc.scalar.copy(out=mask[rows], in_=band[rows, Q * s : Q * s + STRIP].unsqueeze(1).to_broadcast([Q, NT, STRIP]))
-            nc.scalar.copy(out=mask[0:Q, 0, 0:MARGIN], in_=band[0:Q, Q + STRIP - MARGIN : Q + STRIP])
-            nc.scalar.copy(out=mask[Q:P, NT - 1, STRIP - MARGIN : STRIP], in_=band[Q:P, 0:MARGIN])
+        load_mask()
 
         xt, xc, xsc, ktp, acc, qp = {}, {}, {}, {}, {}, {}
         sc, sm, nm, ss, rs = {}, {}, {}, {}, {}
@@ -164,8 +186,8 @@ def tile_localattention_pa_t_w4_kernel(tc, x_bytes, x_scale, Wq_words, Wq_scales
             return ring[(b + 1) % 3][:, D * i : D * (i + n)]
 
         def widen_s(b, i):
-            codes = x_first[i][:] if b == 0 and i < 2 else x_tiles[b][:, i, :]
-            nc.scalar.activation(out=wide(b, i), in_=codes.bitcast(FP8), func=ACT.Copy)
+            codes = x_tiles[b][:, i, :] if b > 1 or i > 1 else x_second[:, i, :] if b else x_first[i][:]
+            nc.scalar.copy(out=wide(b, i), in_=codes.bitcast(FP8))
 
         def widen_v(b, i):
             nc.vector.tensor_copy(out=wide(b, i), in_=x_first[i][:].bitcast(FP8))
@@ -227,22 +249,26 @@ def tile_localattention_pa_t_w4_kernel(tc, x_bytes, x_scale, Wq_words, Wq_scales
                     out=xc[b, 0][:, cols].bitcast(FP8X4), scales=xsc[b, 0][:, cols], in_=woven_x(b)[:, 4 * cols.start : 4 * cols.stop]
                 )
 
-        def turn_k(b, half):
-            ktp[b, half] = psum.tile([P, 2, 2, P], F32, name="tp", bufs=4)
-            for j in range(2):
-                words = k_tiles[b][:, 2 * half + j, :].bitcast(F32)
-                for h in range(2):
-                    nc.tensor.transpose(ktp[b, half][:, j, h, :], words[:, h:256:2], ident[:])
+        def rows_k(b):
+            return k_last[:] if b == L else kt[b % 3][:]
 
-        def empty_k(b, half):
-            dst = kt[b % 3][:, 2 * S * half : 2 * S * (half + 1)].bitcast(F32).rearrange("p (j r h) -> p j r h", j=2, h=2)
-            nc.scalar.copy(out=dst, in_=ktp[b, half][:].rearrange("p j h r -> p j r h"))
+        def turn_k(b, j0, n=2, tag="tp", bufs=4):
+            ktp[b, j0] = psum.tile([P, n, 2, P], F32, name=tag, bufs=bufs)
+            for j in range(n):
+                words = k_tiles[b][:, j0 + j, :].bitcast(F32)
+                for h in range(2):
+                    nc.tensor.transpose(ktp[b, j0][:, j, h, :], words[:, h:256:2], ident[:])
+
+        def empty_k(b, j0, n=2):
+            dst = rows_k(b)[:, S * j0 : S * (j0 + n)].bitcast(F32).rearrange("p (j r h) -> p j r h", j=n, h=2)
+            nc.scalar.copy(out=dst, in_=ktp[b, j0][:].rearrange("p j h r -> p j r h"))
+
+        def quant_seam():
+            nc.vector.quantize_mx(out=kc[:, 0:Q].bitcast(FP8X4), scales=ksc[:, 0:Q], in_=rows_k(L)[:, 4 * (S - Q) :])
 
         def quant_k(b):
-            rows = kt[b % 3][:]
-            if b == 0:
-                nc.vector.quantize_mx(out=kc[:, B * S :].bitcast(FP8X4), scales=ksc[:, B * S :], in_=rows[:, 0 : 4 * Q])
-            nc.vector.quantize_mx(out=kc[:, S * b : S * (b + 1)].bitcast(FP8X4), scales=ksc[:, S * b : S * (b + 1)], in_=rows)
+            cols = slice(S * b + Q, S * (b + 1) + Q)
+            nc.vector.quantize_mx(out=kc[:, cols].bitcast(FP8X4), scales=ksc[:, cols], in_=rows_k(b))
 
         def project(b, t, passes=range(G), i0=0, n=NT, tag="acc", bufs=3):
             per = NT // n
@@ -306,17 +332,6 @@ def tile_localattention_pa_t_w4_kernel(tc, x_bytes, x_scale, Wq_words, Wq_scales
                         start=(s == 0),
                         stop=(s == 1),
                     )
-
-        def parked(b):
-            return (L - 1) * S * S + b * ROOM
-
-        def park_edges():
-            for s in range(2):
-                lo = parked(0) + s * (ROOM - Q * (STRIP + 1) + STRIP - MARGIN)
-                view = flat[lo : lo + PARKED * ROOM].rearrange("(b y) -> b y", b=PARKED)[:, 0 : Q * STRIP]
-                cells = view.rearrange("b (r j) -> r b j", r=Q)[:, :, 0:MARGIN]
-                at = (1 - s) * (Q + STRIP - MARGIN)
-                nc.sync.dma_start(out=cells, in_=band[Q * s : Q * (s + 1), at : at + MARGIN].unsqueeze(1).to_broadcast([Q, PARKED, MARGIN]))
 
         def empty_scores(b):
             raw[b] = work.tile([P, NT, STRIP], F32, name="raw", bufs=PARKED, align_bytes=64)
@@ -454,8 +469,10 @@ def tile_localattention_pa_t_w4_kernel(tc, x_bytes, x_scale, Wq_words, Wq_scales
 
         warm_up()
         warm_up()
+        warm_up()
         widen_v(0, 0)
         permute_codes()
+        widen(0, 3, 1)
         permute_scales()
         turn_x(0, 0)
         widen_s(0, 1)
@@ -465,42 +482,37 @@ def tile_localattention_pa_t_w4_kernel(tc, x_bytes, x_scale, Wq_words, Wq_scales
         widen_s(0, 2)
         empty_x(0, 1)
         turn_x(0, 2)
-        widen_s(0, 3)
-        widen(1, 2, 2)
         turn_x(0, 3)
+        warm_up()
         widen_s(1, 0)
         widen_s(1, 1)
-        turn_k(0, 0)
+        widen_s(1, 2)
+        widen_s(1, 3)
+        turn_x(1, 0)
         empty_x(0, 2)
-        turn_k(0, 1)
-        warm_up()
-        empty_k(0, 0)
+        turn_x(1, 1)
         empty_x(0, 3, 0, NT, 0, 1)
         empty_x(0, 3, 0, NT, 1, 2)
-        turn_x(1, 0)
-        empty_k(0, 1)
-        turn_x(1, 1)
+        turn_x(1, 2)
         for n in range(L - 1):
             step(quant_q, n - 2)
-            step(quant_k, n - 1)
+            if n == 2:
+                quant_seam()
+            step(quant_k, n - 2)
             quant_x(n)
             widen(n + 2, 0, 2)
-            if n == 0:
-                cut_band(1)
             if n < 2:
                 widen(n + 2, 2, 1)
             else:
                 widen_most(n + 2)
-            if n == 0:
-                cut_band(-1)
-                park_edges()
             if n < 2:
                 widen_s(n + 2, 3)
             step(scores, n - 2)
             project(n, 0, [0])
             project(n, 1, [0])
             project(n, 0, [1])
-            turn_x(n + 1, 2)
+            if n > 0:
+                turn_x(n + 1, 2)
             empty_x(n + 1, 0)
             turn_x(n + 1, 3)
             step(empty_scores, n - 2)
@@ -509,38 +521,39 @@ def tile_localattention_pa_t_w4_kernel(tc, x_bytes, x_scale, Wq_words, Wq_scales
                 fetch(n - 3)
                 fetch(n - 2)
             empty_q(n, 0)
-            turn_k(n + 1, 0)
+            if n >= 2:
+                widen_rest(n + 2)
+            if n == 0:
+                turn_k(L, NT - 1, 1, "sc", 1)
+            turn_k(n, 0)
             empty_x(n + 1, 1)
             project(n, 1, [1])
             project(n, 2)
-            empty_k(n + 1, 0)
+            if n == 0:
+                empty_k(L, NT - 1, 1)
+            empty_k(n, 0)
             empty_q(n, 1)
             project(n, 3)
             empty_x(n + 1, 2)
             empty_q(n, 2)
-            if n == 1:
-                build_mask()
-            turn_k(n + 1, 1)
+            turn_k(n, 2)
             turn_x(n + 2, 0)
             empty_q(n, 3)
-            empty_k(n + 1, 1)
+            empty_k(n, 2)
             if n < 1:
                 empty_x(n + 1, 3, 0, NT, 0, 1)
                 empty_x(n + 1, 3, 0, NT, 1, 2)
             else:
                 empty_x(n + 1, 3)
             turn_x(n + 2, 1)
-            if n == 5:
-                pair_max(0)
             weave_q(n)
-            if n >= 2:
-                widen_rest(n + 2)
         quant_q(L - 3)
-        pair_shift(0)
-        pair_exp(0)
         clear(L - 1)
-        quant_k(L - 2)
+        quant_k(L - 3)
         quant_x(L - 1)
+        pair_max(0)
+        mask_edges()
+        pair_shift(0)
         scores(L - 3)
         project(L - 1, 0, [0])
         project(L - 1, 1, [0])
@@ -548,64 +561,70 @@ def tile_localattention_pa_t_w4_kernel(tc, x_bytes, x_scale, Wq_words, Wq_scales
         empty_x(L, 0, 0, 2)
         turn_x(L, 2)
         turn_x(L, 3)
+        pair_exp(0)
         empty_q(L - 1, 0)
         project(L - 1, 1, [1])
         project(L - 1, 2)
         mask_scores(L - 3)
+        pair_max(1)
         empty_x(L, 1, 0, 2)
         pair_sum(0)
-        pair_max(1)
+        pair_shift(1)
         row_max(L - 3)
         pair_recip(0)
-        pair_shift(1)
         quant_x(L, 0, 2, 1)
         pair_finish(0)
         store_boxes(0)
         empty_q(L - 1, 1)
         pair_exp(1)
-        turn_k(L, 0)
-        turn_k(L, 1)
+        turn_k(L - 1, 0)
+        turn_k(L - 1, 2)
+        turn_k(L, 2, 1, "sc", 1)
         empty_x(L, 2, 2, 1)
         pair_sum(1)
         empty_q(L - 1, 2)
-        exps(L - 3)
+        empty_k(L, 2, 1)
         project(L - 1, 3)
         project(L, 0, range(G), 0, 2)
         project(L, 1, range(G), 0, 2)
         quant_q(L - 2)
         pair_recip(1)
+        quant_k(L - 2)
         quant_x(L, 2, 1, 1)
         pair_finish(1)
         store_boxes(1)
-        empty_k(L, 0)
-        empty_x(L, 3, 3, 1)
         empty_q(L - 1, 3)
+        empty_k(L - 1, 0)
+        empty_x(L, 3, 3, 1)
         project(L, 2, range(G), 0, 2)
         project(L, 3, range(G), 0, 2)
-        empty_k(L, 1)
-        quant_k(L - 1)
-        quant_x(L, 3, 1, 1)
-        for t in range(4):
-            project(L, t, range(G), 2, 1, "tp", 4)
-        weave_q(L - 1)
-        recip(L - 3)
+        turn_k(L, 0)
         scores(L - 2)
         for t in range(4):
+            project(L, t, range(G), 2, 1)
+        weave_q(L - 1)
+        empty_k(L - 1, 2)
+        exps(L - 3)
+        mask_scores(L - 2)
+        quant_x(L, 3, 1, 1)
+        for t in range(4):
             project(L, t, range(G), 3, 1, "tp", 4)
+        empty_q_v(L, 2)
+        quant_q(L - 1)
+        quant_k(L - 1)
+        scores(L - 1)
+        empty_k(L, 0)
         for t in range(4):
             empty_q(L, t, 0, 2)
-        finish(L - 3)
-        store(L - 3)
         weave_q(L, 0, 2)
-        quant_k(L)
-        empty_q_v(L, 2)
-        mask_scores(L - 2)
-        quant_q(L - 1)
+        recip(L - 3)
         empty_q_v(L, 3)
-        scores(L - 1)
         row_max(L - 2)
+        quant_k(L)
         quant_q(L, 2, 2)
         scores(L, 2, 2, "tp", 4)
+        finish(L - 3)
+        store(L - 3)
         exps(L - 2)
         mask_scores(L - 1)
         quant_q(L, 0, 2)

@@ -32,11 +32,12 @@ WIDTH = Q + 2 * HALF
 MASKED = -1e9
 SCALE = 1.0 / math.sqrt(E)
 L = B - 1
-PARKED = 4
+PARKED = 5
 BAND = 2 * HALF + 1
 ROWS = 8
 PITCH = 16
 BOX = 3 * MARGIN
+PAIRS = (PARKED + 1) // 2
 ROOM = S * (STRIP + 1)
 STENCIL = Q + STRIP + 2 * MARGIN
 SHARE = 512
@@ -70,8 +71,8 @@ def tile_localattention_pa_t_w4_kernel(tc, x_bytes, x_scale, Wq_words, Wq_scales
         qc = [keep.tile([P, NT * 3 * Q], U32, name=f"qc{j}", align_bytes=64) for j in range(2)]
         qsc = [keep.tile([P, NT * 3 * Q], U8, name=f"qsc{j}", align_bytes=64) for j in range(2)]
 
-        diag = [keep.tile([P, ROWS, PITCH], F32, name=f"diag{j}", align_bytes=64) for j in range(PARKED // 2)]
-        boxes = [keep.tile([P, ROWS * BOX + ROWS], F32, name=f"boxes{j}", align_bytes=64) for j in range(PARKED // 2)]
+        diag = [keep.tile([P, ROWS, PITCH], F32, name=f"diag{j}", align_bytes=64) for j in range(PAIRS)]
+        boxes = [keep.tile([P, ROWS * BOX + ROWS], F32, name=f"boxes{j}", align_bytes=64) for j in range(PAIRS)]
 
         x_first = [keep.tile([P, D], U8, name=f"x_codes_first{i}", align_bytes=64) for i in range(2)]
         x_second = keep.tile([P, 2, D], U8, name="x_codes_second", align_bytes=64)
@@ -125,13 +126,16 @@ def tile_localattention_pa_t_w4_kernel(tc, x_bytes, x_scale, Wq_words, Wq_scales
             nc.vector.memset(qsc[j][:].bitcast(I32).rearrange("p (i u n) -> p i u n", i=NT, u=3)[:, :, 1, :], 0)
         for margin in (slice(0, LIVE.start), slice(LIVE.stop, STRIP)):
             nc.vector.memset(strips[:].rearrange("p j i c -> p (j i) c")[:, :, margin], 0.0)
-        for j in range(PARKED // 2):
+        for j in range(PAIRS):
             nc.scalar.activation(out=boxes[j][:], in_=zeros[:, 0 : ROWS * (BOX + 1)], func=ACT.Copy)
 
+        def clear_words(lo, hi, r):
+            n = (hi - lo) // (P * r)
+            rows = flat[lo:hi].rearrange("(p r n) -> p r n", p=P, r=r)
+            nc.sync.dma_start(out=rows, in_=zeros[:, 0:n].unsqueeze(1).to_broadcast([P, r, n]))
+
         def clear(b):
-            nc.sync.dma_start(
-                out=oflat[b].rearrange("(p r n) -> p r n", p=P, r=NT), in_=zeros[:].unsqueeze(1).to_broadcast([P, NT, S])
-            )
+            clear_words(b * S * S, (b + 1) * S * S, NT)
 
         def parked(b):
             return (L - 1) * S * S + b * ROOM
@@ -145,11 +149,16 @@ def tile_localattention_pa_t_w4_kernel(tc, x_bytes, x_scale, Wq_words, Wq_scales
             for s in range(2):
                 at = lo + Q * STENCIL * s + Q
                 rows = flat[at : at + Q * (STENCIL - 1)].rearrange("(r c) -> r c", r=Q)[:, 0:STRIP]
-                nc.sync.dma_start(out=mask[Q * s : Q * (s + 1)], in_=rows.unsqueeze(1).to_broadcast([Q, NT, STRIP]))
+                inner, outer = strip_parts(s)
+                nc.sync.dma_start(out=mask[Q * s : Q * (s + 1), inner, :], in_=rows.unsqueeze(1).to_broadcast([Q, NT - 1, STRIP]))
+                nc.sync.dma_start(out=mask[Q * s : Q * (s + 1), outer[0], outer[1]], in_=rows[:, outer[1]])
 
         def mask_edges():
             nc.vector.memset(mask[0:Q, 0, 0:MARGIN], MASKED)
             nc.vector.memset(mask[Q:P, NT - 1, STRIP - MARGIN : STRIP], MASKED)
+
+        def strip_parts(s):
+            return slice(1 - s, NT - s), (s * (NT - 1), slice(MARGIN * (1 - s), STRIP - MARGIN * s))
 
         def park_edges():
             for s in range(2):
@@ -158,6 +167,7 @@ def tile_localattention_pa_t_w4_kernel(tc, x_bytes, x_scale, Wq_words, Wq_scales
                 cells = view.rearrange("b (r j) -> r b j", r=Q)[:, :, 0:MARGIN]
                 nc.sync.dma_start(out=cells, in_=stencil[Q * s : Q * (s + 1), 0 : PARKED * MARGIN].rearrange("p (b j) -> p b j", b=PARKED))
 
+        mask_edges()
         park_edges()
         lay_stencil()
         for b in range(B):
@@ -334,7 +344,7 @@ def tile_localattention_pa_t_w4_kernel(tc, x_bytes, x_scale, Wq_words, Wq_scales
                     )
 
         def empty_scores(b):
-            raw[b] = work.tile([P, NT, STRIP], F32, name="raw", bufs=PARKED, align_bytes=64)
+            raw[b] = work.tile([P, NT, STRIP], F32, name="raw", bufs=4, align_bytes=64)
             window = sc[b, 0][:, :, SHIFT - MARGIN : SHIFT - MARGIN + STRIP]
             nc.scalar.activation(out=raw[b][:], in_=window, func=ACT.Copy, scale=SCALE)
 
@@ -343,9 +353,8 @@ def tile_localattention_pa_t_w4_kernel(tc, x_bytes, x_scale, Wq_words, Wq_scales
                 lo = parked(b) + (STRIP + 1) * Q * s
                 view = flat[lo : lo + ROOM].rearrange("(i y) -> i y", i=NT)[:, 0 : Q * STRIP].rearrange("i (r j) -> r i j", r=Q)
                 rows = raw[b][Q * s : Q * (s + 1)]
-                inner = slice(1 - s, NT - s)
+                inner, outer = strip_parts(s)
                 nc.sync.dma_start(out=view[:, inner, :], in_=rows[:, inner, :])
-                outer = (s * (NT - 1), slice(MARGIN * (1 - s), STRIP - MARGIN * s))
                 nc.sync.dma_start(out=view[:, outer[0], outer[1]], in_=rows[:, outer[0], outer[1]])
 
         def fetch(b):
@@ -353,31 +362,37 @@ def tile_localattention_pa_t_w4_kernel(tc, x_bytes, x_scale, Wq_words, Wq_scales
             view = flat[lo : lo + ROOM].rearrange("(p r y) -> p r y", r=ROWS, y=STRIP + 1)[:, :, 0:BAND]
             nc.sync.dma_start(out=diag[b // 2][Q * (b % 2) : Q * (b % 2 + 1), :, 0:BAND], in_=view)
 
+        def members(j):
+            return min(2, PARKED - 2 * j)
+
+        def held(j):
+            return slice(0, Q * members(j))
+
         def pair_max(j):
             top[j] = work.tile([P, ROWS], F32, name="top")
-            nc.vector.tensor_reduce(out=top[j][:], in_=diag[j][:, :, 0:BAND], axis=AX.X, op=ALU.max, negate=True)
+            nc.vector.tensor_reduce(out=top[j][held(j)], in_=diag[j][held(j), :, 0:BAND], axis=AX.X, op=ALU.max, negate=True)
 
-        def pair_shift(j):
-            live = diag[j][:, :, 0:BAND]
-            nc.vector.tensor_tensor(out=live, in0=live, in1=top[j][:].unsqueeze(2).to_broadcast([P, ROWS, BAND]), op=ALU.add)
+        def pair_shift(j, eng=nc.gpsimd):
+            live = diag[j][held(j), :, 0:BAND]
+            eng.tensor_tensor(out=live, in0=live, in1=top[j][held(j)].unsqueeze(2).to_broadcast([Q * members(j), ROWS, BAND]), op=ALU.add)
 
         def pair_exp(j):
-            live = diag[j][:, :, 0:BAND]
+            live = diag[j][held(j), :, 0:BAND]
             nc.scalar.activation(out=live, in_=live, func=ACT.Exp)
 
         def pair_sum(j):
             total[j] = work.tile([P, ROWS], F32, name="total")
-            nc.vector.tensor_reduce(out=total[j][:], in_=diag[j][:, :, 0:BAND], axis=AX.X, op=ALU.add)
+            nc.vector.tensor_reduce(out=total[j][held(j)], in_=diag[j][held(j), :, 0:BAND], axis=AX.X, op=ALU.add)
 
         def pair_recip(j):
             inverse[j] = work.tile([P, ROWS], F32, name="inverse")
-            nc.vector.reciprocal(out=inverse[j][:], in_=total[j][:])
+            nc.vector.reciprocal(out=inverse[j][held(j)], in_=total[j][held(j)])
 
-        def pair_finish(j):
+        def pair_finish(j, eng=nc.gpsimd):
             first = MARGIN - HALF
-            skew = boxes[j][:].rearrange("p (r c) -> p r c", r=ROWS)[:, :, first : first + BAND]
-            nc.vector.tensor_tensor(
-                out=skew, in0=diag[j][:, :, 0:BAND], in1=inverse[j][:].unsqueeze(2).to_broadcast([P, ROWS, BAND]), op=ALU.mult
+            skew = boxes[j][held(j)].rearrange("p (r c) -> p r c", r=ROWS)[:, :, first : first + BAND]
+            eng.tensor_tensor(
+                out=skew, in0=diag[j][held(j), :, 0:BAND], in1=inverse[j][held(j)].unsqueeze(2).to_broadcast([Q * members(j), ROWS, BAND]), op=ALU.mult
             )
 
         def box_rows(b, at, n, r):
@@ -387,22 +402,22 @@ def tile_localattention_pa_t_w4_kernel(tc, x_bytes, x_scale, Wq_words, Wq_scales
         def box_view(j):
             return boxes[j][:, 0 : ROWS * BOX].rearrange("p (r c) -> p r c", r=ROWS)
 
-        def store_later_rows(j):
-            for u in range(2):
-                nc.sync.dma_start(out=box_rows(2 * j + u, S, Q, ROWS - 1)[:, :, 0:BOX], in_=box_view(j)[Q * u : Q * (u + 1), 1:ROWS, :])
+        def store_later_rows(j, eng=nc.sync):
+            for u in range(members(j)):
+                eng.dma_start(out=box_rows(2 * j + u, S, Q, ROWS - 1)[:, :, 0:BOX], in_=box_view(j)[Q * u : Q * (u + 1), 1:ROWS, :])
 
-        def store_first_left(j):
-            for u in range(2):
-                nc.sync.dma_start(out=box_rows(2 * j + u, ROWS * (S + 1), Q - 1, 1)[:, 0, 0:MARGIN], in_=box_view(j)[Q * u + 1 : Q * (u + 1), 0, 0:MARGIN])
+        def store_first_left(j, eng=nc.sync):
+            for u in range(members(j)):
+                eng.dma_start(out=box_rows(2 * j + u, ROWS * (S + 1), Q - 1, 1)[:, 0, 0:MARGIN], in_=box_view(j)[Q * u + 1 : Q * (u + 1), 0, 0:MARGIN])
 
-        def store_first_right(j):
-            for u in range(2):
-                nc.sync.dma_start(out=box_rows(2 * j + u, MARGIN, Q, 1)[:, 0, 0 : BOX - MARGIN], in_=box_view(j)[Q * u : Q * (u + 1), 0, MARGIN:BOX])
+        def store_first_right(j, eng=nc.sync):
+            for u in range(members(j)):
+                eng.dma_start(out=box_rows(2 * j + u, MARGIN, Q, 1)[:, 0, 0 : BOX - MARGIN], in_=box_view(j)[Q * u : Q * (u + 1), 0, MARGIN:BOX])
 
-        def store_boxes(j):
-            store_later_rows(j)
-            store_first_left(j)
-            store_first_right(j)
+        def store_boxes(j, eng):
+            store_later_rows(j, eng)
+            store_first_left(j, eng)
+            store_first_right(j, eng)
 
         def mask_scores(b, i0=0, n=NT):
             sm[b, i0] = work.tile([P, n, WIDTH], F32, name="sm", bufs=6)
@@ -459,17 +474,17 @@ def tile_localattention_pa_t_w4_kernel(tc, x_bytes, x_scale, Wq_words, Wq_scales
                 op=ALU.mult,
             )
 
-        def warm_up():
+        def warm_up(n):
             idle = psum.tile([P, 2 * P], F32, name="acc", bufs=3)
-            nc.tensor.matmul(out=idle[:], lhsT=zeros[:, 0:P], rhs=zeros[:, 0 : 2 * P], start=True, stop=True)
+            nc.tensor.matmul(out=idle[:, 0:n], lhsT=zeros[:, 0:P], rhs=zeros[:, 0:n], start=True, stop=True)
 
         def step(fn, b, *args):
             if 0 <= b < B:
                 fn(b, *args)
 
-        warm_up()
-        warm_up()
-        warm_up()
+        warm_up(256)
+        warm_up(256)
+        warm_up(128)
         widen_v(0, 0)
         permute_codes()
         widen(0, 3, 1)
@@ -478,12 +493,12 @@ def tile_localattention_pa_t_w4_kernel(tc, x_bytes, x_scale, Wq_words, Wq_scales
         widen_s(0, 1)
         empty_x(0, 0)
         turn_x(0, 1)
-        warm_up()
+        warm_up(192)
         widen_s(0, 2)
         empty_x(0, 1)
         turn_x(0, 2)
         turn_x(0, 3)
-        warm_up()
+        warm_up(192)
         widen_s(1, 0)
         widen_s(1, 1)
         widen_s(1, 2)
@@ -494,6 +509,7 @@ def tile_localattention_pa_t_w4_kernel(tc, x_bytes, x_scale, Wq_words, Wq_scales
         empty_x(0, 3, 0, NT, 0, 1)
         empty_x(0, 3, 0, NT, 1, 2)
         turn_x(1, 2)
+        warm_up(128)
         for n in range(L - 1):
             step(quant_q, n - 2)
             if n == 2:
@@ -548,102 +564,108 @@ def tile_localattention_pa_t_w4_kernel(tc, x_bytes, x_scale, Wq_words, Wq_scales
             turn_x(n + 2, 1)
             weave_q(n)
         quant_q(L - 3)
-        clear(L - 1)
         quant_k(L - 3)
         quant_x(L - 1)
         pair_max(0)
-        mask_edges()
         pair_shift(0)
         scores(L - 3)
         project(L - 1, 0, [0])
         project(L - 1, 1, [0])
         project(L - 1, 0, [1])
-        empty_x(L, 0, 0, 2)
-        turn_x(L, 2)
-        turn_x(L, 3)
-        pair_exp(0)
-        empty_q(L - 1, 0)
         project(L - 1, 1, [1])
         project(L - 1, 2)
-        mask_scores(L - 3)
+        empty_x(L, 0, 0, 2)
+        quant_k(L - 2)
+        quant_q(L - 2)
+        turn_x(L, 2)
+        turn_x(L, 3)
+        turn_k(L - 1, 0)
+        empty_scores(L - 3)
+        park(L - 3)
+        clear_words(parked(0), parked(4), 3)
+        fetch(L - 3)
+        pair_exp(0)
+        empty_q(L - 1, 0)
+        project(L - 1, 3)
+        scores(L - 2)
         pair_max(1)
+        pair_shift(1)
         empty_x(L, 1, 0, 2)
         pair_sum(0)
-        pair_shift(1)
-        row_max(L - 3)
-        pair_recip(0)
         quant_x(L, 0, 2, 1)
+        pair_recip(0)
         pair_finish(0)
-        store_boxes(0)
+        store_later_rows(0)
+        store_first_left(0)
         empty_q(L - 1, 1)
         pair_exp(1)
-        turn_k(L - 1, 0)
-        turn_k(L - 1, 2)
-        turn_k(L, 2, 1, "sc", 1)
-        empty_x(L, 2, 2, 1)
-        pair_sum(1)
         empty_q(L - 1, 2)
-        empty_k(L, 2, 1)
-        project(L - 1, 3)
-        project(L, 0, range(G), 0, 2)
-        project(L, 1, range(G), 0, 2)
-        quant_q(L - 2)
-        pair_recip(1)
-        quant_k(L - 2)
-        quant_x(L, 2, 1, 1)
-        pair_finish(1)
-        store_boxes(1)
         empty_q(L - 1, 3)
         empty_k(L - 1, 0)
-        empty_x(L, 3, 3, 1)
-        project(L, 2, range(G), 0, 2)
-        project(L, 3, range(G), 0, 2)
+        for t in range(4):
+            project(L, t, range(G), 0, 2)
+        turn_k(L - 1, 2)
+        empty_x(L, 2, 2, 1)
+        mask_scores(L - 2)
         turn_k(L, 0)
-        scores(L - 2)
+        turn_k(L, 2, 1, "sc", 1)
+        pair_sum(1)
+        quant_x(L, 2, 1, 1)
+        pair_recip(1)
+        pair_finish(1)
+        store_later_rows(1)
+        store_first_right(0)
+        store_first_left(1)
+        clear_words(parked(4), L * S * S, 2)
+        store_first_right(1)
+        empty_x(L, 3, 3, 1)
+        row_max(L - 2)
         for t in range(4):
             project(L, t, range(G), 2, 1)
         weave_q(L - 1)
         empty_k(L - 1, 2)
-        exps(L - 3)
-        mask_scores(L - 2)
+        empty_k(L, 0)
+        empty_k(L, 2, 1)
+        pair_max(2)
         quant_x(L, 3, 1, 1)
+        pair_shift(2, nc.vector)
+        pair_exp(2)
         for t in range(4):
             project(L, t, range(G), 3, 1, "tp", 4)
-        empty_q_v(L, 2)
         quant_q(L - 1)
+        pair_sum(2)
         quant_k(L - 1)
+        pair_recip(2)
+        pair_finish(2)
+        store_boxes(2, nc.gpsimd)
+        empty_q_v(L, 2)
         scores(L - 1)
-        empty_k(L, 0)
         for t in range(4):
             empty_q(L, t, 0, 2)
         weave_q(L, 0, 2)
-        recip(L - 3)
+        exps(L - 2)
         empty_q_v(L, 3)
-        row_max(L - 2)
         quant_k(L)
         quant_q(L, 2, 2)
-        scores(L, 2, 2, "tp", 4)
-        finish(L - 3)
-        store(L - 3)
-        exps(L - 2)
-        mask_scores(L - 1)
         quant_q(L, 0, 2)
+        scores(L, 2, 2, "tp", 4)
         scores(L, 0, 2, "tp", 4)
         recip(L - 2)
-        row_max(L - 1)
         finish(L - 2)
         store_inner(L - 2)
+        mask_scores(L - 1)
         mask_scores(L, 2, 2)
-        exps(L - 1)
+        row_max(L - 1)
         mask_scores(L, 0, 2)
+        exps(L - 1)
         row_max(L, 2, 2)
         row_max(L, 0, 2)
-        recip(L - 1)
         exps(L, 2, 2)
         exps(L, 0, 2)
+        recip(L - 1)
+        recip(L, 2, 2)
         finish_v(L - 1)
         store_inner(L - 1)
-        recip(L, 2, 2)
         recip(L, 0, 2)
         finish(L, 2, 2)
         finish_v(L, 0, 2)

@@ -77,12 +77,18 @@ def tile_localattention_pa_t_w4_kernel(tc, x_bytes, x_scale, Wq_words, Wq_scales
         x_first = [keep.tile([P, D], U8, name=f"x_codes_first{i}", align_bytes=64) for i in range(2)]
         x_second = keep.tile([P, 2, D], U8, name="x_codes_second", align_bytes=64)
         x_tiles = [keep.tile([P, NT, D], U8, name=f"x_codes{b}", align_bytes=64) for b in range(B)]
+        x_rest = keep.tile([P, B - 2, SHARE], U8, name="x_rest", align_bytes=64)
+        rest = keep.tile([P, B - 2, SHARE], BF16, name="rest", align_bytes=64)
         k_tiles = [keep.tile([P, NT, E], BF16, name=f"k_rows{b}", align_bytes=64) for b in range(B)]
 
         xv = x_bytes.rearrange("b (i p) k -> b p i k", p=P)
         kflat = k.rearrange("b s e -> (b s) e")
         oflat = out.rearrange("b s j -> b (s j)")
         flat = out.rearrange("b s j -> (b s j)")
+
+        def load_x(b):
+            nc.sync.dma_start(out=x_tiles[b][:, 0 : NT - 1, :], in_=xv[b][:, 0 : NT - 1, :])
+            nc.sync.dma_start(out=x_tiles[b][:, NT - 1, 0 : D - SHARE], in_=xv[b][:, NT - 1, 0 : D - SHARE])
 
         def load_k(b):
             n = NT - (b == L)
@@ -105,7 +111,8 @@ def tile_localattention_pa_t_w4_kernel(tc, x_bytes, x_scale, Wq_words, Wq_scales
                 in_=Wq_scales[:, 4 * q : 4 * q + 4, :].rearrange("g r n -> r g n").bitcast(I32),
             )
         nc.sync.dma_start(out=x_tiles[1][:, 2:NT, :], in_=xv[1][:, 2:NT, :])
-        nc.sync.dma_start(out=x_tiles[2][:], in_=xv[2])
+        nc.sync.dma_start(out=x_rest[:], in_=x_bytes[2:B, S - P : S, D - SHARE : D].rearrange("b p k -> p b k"))
+        load_x(2)
         nc.sync.dma_start(out=bias[:], in_=bq.rearrange("(p t) -> p t", t=4))
         load_k(0)
         seam = B * S - (P - SHIFT)
@@ -113,7 +120,7 @@ def tile_localattention_pa_t_w4_kernel(tc, x_bytes, x_scale, Wq_words, Wq_scales
         nc.sync.dma_start(out=k_tiles[L][Q : P - SHIFT, NT - 1, :], in_=kflat[seam + Q : B * S, :])
         nc.sync.dma_start(out=k_tiles[L][P - SHIFT : P, NT - 1, :], in_=kflat[0:SHIFT, :])
         for b in range(3, B):
-            nc.sync.dma_start(out=x_tiles[b][:], in_=xv[b])
+            load_x(b)
             load_k(b - 2)
         load_k(L - 1)
         load_k(L)
@@ -210,17 +217,20 @@ def tile_localattention_pa_t_w4_kernel(tc, x_bytes, x_scale, Wq_words, Wq_scales
             codes = x_tiles[b][:].rearrange("p i k -> p (i k)")[:, 2 * D : NT * D - SHARE]
             nc.gpsimd.tensor_copy(out=wide(b, 0, NT)[:, 2 * D : NT * D - SHARE], in_=codes.bitcast(FP8))
 
-        def widen_rest(b):
-            codes = x_tiles[b][:].rearrange("p i k -> p (i k)")[:, NT * D - SHARE :]
-            nc.scalar.copy(out=wide(b, 0, NT)[:, NT * D - SHARE :], in_=codes.bitcast(FP8))
+        def widen_rest(lo, hi):
+            codes = x_rest[:, lo - 2 : hi - 2, :].rearrange("p b k -> p (b k)")
+            nc.scalar.copy(out=rest[:, lo - 2 : hi - 2, :].rearrange("p b k -> p (b k)"), in_=codes.bitcast(FP8))
 
         def turn_x(b, i, passes=range(G)):
             words = wide(b, i).bitcast(F32)
             if (b, i) not in xt:
                 xt[b, i] = psum.tile([P, 2, G, P], F32, name="tp", bufs=4)
             for g in passes:
+                part = words[:, 256 * g : 256 * (g + 1)]
+                if b > 1 and (i, g) == (NT - 1, G - 1):
+                    part = rest[:, b - 2, :].bitcast(F32)
                 for h in range(2):
-                    nc.tensor.transpose(xt[b, i][:, h, g, :], words[:, 256 * g + h : 256 * (g + 1) : 2], ident[:])
+                    nc.tensor.transpose(xt[b, i][:, h, g, :], part[:, h:256:2], ident[:])
 
         def woven_x(b):
             return ring[b % 3][:]
@@ -501,8 +511,9 @@ def tile_localattention_pa_t_w4_kernel(tc, x_bytes, x_scale, Wq_words, Wq_scales
         warm_up(192)
         widen_s(1, 0)
         widen_s(1, 1)
-        widen_s(1, 2)
+        widen(1, 2, 1)
         widen_s(1, 3)
+        widen_rest(2, 6)
         turn_x(1, 0)
         empty_x(0, 2)
         turn_x(1, 1)
@@ -517,12 +528,7 @@ def tile_localattention_pa_t_w4_kernel(tc, x_bytes, x_scale, Wq_words, Wq_scales
             step(quant_k, n - 2)
             quant_x(n)
             widen(n + 2, 0, 2)
-            if n < 2:
-                widen(n + 2, 2, 1)
-            else:
-                widen_most(n + 2)
-            if n < 2:
-                widen_s(n + 2, 3)
+            widen_most(n + 2)
             step(scores, n - 2)
             project(n, 0, [0])
             project(n, 1, [0])
@@ -537,8 +543,8 @@ def tile_localattention_pa_t_w4_kernel(tc, x_bytes, x_scale, Wq_words, Wq_scales
                 fetch(n - 3)
                 fetch(n - 2)
             empty_q(n, 0)
-            if n >= 2:
-                widen_rest(n + 2)
+            if n == 2:
+                widen_rest(6, B)
             if n == 0:
                 turn_k(L, NT - 1, 1, "sc", 1)
             turn_k(n, 0)

@@ -40,7 +40,9 @@ BOX = 3 * MARGIN
 PAIRS = (PARKED + 1) // 2
 ROOM = S * (STRIP + 1)
 STENCIL = Q + STRIP + 2 * MARGIN
-SHARE = 512
+COUNTS = [(0, 2, 2, 1, 4), (2, 2, 3, 1, 2), (1, 2, 3, 1, 0), (1, 2, 3, 1, 0), (1, 2, 3, 1, 0), (1, 2, 3, 1, 0)]
+SHARED = (1, 3, 4, 5, 6, 7)
+WIDE = 4
 
 
 def tile_localattention_pa_t_w4_kernel(tc, x_bytes, x_scale, Wq_words, Wq_scales, bq, k, out):
@@ -53,9 +55,12 @@ def tile_localattention_pa_t_w4_kernel(tc, x_bytes, x_scale, Wq_words, Wq_scales
 
         ident = keep.tile([P, P], F32, name="ident")
         scale_p = keep.tile([P, G, 4], F32, name="scale_p")
-        ring = [keep.tile([P, NT * D], BF16, name=f"ring{j}", align_bytes=64) for j in range(3)]
-        qi = [keep.tile([P, S * 4], BF16, name=f"qi{j}", align_bytes=64) for j in range(2)]
-        kt = [keep.tile([P, S * 4], BF16, name=f"kt{j}", align_bytes=64) for j in range(3)]
+        wides = [keep.tile([P, NT * D], BF16, name=f"wide{j}", align_bytes=64) for j in range(WIDE)]
+        rows = keep.tile([P, 4 * S * (G + 1)], BF16, name="rows", align_bytes=64)
+        planes = [keep.tile([P, 4, P + S], BF16, name=f"planes{j}", align_bytes=64) for j in range(2)]
+        first_planes = keep.tile([P, G, 4, P], BF16, name="first_planes", align_bytes=64)
+        q_tail = [keep.tile([P, S * 4], BF16, name=f"q_tail{j}", align_bytes=64) for j in range(2)]
+        kt = [keep.tile([P, S * 4], BF16, name=f"kt{j}", align_bytes=64) for j in range(2)]
         k_last = keep.tile([P, S * 4], BF16, name="k_last", align_bytes=64)
         strips = keep.tile([P, B - PARKED, NT, STRIP], F32, name="strips")
         w_raw = [keep.tile([P, 2 * E], U8, name=f"w_raw{g}", align_bytes=64) for g in range(G)]
@@ -77,9 +82,8 @@ def tile_localattention_pa_t_w4_kernel(tc, x_bytes, x_scale, Wq_words, Wq_scales
         x_first = [keep.tile([P, D], U8, name=f"x_codes_first{i}", align_bytes=64) for i in range(2)]
         x_second = keep.tile([P, 2, D], U8, name="x_codes_second", align_bytes=64)
         x_tiles = [keep.tile([P, NT, D], U8, name=f"x_codes{b}", align_bytes=64) for b in range(B)]
-        x_rest = keep.tile([P, B - 2, SHARE], U8, name="x_rest", align_bytes=64)
-        rest = keep.tile([P, B - 2, SHARE], BF16, name="rest", align_bytes=64)
         k_tiles = [keep.tile([P, NT, E], BF16, name=f"k_rows{b}", align_bytes=64) for b in range(B)]
+        k_seam = keep.tile([P, E], BF16, name="k_seam", align_bytes=64)
 
         xv = x_bytes.rearrange("b (i p) k -> b p i k", p=P)
         kflat = k.rearrange("b s e -> (b s) e")
@@ -87,23 +91,28 @@ def tile_localattention_pa_t_w4_kernel(tc, x_bytes, x_scale, Wq_words, Wq_scales
         flat = out.rearrange("b s j -> (b s j)")
 
         def load_x(b):
-            nc.sync.dma_start(out=x_tiles[b][:, 0 : NT - 1, :], in_=xv[b][:, 0 : NT - 1, :])
-            nc.sync.dma_start(out=x_tiles[b][:, NT - 1, 0 : D - SHARE], in_=xv[b][:, NT - 1, 0 : D - SHARE])
+            nc.sync.dma_start(out=x_tiles[b][:], in_=xv[b])
 
         def load_k(b):
             n = NT - (b == L)
-            rows = kflat[S * b + SHIFT : S * b + SHIFT + P * n, :]
-            nc.sync.dma_start(out=k_tiles[b][:, 0:n, :], in_=rows.rearrange("(i p) e -> p i e", p=P))
+            source = kflat[S * b + SHIFT : S * b + SHIFT + P * n, :]
+            nc.sync.dma_start(out=k_tiles[b][:, 0:n, :], in_=source.rearrange("(i p) e -> p i e", p=P))
+
+        def load_seam():
+            seam = B * S - (P - SHIFT)
+            nc.sync.dma_start(out=k_seam[0:Q, :], in_=kflat[seam : seam + Q, :])
+            nc.sync.dma_start(out=k_seam[Q : P - SHIFT, :], in_=kflat[seam + Q : B * S, :])
+            nc.sync.dma_start(out=k_seam[P - SHIFT : P, :], in_=kflat[0:SHIFT, :])
 
         nc.vector.memset(zeros[:], 0.0)
         nc.vector.memset(ident[:], 0.0)
         nc.vector.memset(ws_raw[:].rearrange("p g n -> p (g n)").bitcast(I32), 0)
         nc.sync.dma_start(out=x_first[0][:], in_=xv[0][:, 0, :])
         nc.sync.dma_start(out=x_first[1][:], in_=xv[0][:, 1, :])
-        for g in range(G):
-            nc.sync.dma_start(out=w_raw[g][:].bitcast(I32), in_=Wq_words[g].bitcast(I32))
-        nc.sync.dma_start(out=scale_p[:], in_=x_scale.rearrange("a b (g p c) -> p (a b g) c", p=P, c=4))
+        nc.sync.dma_start(out=w_raw[0][:].bitcast(I32), in_=Wq_words[0].bitcast(I32))
         nc.sync.dma_start(out=x_tiles[0][:, 2:NT, :], in_=xv[0][:, 2:NT, :])
+        nc.sync.dma_start(out=w_raw[1][:].bitcast(I32), in_=Wq_words[1].bitcast(I32))
+        nc.sync.dma_start(out=scale_p[:], in_=x_scale.rearrange("a b (g p c) -> p (a b g) c", p=P, c=4))
         nc.sync.dma_start(out=x_second[:], in_=xv[1][:, 0:2, :])
         for q in range(4):
             nc.sync.dma_start(
@@ -111,17 +120,13 @@ def tile_localattention_pa_t_w4_kernel(tc, x_bytes, x_scale, Wq_words, Wq_scales
                 in_=Wq_scales[:, 4 * q : 4 * q + 4, :].rearrange("g r n -> r g n").bitcast(I32),
             )
         nc.sync.dma_start(out=x_tiles[1][:, 2:NT, :], in_=xv[1][:, 2:NT, :])
-        nc.sync.dma_start(out=x_rest[:], in_=x_bytes[2:B, S - P : S, D - SHARE : D].rearrange("b p k -> p b k"))
+        load_k(0)
         load_x(2)
         nc.sync.dma_start(out=bias[:], in_=bq.rearrange("(p t) -> p t", t=4))
-        load_k(0)
-        seam = B * S - (P - SHIFT)
-        nc.sync.dma_start(out=k_tiles[L][0:Q, NT - 1, :], in_=kflat[seam : seam + Q, :])
-        nc.sync.dma_start(out=k_tiles[L][Q : P - SHIFT, NT - 1, :], in_=kflat[seam + Q : B * S, :])
-        nc.sync.dma_start(out=k_tiles[L][P - SHIFT : P, NT - 1, :], in_=kflat[0:SHIFT, :])
+        load_seam()
         for b in range(3, B):
-            load_x(b)
             load_k(b - 2)
+            load_x(b)
         load_k(L - 1)
         load_k(L)
 
@@ -177,21 +182,19 @@ def tile_localattention_pa_t_w4_kernel(tc, x_bytes, x_scale, Wq_words, Wq_scales
         mask_edges()
         park_edges()
         lay_stencil()
-        for b in range(B):
-            if b != L - 1:
-                clear(b)
+        clear(0)
         load_mask()
+        clear(1)
 
         xt, xc, xsc, ktp, acc, qp = {}, {}, {}, {}, {}, {}
         sc, sm, nm, ss, rs = {}, {}, {}, {}, {}
         raw, top, total, inverse = {}, {}, {}, {}
 
-        def permute_codes():
-            for g in range(G):
-                nc.vector.tensor_copy(
-                    out=w_perm[:, g, :].rearrange("p (t m c) -> p t m c", t=4, c=2),
-                    in_=w_raw[g][:].rearrange("p (m t c) -> p t m c", t=4, c=2),
-                )
+        def permute_codes(g):
+            nc.vector.tensor_copy(
+                out=w_perm[:, g, :].rearrange("p (t m c) -> p t m c", t=4, c=2),
+                in_=w_raw[g][:].rearrange("p (m t c) -> p t m c", t=4, c=2),
+            )
 
         def permute_scales():
             nc.gpsimd.tensor_copy(
@@ -200,82 +203,85 @@ def tile_localattention_pa_t_w4_kernel(tc, x_bytes, x_scale, Wq_words, Wq_scales
             )
 
         def wide(b, i, n=1):
-            return ring[(b + 1) % 3][:, D * i : D * (i + n)]
+            return wides[b % WIDE][:, D * i : D * (i + n)]
 
-        def widen_s(b, i):
-            codes = x_tiles[b][:, i, :] if b > 1 or i > 1 else x_second[:, i, :] if b else x_first[i][:]
-            nc.scalar.copy(out=wide(b, i), in_=codes.bitcast(FP8))
+        def widen(copy, b, i):
+            codes = x_tiles[b][:, i, :] if i > 1 else x_second[:, i, :] if b else x_first[i][:]
+            copy(out=wide(b, i), in_=codes.bitcast(FP8))
 
-        def widen_v(b, i):
-            nc.vector.tensor_copy(out=wide(b, i), in_=x_first[i][:].bitcast(FP8))
+        halves = [(b, u) for b in range(2, B) for u in [2 * NT - 1] + list(range(2 * NT - 1))]
 
-        def widen(b, i0=0, n=NT):
-            codes = x_tiles[b][:, i0 : i0 + n, :].rearrange("p i k -> p (i k)")
-            nc.gpsimd.tensor_copy(out=wide(b, i0, n), in_=codes.bitcast(FP8))
+        def widen_next(copy, count):
+            while count:
+                b, u = halves[0]
+                run = 1
+                while run < count and halves[run] == (b, u + run):
+                    run += 1
+                cols = slice(512 * u, 512 * (u + run))
+                codes = x_tiles[b][:].rearrange("p i k -> p (i k)")[:, cols]
+                copy(out=wide(b, 0, NT)[:, cols], in_=codes.bitcast(FP8))
+                for j in range(run):
+                    halves.remove(halves[0])
+                count -= run
 
-        def widen_most(b):
-            codes = x_tiles[b][:].rearrange("p i k -> p (i k)")[:, 2 * D : NT * D - SHARE]
-            nc.gpsimd.tensor_copy(out=wide(b, 0, NT)[:, 2 * D : NT * D - SHARE], in_=codes.bitcast(FP8))
+        def bank(name, shape):
+            return psum.tile(shape, F32, name=name, bufs=1)
 
-        def widen_rest(lo, hi):
-            codes = x_rest[:, lo - 2 : hi - 2, :].rearrange("p b k -> p (b k)")
-            nc.scalar.copy(out=rest[:, lo - 2 : hi - 2, :].rearrange("p b k -> p (b k)"), in_=codes.bitcast(FP8))
-
-        def turn_x(b, i, passes=range(G)):
+        def turn_x(b, i, room, passes=range(G)):
             words = wide(b, i).bitcast(F32)
-            if (b, i) not in xt:
-                xt[b, i] = psum.tile([P, 2, G, P], F32, name="tp", bufs=4)
             for g in passes:
-                part = words[:, 256 * g : 256 * (g + 1)]
-                if b > 1 and (i, g) == (NT - 1, G - 1):
-                    part = rest[:, b - 2, :].bitcast(F32)
+                xt[b, i, g] = room
                 for h in range(2):
-                    nc.tensor.transpose(xt[b, i][:, h, g, :], part[:, h:256:2], ident[:])
+                    nc.tensor.transpose(room[:, h, g, :], words[:, 256 * g + h : 256 * (g + 1) : 2], ident[:])
 
-        def woven_x(b):
-            return ring[b % 3][:]
+        def x_bank(name):
+            return bank(name, [P, 2, G, P])
 
-        def rows_x(b, i0, n):
-            room = woven_x(b)[:, G * 4 * P * i0 : G * 4 * P * (i0 + n)]
+        def rows_x(i0, n):
+            room = rows[:, G * 4 * P * i0 : G * 4 * P * (i0 + n)]
             return room.rearrange("p (g n h e) -> p g n h e", g=G, h=2, e=2)
 
         def empty_x(b, i, i0=0, n=NT, g0=0, g1=G):
-            dst = rows_x(b, i0, n)[:, g0:g1, P * (i - i0) : P * (i - i0 + 1)]
-            values = xt[b, i][:].bitcast(BF16).rearrange("p h g (r e) -> p g r h e", e=2)[:, g0:g1]
+            dst = rows_x(i0, n)[:, g0:g1, P * (i - i0) : P * (i - i0 + 1)]
+            values = xt[b, i, g0][:].bitcast(BF16).rearrange("p h g (r e) -> p g r h e", e=2)[:, g0:g1]
             scales = scale_p[:, g0:g1].rearrange("p g (h e) -> p g h e", e=2).unsqueeze(2).to_broadcast([P, g1 - g0, P, 2, 2])
             nc.vector.tensor_tensor(out=dst, in0=values, in1=scales, op=ALU.mult)
 
-        def empty_x_s(b, i, g, i0=0, n=NT):
-            dst = rows_x(b, i0, n)[:, g, P * (i - i0) : P * (i - i0 + 1)].rearrange("p n h e -> p (n h e)")
-            planes = work.tile([P, 2, P], F32, name="x_planes", align_bytes=64)
-            for e in range(2):
-                for h in range(2):
-                    nc.scalar.activation(
-                        out=planes[:, h, :].bitcast(BF16)[:, e::2],
-                        in_=xt[b, i][:, h, g, :].bitcast(BF16)[:, e::2],
-                        func=ACT.Copy,
-                        scale=scale_p[:, g, 2 * h + e : 2 * h + e + 1],
-                    )
-            nc.scalar.copy(out=dst.bitcast(F32).rearrange("p (r h) -> p r h", h=2), in_=planes[:].rearrange("p h r -> p r h"))
+        def plane_x(b, i, g, dst):
+            for t in range(4):
+                values = xt[b, i, g][:, t // 2, g, :].bitcast(BF16)[:, t % 2 :: 2]
+                nc.scalar.activation(out=dst[:, t, :], in_=values, func=ACT.Copy, scale=scale_p[:, g, t : t + 1])
 
-        def quant_x(b, i0=0, n=NT, cuts=G):
-            if (b, 0) not in xc:
-                xc[b, 0] = work.tile([P, G * S], U32, name="xc", align_bytes=64)
-                xsc[b, 0] = work.tile([P, G * S], U8, name="xsc", align_bytes=64)
+        def share_x(b):
+            plane_x(b, NT - 1, G - 1, planes[b % 2][:, :, 0:P])
+
+        def lace(b, lo=0, hi=P + S):
+            at = 4 * (G * S - P)
+            dst = rows[:, at + 4 * lo : at + 4 * hi].rearrange("p (n t) -> p n t", t=4)
+            nc.gpsimd.tensor_copy(out=dst, in_=planes[b % 2][:, :, lo:hi].rearrange("p t n -> p n t"))
+
+        def lace_first(i, g):
+            dst = rows_x(0, NT)[:, g, P * i : P * (i + 1)].rearrange("p n h e -> p n (h e)")
+            nc.gpsimd.tensor_copy(out=dst, in_=first_planes[:, g].rearrange("p t n -> p n t"))
+
+        def quant_x(b, i0=0, n=NT, cuts=G, parts=range(G)):
+            if b not in xc:
+                xc[b] = work.tile([P, G * S], U32, name="xc", align_bytes=64)
+                xsc[b] = work.tile([P, G * S], U8, name="xsc", align_bytes=64)
             w = G * P * n // cuts
-            for g in range(cuts):
+            for g in parts[:cuts]:
                 cols = slice(G * P * i0 + w * g, G * P * i0 + w * (g + 1))
                 nc.vector.quantize_mx(
-                    out=xc[b, 0][:, cols].bitcast(FP8X4), scales=xsc[b, 0][:, cols], in_=woven_x(b)[:, 4 * cols.start : 4 * cols.stop]
+                    out=xc[b][:, cols].bitcast(FP8X4), scales=xsc[b][:, cols], in_=rows[:, 4 * cols.start : 4 * cols.stop]
                 )
 
         def rows_k(b):
-            return k_last[:] if b == L else kt[b % 3][:]
+            return k_last[:] if b == L else kt[b % 2][:] if b else rows[:, 4 * G * S :]
 
-        def turn_k(b, j0, n=2, tag="tp", bufs=4):
-            ktp[b, j0] = psum.tile([P, n, 2, P], F32, name=tag, bufs=bufs)
+        def turn_k(b, j0, name, n=2):
+            ktp[b, j0] = bank(name, [P, n, 2, P])
             for j in range(n):
-                words = k_tiles[b][:, j0 + j, :].bitcast(F32)
+                words = (k_seam[:] if (b, j0 + j) == (L, NT - 1) else k_tiles[b][:, j0 + j, :]).bitcast(F32)
                 for h in range(2):
                     nc.tensor.transpose(ktp[b, j0][:, j, h, :], words[:, h:256:2], ident[:])
 
@@ -290,21 +296,24 @@ def tile_localattention_pa_t_w4_kernel(tc, x_bytes, x_scale, Wq_words, Wq_scales
             cols = slice(S * b + Q, S * (b + 1) + Q)
             nc.vector.quantize_mx(out=kc[:, cols].bitcast(FP8X4), scales=ksc[:, cols], in_=rows_k(b))
 
-        def project(b, t, passes=range(G), i0=0, n=NT, tag="acc", bufs=3):
+        def project(b, t, passes=range(G), i0=0, n=NT, name=None):
             per = NT // n
             if (b, i0, t // per) not in acc:
-                acc[b, i0, t // per] = psum.tile([P, per, n * P], F32, name=tag, bufs=bufs)
+                acc[b, i0, t // per] = bank(name or f"sum{(4 * b + t) % 3}", [P, per, n * P])
             for g in passes:
                 cols = slice(G * P * i0 + n * P * g, G * P * i0 + n * P * (g + 1))
                 nc.tensor.matmul_mx(
                     out=acc[b, i0, t // per][:, t % per, :],
                     lhsT=w_perm[:, g, 256 * t : 256 * (t + 1)].bitcast(FP4X4),
                     lhsT_scale=ws_perm[:, g, P * t : P * (t + 1)],
-                    rhs=xc[b, 0][:, cols].bitcast(FP8X4),
-                    rhs_scale=xsc[b, 0][:, cols],
+                    rhs=xc[b][:, cols].bitcast(FP8X4),
+                    rhs_scale=xsc[b][:, cols],
                     start=(g == 0),
                     stop=(g == G - 1),
                 )
+
+        def plane_q(b, t):
+            nc.scalar.activation(out=planes[b % 2][:, t, P:], in_=acc[b, 0, t][:, 0, :], func=ACT.Identity, bias=bias[:, t : t + 1])
 
         def empty_q(b, t, i0=0, n=NT):
             if b not in qp:
@@ -314,7 +323,7 @@ def tile_localattention_pa_t_w4_kernel(tc, x_bytes, x_scale, Wq_words, Wq_scales
             nc.scalar.activation(out=pair[:, t % 2 :: 2], in_=acc[b, i0, t // per][:, t % per, :], func=ACT.Identity, bias=bias[:, t : t + 1])
 
         def rows_q(b):
-            return qi[b % 2][:]
+            return rows[:, 4 * G * S :] if b < L - 1 else q_tail[b % 2][:]
 
         def weave_q(b, i0=0, n=NT):
             dst = rows_q(b)[:, 4 * P * i0 : 4 * P * (i0 + n)].bitcast(F32).rearrange("p (n h) -> p n h", h=2)
@@ -337,8 +346,8 @@ def tile_localattention_pa_t_w4_kernel(tc, x_bytes, x_scale, Wq_words, Wq_scales
                     out=qc[b % 2][:, cols].bitcast(FP8X4), scales=qsc[b % 2][:, cols], in_=rows_q(b)[:, 4 * lo : 4 * hi]
                 )
 
-        def scores(b, i0=0, n=NT, tag="sc", bufs=1):
-            sc[b, i0] = psum.tile([P, n, P], F32, name=tag, bufs=bufs)
+        def scores(b, i0=0, n=NT, name="scores"):
+            sc[b, i0] = bank(name, [P, n, P])
             for i in range(i0, i0 + n):
                 for s in range(2):
                     qcols = slice(Q * (3 * i + s), Q * (3 * i + s) + P)
@@ -476,201 +485,224 @@ def tile_localattention_pa_t_w4_kernel(tc, x_bytes, x_scale, Wq_words, Wq_scales
             for i in range(n):
                 nc.scalar.activation(out=strip[:, i, :], in_=sm[b, i0][:, i, :], func=ACT.Copy, scale=rs[b, i0][:, i : i + 1])
 
-        def finish_v(b, i0=0, n=NT):
+        def finish_v(b, i0=0, n=NT, lo=0):
             nc.vector.tensor_tensor(
-                out=strips[:, b - PARKED, i0 : i0 + n, LIVE],
-                in0=sm[b, i0][:],
-                in1=rs[b, i0][:].unsqueeze(2).to_broadcast([P, n, WIDTH]),
+                out=strips[:, b - PARKED, i0 + lo : i0 + n, LIVE],
+                in0=sm[b, i0][:, lo:n],
+                in1=rs[b, i0][:, lo:n].unsqueeze(2).to_broadcast([P, n - lo, WIDTH]),
                 op=ALU.mult,
             )
-
-        def warm_up(n):
-            idle = psum.tile([P, 2 * P], F32, name="acc", bufs=3)
-            nc.tensor.matmul(out=idle[:, 0:n], lhsT=zeros[:, 0:P], rhs=zeros[:, 0:n], start=True, stop=True)
 
         def step(fn, b, *args):
             if 0 <= b < B:
                 fn(b, *args)
 
-        warm_up(256)
-        warm_up(256)
-        warm_up(128)
-        widen_v(0, 0)
-        permute_codes()
-        widen(0, 3, 1)
+        def turning(n):
+            return f"turn{1 + n % 3}"
+
+        on_s, on_v, on_g = nc.scalar.copy, nc.vector.tensor_copy, nc.gpsimd.tensor_copy
+
+        widen(on_v, 0, 0)
+        widen(on_s, 0, 1)
+        widen(on_s, 0, 2)
+        widen(on_s, 0, 3)
+        for g in range(G):
+            permute_codes(g)
         permute_scales()
-        turn_x(0, 0)
-        widen_s(0, 1)
+        turn_x(0, 0, x_bank("sum0"))
+        turn_x(0, 1, x_bank("sum1"))
+        turn_x(0, 2, x_bank("sum2"))
+        turn_x(0, 3, x_bank("scores"))
         empty_x(0, 0)
-        turn_x(0, 1)
-        warm_up(192)
-        widen_s(0, 2)
-        empty_x(0, 1)
-        turn_x(0, 2)
-        turn_x(0, 3)
-        warm_up(192)
-        widen_s(1, 0)
-        widen_s(1, 1)
-        widen(1, 2, 1)
-        widen_s(1, 3)
-        widen_rest(2, 6)
-        turn_x(1, 0)
+        for g in range(G):
+            plane_x(0, 1, g, first_planes[:, g])
+            lace_first(1, g)
         empty_x(0, 2)
-        turn_x(1, 1)
+        widen(on_s, 1, 0)
+        widen(on_s, 1, 3)
+        widen(on_s, 1, 1)
+        turn_x(1, 0, x_bank("turn0"))
+        turn_x(1, 3, x_bank("sum0"), [1])
+        turn_x(1, 1, x_bank(turning(0)))
+        turn_k(0, 0, turning(1))
+        turn_k(0, 2, turning(-1))
         empty_x(0, 3, 0, NT, 0, 1)
         empty_x(0, 3, 0, NT, 1, 2)
-        turn_x(1, 2)
-        warm_up(128)
+        share_x(1)
+        widen(on_s, 1, 2)
+        empty_k(0, 0)
+        empty_k(0, 2)
+        widen_next(on_s, 1)
         for n in range(L - 1):
-            step(quant_q, n - 2)
+            counts = COUNTS[n]
+            if n > 1:
+                quant_k(n - 1)
             if n == 2:
                 quant_seam()
-            step(quant_k, n - 2)
+            if n == L - 2:
+                pair_shift(0, nc.vector)
+                pair_exp(0)
+            if n + 1 in SHARED:
+                step(quant_q, n - 2)
             quant_x(n)
-            widen(n + 2, 0, 2)
-            widen_most(n + 2)
+            if n + 1 not in SHARED:
+                step(quant_q, n - 2)
+            if n == 1:
+                quant_k(0)
+            widen_next(on_s, counts[0])
             step(scores, n - 2)
             project(n, 0, [0])
             project(n, 1, [0])
             project(n, 0, [1])
-            if n > 0:
-                turn_x(n + 1, 2)
-            empty_x(n + 1, 0)
-            turn_x(n + 1, 3)
+            empty_x(n + 1, 0, 0, NT, 0, 1)
+            if n + 1 not in SHARED:
+                empty_x(n + 1, 3, 0, NT, 1, 2)
+            turn_x(n + 1, 2, x_bank(turning(n + 1)))
+            empty_x(n + 1, 0, 0, NT, 1, 2)
             step(empty_scores, n - 2)
-            step(park, n - 2)
+            if n == L - 2:
+                pair_sum(0)
+            if n >= 2:
+                park(n - 2)
+                clear(n)
             if n % 2 and n > 2:
                 fetch(n - 3)
                 fetch(n - 2)
-            empty_q(n, 0)
-            if n == 2:
-                widen_rest(6, B)
+            if n == 3:
+                clear(L)
+            mixed = x_bank(turning(n - 1))
+            turn_x(n + 1, 3, mixed, [0])
+            turn_x(n + 2, 3, mixed, [1])
+            widen_next(on_s, counts[1])
+            lace(n + 1, 0 if n + 1 in SHARED else P, P + S if n else P)
+            widen_next(on_g, counts[4])
+            plane_q(n, 0)
+            widen_next(on_s, counts[2])
             if n == 0:
-                turn_k(L, NT - 1, 1, "sc", 1)
-            turn_k(n, 0)
+                turn_k(L, NT - 1, "scores", 1)
+            else:
+                turn_k(n, 2, "turn0")
             empty_x(n + 1, 1)
+            if n == L - 2:
+                pair_recip(0)
             project(n, 1, [1])
             project(n, 2)
+            project(n, 3)
             if n == 0:
                 empty_k(L, NT - 1, 1)
-            empty_k(n, 0)
-            empty_q(n, 1)
-            project(n, 3)
-            empty_x(n + 1, 2)
-            empty_q(n, 2)
-            turn_k(n, 2)
-            turn_x(n + 2, 0)
-            empty_q(n, 3)
-            empty_k(n, 2)
-            if n < 1:
-                empty_x(n + 1, 3, 0, NT, 0, 1)
-                empty_x(n + 1, 3, 0, NT, 1, 2)
             else:
-                empty_x(n + 1, 3)
-            turn_x(n + 2, 1)
-            weave_q(n)
-        quant_q(L - 3)
-        quant_k(L - 3)
-        quant_x(L - 1)
-        pair_max(0)
-        pair_shift(0)
-        scores(L - 3)
-        project(L - 1, 0, [0])
-        project(L - 1, 1, [0])
-        project(L - 1, 0, [1])
-        project(L - 1, 1, [1])
-        project(L - 1, 2)
-        empty_x(L, 0, 0, 2)
-        quant_k(L - 2)
-        quant_q(L - 2)
-        turn_x(L, 2)
-        turn_x(L, 3)
-        turn_k(L - 1, 0)
-        empty_scores(L - 3)
-        park(L - 3)
-        clear_words(parked(0), parked(4), 3)
-        fetch(L - 3)
-        pair_exp(0)
-        empty_q(L - 1, 0)
-        project(L - 1, 3)
-        scores(L - 2)
-        pair_max(1)
-        pair_shift(1)
-        empty_x(L, 1, 0, 2)
-        pair_sum(0)
-        quant_x(L, 0, 2, 1)
-        pair_recip(0)
-        pair_finish(0)
+                empty_k(n, 2)
+            plane_q(n, 1)
+            widen_next(on_s, counts[3])
+            empty_x(n + 1, 2, 0, NT, 0, 1)
+            empty_x(n + 1, 3, 0, NT, 0, 1)
+            empty_x(n + 1, 2, 0, NT, 1, 2)
+            plane_q(n, 2)
+            turn_k(n + 1, 0, turning(n))
+            turn_x(n + 2, 0, x_bank("turn0"))
+            if n == L - 3:
+                pair_max(0)
+            turn_x(n + 2, 1, x_bank(turning(n + 1)))
+            if n + 2 in SHARED:
+                share_x(n + 2)
+            plane_q(n, 3)
+            empty_k(n + 1, 0)
+        n = L - 1
+        quant_k(n - 1)
+        pair_finish(0, nc.vector)
+        quant_q(n - 2)
+        quant_x(n)
+        lace(L)
         store_later_rows(0)
         store_first_left(0)
-        empty_q(L - 1, 1)
-        pair_exp(1)
-        empty_q(L - 1, 2)
-        empty_q(L - 1, 3)
-        empty_k(L - 1, 0)
-        for t in range(4):
-            project(L, t, range(G), 0, 2)
-        turn_k(L - 1, 2)
-        empty_x(L, 2, 2, 1)
-        mask_scores(L - 2)
-        turn_k(L, 0)
-        turn_k(L, 2, 1, "sc", 1)
-        pair_sum(1)
-        quant_x(L, 2, 1, 1)
-        pair_recip(1)
-        pair_finish(1)
-        store_later_rows(1)
         store_first_right(0)
+        scores(n - 2)
+        project(n, 0, [0])
+        project(n, 1, [0])
+        project(n, 0, [1])
+        project(n, 1, [1])
+        turn_x(L, 2, x_bank(turning(n + 1)))
+        empty_x(L, 0, 0, 2)
+        empty_scores(n - 2)
+        park(n - 2)
+        clear_words(parked(0), parked(4), 3)
+        fetch(n - 2)
+        turn_x(L, 3, x_bank(turning(n - 1)), [0])
+        empty_q(n, 0)
+        empty_q(n, 1)
+        empty_x(L, 1, 0, 2)
+        project(n, 2)
+        project(n, 3)
+        turn_k(n, 2, "turn0")
+        turn_k(L, 0, turning(n))
+        turn_k(L, 2, "scores", 1)
+        empty_x(L, 2, 2, 1)
+        pair_max(1)
+        empty_x(L, 3, 3, 1, 0, 1)
+        quant_x(L, 0, 2, 1)
+        pair_shift(1, nc.vector)
+        quant_x(L, 2, 1, 1)
+        quant_x(L, 3, 1, 1)
+        quant_q(L - 2)
+        empty_q(n, 2)
+        empty_q(n, 3)
+        empty_k(n, 2)
+        weave_q(n)
+        pair_exp(1)
+        quant_k(L - 1)
+        pair_max(2)
+        empty_k(L, 0)
+        empty_k(L, 2, 1)
+        for t in range(4):
+            project(L, t, range(G), 0, 2, f"sum{1 + t // 2}")
+        for t in range(4):
+            project(L, t, range(G), 2, 1, turning(n + 1))
+        scores(L - 2, 0, NT, "sum0")
+        for t in range(4):
+            project(L, t, range(G), 3, 1, turning(n - 1))
+        quant_q(L - 1)
+        pair_shift(2, nc.vector)
+        pair_exp(2)
+        pair_sum(1)
+        quant_k(L)
+        pair_recip(1)
+        empty_q_v(L, 2)
+        pair_finish(1, nc.vector)
+        store_later_rows(1)
         store_first_left(1)
         clear_words(parked(4), L * S * S, 2)
         store_first_right(1)
-        empty_x(L, 3, 3, 1)
-        row_max(L - 2)
-        for t in range(4):
-            project(L, t, range(G), 2, 1)
-        weave_q(L - 1)
-        empty_k(L - 1, 2)
-        empty_k(L, 0)
-        empty_k(L, 2, 1)
-        pair_max(2)
-        quant_x(L, 3, 1, 1)
-        pair_shift(2, nc.vector)
-        pair_exp(2)
-        for t in range(4):
-            project(L, t, range(G), 3, 1, "tp", 4)
-        quant_q(L - 1)
         pair_sum(2)
-        quant_k(L - 1)
-        pair_recip(2)
-        pair_finish(2)
-        store_boxes(2, nc.gpsimd)
-        empty_q_v(L, 2)
-        scores(L - 1)
         for t in range(4):
             empty_q(L, t, 0, 2)
         weave_q(L, 0, 2)
-        exps(L - 2)
+        scores(L - 1, 0, NT, "turn0")
+        mask_scores(L - 2)
+        pair_recip(2)
         empty_q_v(L, 3)
-        quant_k(L)
+        pair_finish(2, nc.vector)
+        store_boxes(2, nc.gpsimd)
+        row_max(L - 2)
+        exps(L - 2)
         quant_q(L, 2, 2)
-        quant_q(L, 0, 2)
-        scores(L, 2, 2, "tp", 4)
-        scores(L, 0, 2, "tp", 4)
-        recip(L - 2)
-        finish(L - 2)
-        store_inner(L - 2)
+        scores(L, 2, 2, turning(n))
         mask_scores(L - 1)
-        mask_scores(L, 2, 2)
+        quant_q(L, 0, 2)
+        scores(L, 0, 2, "scores")
+        recip(L - 2)
         row_max(L - 1)
-        mask_scores(L, 0, 2)
+        finish(L - 2)
         exps(L - 1)
+        mask_scores(L, 2, 2)
+        store_inner(L - 2)
+        mask_scores(L, 0, 2)
         row_max(L, 2, 2)
+        recip(L - 1)
         row_max(L, 0, 2)
         exps(L, 2, 2)
         exps(L, 0, 2)
-        recip(L - 1)
-        recip(L, 2, 2)
         finish_v(L - 1)
+        recip(L, 2, 2)
         store_inner(L - 1)
         recip(L, 0, 2)
         finish(L, 2, 2)

@@ -40,7 +40,8 @@ BOX = 3 * MARGIN
 PAIRS = (PARKED + 1) // 2
 ROOM = S * (STRIP + 1)
 STENCIL = Q + STRIP + 2 * MARGIN
-COUNTS = [(0, 2, 2, 1, 4), (2, 2, 3, 1, 2), (1, 2, 3, 1, 0), (1, 2, 3, 1, 0), (1, 2, 3, 1, 0), (1, 2, 3, 1, 0)]
+ORDER = (1, 0)
+COUNTS = [(0, 3, 2, 1, 4), (2, 2, 3, 2, 2), (1, 2, 3, 1, 0), (1, 2, 3, 1, 0), (1, 2, 2, 1, 0), (1, 2, 2, 1, 0)]
 SHARED = (1, 3, 4, 5, 6, 7)
 WIDE = 4
 
@@ -70,7 +71,7 @@ def tile_localattention_pa_t_w4_kernel(tc, x_bytes, x_scale, Wq_words, Wq_scales
         bias = keep.tile([P, 4], BF16, name="bias")
         stencil = keep.tile([P, STENCIL], F32, name="stencil")
         mask = keep.tile([P, NT, STRIP], F32, name="mask")
-        zeros = keep.tile([P, S], F32, name="zeros")
+        zeros = keep.tile([P, 2 * S], F32, name="zeros")
         kc = keep.tile([P, B * S + Q], U32, name="kc", align_bytes=64)
         ksc = keep.tile([P, B * S + Q], U8, name="ksc", align_bytes=64)
         qc = [keep.tile([P, NT * 3 * Q], U32, name=f"qc{j}", align_bytes=64) for j in range(2)]
@@ -104,7 +105,7 @@ def tile_localattention_pa_t_w4_kernel(tc, x_bytes, x_scale, Wq_words, Wq_scales
             nc.sync.dma_start(out=k_seam[Q : P - SHIFT, :], in_=kflat[seam + Q : B * S, :])
             nc.sync.dma_start(out=k_seam[P - SHIFT : P, :], in_=kflat[0:SHIFT, :])
 
-        nc.vector.memset(zeros[:], 0.0)
+        nc.vector.memset(zeros[:, 0:256], 0.0)
         nc.vector.memset(ident[:], 0.0)
         nc.vector.memset(ws_raw[:].rearrange("p g n -> p (g n)").bitcast(I32), 0)
         nc.sync.dma_start(out=x_first[0][:], in_=xv[0][:, 0, :])
@@ -131,6 +132,7 @@ def tile_localattention_pa_t_w4_kernel(tc, x_bytes, x_scale, Wq_words, Wq_scales
         load_k(L)
 
         make_identity(nc, ident[:], nomemset=True)
+        nc.vector.memset(zeros[:, 256:], 0.0)
         nc.vector.memset(stencil[:], MASKED)
         nc.vector.memset(stencil[:, Q + MARGIN - HALF : Q + MARGIN + HALF + 1], 0.0)
         for j in range(2):
@@ -147,7 +149,7 @@ def tile_localattention_pa_t_w4_kernel(tc, x_bytes, x_scale, Wq_words, Wq_scales
             nc.sync.dma_start(out=rows, in_=zeros[:, 0:n].unsqueeze(1).to_broadcast([P, r, n]))
 
         def clear(b):
-            clear_words(b * S * S, (b + 1) * S * S, NT)
+            clear_words(b * S * S, (b + 1) * S * S, 2)
 
         def parked(b):
             return (L - 1) * S * S + b * ROOM
@@ -197,7 +199,7 @@ def tile_localattention_pa_t_w4_kernel(tc, x_bytes, x_scale, Wq_words, Wq_scales
             )
 
         def permute_scales():
-            nc.gpsimd.tensor_copy(
+            nc.vector.tensor_copy(
                 out=ws_perm[:].rearrange("p g (t m) -> p g t m", t=4),
                 in_=ws_raw[:].rearrange("p g (m t) -> p g t m", t=4),
             )
@@ -264,12 +266,12 @@ def tile_localattention_pa_t_w4_kernel(tc, x_bytes, x_scale, Wq_words, Wq_scales
             dst = rows_x(0, NT)[:, g, P * i : P * (i + 1)].rearrange("p n h e -> p n (h e)")
             nc.gpsimd.tensor_copy(out=dst, in_=first_planes[:, g].rearrange("p t n -> p n t"))
 
-        def quant_x(b, i0=0, n=NT, cuts=G, parts=range(G)):
+        def quant_x(b, i0=0, n=NT, cuts=G, parts=ORDER):
             if b not in xc:
                 xc[b] = work.tile([P, G * S], U32, name="xc", align_bytes=64)
                 xsc[b] = work.tile([P, G * S], U8, name="xsc", align_bytes=64)
             w = G * P * n // cuts
-            for g in parts[:cuts]:
+            for g in parts if cuts > 1 else [0]:
                 cols = slice(G * P * i0 + w * g, G * P * i0 + w * (g + 1))
                 nc.vector.quantize_mx(
                     out=xc[b][:, cols].bitcast(FP8X4), scales=xsc[b][:, cols], in_=rows[:, 4 * cols.start : 4 * cols.stop]
@@ -296,7 +298,7 @@ def tile_localattention_pa_t_w4_kernel(tc, x_bytes, x_scale, Wq_words, Wq_scales
             cols = slice(S * b + Q, S * (b + 1) + Q)
             nc.vector.quantize_mx(out=kc[:, cols].bitcast(FP8X4), scales=ksc[:, cols], in_=rows_k(b))
 
-        def project(b, t, passes=range(G), i0=0, n=NT, name=None):
+        def project(b, t, passes=ORDER, i0=0, n=NT, name=None):
             per = NT // n
             if (b, i0, t // per) not in acc:
                 acc[b, i0, t // per] = bank(name or f"sum{(4 * b + t) % 3}", [P, per, n * P])
@@ -308,8 +310,8 @@ def tile_localattention_pa_t_w4_kernel(tc, x_bytes, x_scale, Wq_words, Wq_scales
                     lhsT_scale=ws_perm[:, g, P * t : P * (t + 1)],
                     rhs=xc[b][:, cols].bitcast(FP8X4),
                     rhs_scale=xsc[b][:, cols],
-                    start=(g == 0),
-                    stop=(g == G - 1),
+                    start=(g == ORDER[0]),
+                    stop=(g == ORDER[-1]),
                 )
 
         def plane_q(b, t):
@@ -485,8 +487,8 @@ def tile_localattention_pa_t_w4_kernel(tc, x_bytes, x_scale, Wq_words, Wq_scales
             for i in range(n):
                 nc.scalar.activation(out=strip[:, i, :], in_=sm[b, i0][:, i, :], func=ACT.Copy, scale=rs[b, i0][:, i : i + 1])
 
-        def finish_v(b, i0=0, n=NT, lo=0):
-            nc.vector.tensor_tensor(
+        def finish_v(b, i0=0, n=NT, lo=0, eng=nc.vector):
+            eng.tensor_tensor(
                 out=strips[:, b - PARKED, i0 + lo : i0 + n, LIVE],
                 in0=sm[b, i0][:, lo:n],
                 in1=rs[b, i0][:, lo:n].unsqueeze(2).to_broadcast([P, n - lo, WIDTH]),
@@ -508,17 +510,16 @@ def tile_localattention_pa_t_w4_kernel(tc, x_bytes, x_scale, Wq_words, Wq_scales
         widen(on_s, 0, 3)
         for g in range(G):
             permute_codes(g)
-        permute_scales()
+        widen(on_g, 1, 0)
         turn_x(0, 0, x_bank("sum0"))
         turn_x(0, 1, x_bank("sum1"))
         turn_x(0, 2, x_bank("sum2"))
         turn_x(0, 3, x_bank("scores"))
         empty_x(0, 0)
-        for g in range(G):
+        for g in ORDER:
             plane_x(0, 1, g, first_planes[:, g])
             lace_first(1, g)
         empty_x(0, 2)
-        widen(on_s, 1, 0)
         widen(on_s, 1, 3)
         widen(on_s, 1, 1)
         turn_x(1, 0, x_bank("turn0"))
@@ -526,8 +527,8 @@ def tile_localattention_pa_t_w4_kernel(tc, x_bytes, x_scale, Wq_words, Wq_scales
         turn_x(1, 1, x_bank(turning(0)))
         turn_k(0, 0, turning(1))
         turn_k(0, 2, turning(-1))
-        empty_x(0, 3, 0, NT, 0, 1)
         empty_x(0, 3, 0, NT, 1, 2)
+        empty_x(0, 3, 0, NT, 0, 1)
         share_x(1)
         widen(on_s, 1, 2)
         empty_k(0, 0)
@@ -542,23 +543,23 @@ def tile_localattention_pa_t_w4_kernel(tc, x_bytes, x_scale, Wq_words, Wq_scales
             if n == L - 2:
                 pair_shift(0, nc.vector)
                 pair_exp(0)
-            if n + 1 in SHARED:
-                step(quant_q, n - 2)
-            quant_x(n)
-            if n + 1 not in SHARED:
-                step(quant_q, n - 2)
+            step(quant_q, n - 2)
+            if n == 0:
+                permute_scales()
+            quant_x(n, 0, NT, G, [1])
             if n == 1:
                 quant_k(0)
+            quant_x(n, 0, NT, G, [0])
             widen_next(on_s, counts[0])
             step(scores, n - 2)
-            project(n, 0, [0])
-            project(n, 1, [0])
             project(n, 0, [1])
-            empty_x(n + 1, 0, 0, NT, 0, 1)
+            project(n, 1, [1])
+            project(n, 0, [0])
             if n + 1 not in SHARED:
                 empty_x(n + 1, 3, 0, NT, 1, 2)
-            turn_x(n + 1, 2, x_bank(turning(n + 1)))
             empty_x(n + 1, 0, 0, NT, 1, 2)
+            turn_x(n + 1, 2, x_bank(turning(n + 1)))
+            empty_x(n + 1, 0, 0, NT, 0, 1)
             step(empty_scores, n - 2)
             if n == L - 2:
                 pair_sum(0)
@@ -585,7 +586,7 @@ def tile_localattention_pa_t_w4_kernel(tc, x_bytes, x_scale, Wq_words, Wq_scales
             empty_x(n + 1, 1)
             if n == L - 2:
                 pair_recip(0)
-            project(n, 1, [1])
+            project(n, 1, [0])
             project(n, 2)
             project(n, 3)
             if n == 0:
@@ -594,9 +595,8 @@ def tile_localattention_pa_t_w4_kernel(tc, x_bytes, x_scale, Wq_words, Wq_scales
                 empty_k(n, 2)
             plane_q(n, 1)
             widen_next(on_s, counts[3])
-            empty_x(n + 1, 2, 0, NT, 0, 1)
+            empty_x(n + 1, 2)
             empty_x(n + 1, 3, 0, NT, 0, 1)
-            empty_x(n + 1, 2, 0, NT, 1, 2)
             plane_q(n, 2)
             turn_k(n + 1, 0, turning(n))
             turn_x(n + 2, 0, x_bank("turn0"))
@@ -615,17 +615,18 @@ def tile_localattention_pa_t_w4_kernel(tc, x_bytes, x_scale, Wq_words, Wq_scales
         lace(L)
         store_later_rows(0)
         store_first_left(0)
-        store_first_right(0)
         scores(n - 2)
-        project(n, 0, [0])
-        project(n, 1, [0])
         project(n, 0, [1])
         project(n, 1, [1])
+        project(n, 0, [0])
+        project(n, 1, [0])
         turn_x(L, 2, x_bank(turning(n + 1)))
-        empty_x(L, 0, 0, 2)
+        empty_x(L, 0, 0, 2, 1, 2)
+        empty_x(L, 0, 0, 2, 0, 1)
         empty_scores(n - 2)
         park(n - 2)
-        clear_words(parked(0), parked(4), 3)
+        store_first_right(0)
+        clear_words(parked(0), parked(4), 2)
         fetch(n - 2)
         turn_x(L, 3, x_bank(turning(n - 1)), [0])
         empty_q(n, 0)
@@ -643,58 +644,58 @@ def tile_localattention_pa_t_w4_kernel(tc, x_bytes, x_scale, Wq_words, Wq_scales
         pair_shift(1, nc.vector)
         quant_x(L, 2, 1, 1)
         quant_x(L, 3, 1, 1)
-        quant_q(L - 2)
         empty_q(n, 2)
         empty_q(n, 3)
+        pair_exp(1)
         empty_k(n, 2)
         weave_q(n)
-        pair_exp(1)
+        quant_q(L - 2)
+        pair_sum(1)
         quant_k(L - 1)
+        pair_recip(1)
         pair_max(2)
         empty_k(L, 0)
         empty_k(L, 2, 1)
         for t in range(4):
-            project(L, t, range(G), 0, 2, f"sum{1 + t // 2}")
+            project(L, t, ORDER, 0, 2, f"sum{1 + t // 2}")
         for t in range(4):
-            project(L, t, range(G), 2, 1, turning(n + 1))
+            project(L, t, ORDER, 2, 1, turning(n + 1))
         scores(L - 2, 0, NT, "sum0")
         for t in range(4):
-            project(L, t, range(G), 3, 1, turning(n - 1))
-        quant_q(L - 1)
-        pair_shift(2, nc.vector)
-        pair_exp(2)
-        pair_sum(1)
-        quant_k(L)
-        pair_recip(1)
-        empty_q_v(L, 2)
+            project(L, t, ORDER, 3, 1, turning(n - 1))
         pair_finish(1, nc.vector)
         store_later_rows(1)
         store_first_left(1)
-        clear_words(parked(4), L * S * S, 2)
-        store_first_right(1)
+        clear_words(parked(4), L * S * S, 1)
+        pair_shift(2, nc.vector)
+        pair_exp(2)
+        quant_q(L - 1)
+        quant_k(L)
         pair_sum(2)
+        empty_q_v(L, 2)
+        pair_recip(2)
         for t in range(4):
             empty_q(L, t, 0, 2)
         weave_q(L, 0, 2)
         scores(L - 1, 0, NT, "turn0")
+        pair_finish(2)
+        store_first_right(1)
+        store_boxes(2, nc.sync)
         mask_scores(L - 2)
-        pair_recip(2)
         empty_q_v(L, 3)
-        pair_finish(2, nc.vector)
-        store_boxes(2, nc.gpsimd)
         row_max(L - 2)
         exps(L - 2)
+        mask_scores(L - 1)
         quant_q(L, 2, 2)
         scores(L, 2, 2, turning(n))
-        mask_scores(L - 1)
         quant_q(L, 0, 2)
         scores(L, 0, 2, "scores")
-        recip(L - 2)
         row_max(L - 1)
-        finish(L - 2)
+        recip(L - 2)
         exps(L - 1)
-        mask_scores(L, 2, 2)
+        finish_v(L - 2, 0, NT, 0, nc.gpsimd)
         store_inner(L - 2)
+        mask_scores(L, 2, 2)
         mask_scores(L, 0, 2)
         row_max(L, 2, 2)
         recip(L - 1)

@@ -39,9 +39,10 @@ PITCH = 16
 BOX = 3 * MARGIN
 PAIRS = (PARKED + 1) // 2
 ROOM = S * (STRIP + 1)
+FREED = 2 * ROOM // 2048 * 2048
 STENCIL = Q + STRIP + 2 * MARGIN
 ORDER = (1, 0)
-COUNTS = [(0, 3, 2, 1, 4), (2, 2, 3, 2, 2), (1, 2, 3, 1, 0), (1, 2, 3, 1, 0), (1, 2, 2, 1, 0), (1, 2, 2, 1, 0)]
+COUNTS = [(0, 2, 2, 2, 4), (1, 2, 3, 2, 2), (1, 2, 3, 1, 0), (1, 2, 3, 1, 0), (1, 2, 3, 1, 0), (1, 2, 2, 1, 0)]
 SHARED = (1, 3, 4, 5, 6, 7)
 WIDE = 4
 
@@ -71,7 +72,7 @@ def tile_localattention_pa_t_w4_kernel(tc, x_bytes, x_scale, Wq_words, Wq_scales
         bias = keep.tile([P, 4], BF16, name="bias")
         stencil = keep.tile([P, STENCIL], F32, name="stencil")
         mask = keep.tile([P, NT, STRIP], F32, name="mask")
-        zeros = keep.tile([P, 2 * S], F32, name="zeros")
+        zeros = keep.tile([P, S], F32, name="zeros")
         kc = keep.tile([P, B * S + Q], U32, name="kc", align_bytes=64)
         ksc = keep.tile([P, B * S + Q], U8, name="ksc", align_bytes=64)
         qc = [keep.tile([P, NT * 3 * Q], U32, name=f"qc{j}", align_bytes=64) for j in range(2)]
@@ -80,9 +81,9 @@ def tile_localattention_pa_t_w4_kernel(tc, x_bytes, x_scale, Wq_words, Wq_scales
         diag = [keep.tile([P, ROWS, PITCH], F32, name=f"diag{j}", align_bytes=64) for j in range(PAIRS)]
         boxes = [keep.tile([P, ROWS * BOX + ROWS], F32, name=f"boxes{j}", align_bytes=64) for j in range(PAIRS)]
 
-        x_first = [keep.tile([P, D], U8, name=f"x_codes_first{i}", align_bytes=64) for i in range(2)]
+        x_first = [keep.tile([P, D], U8, name=f"x_codes_first{i}", align_bytes=64) for i in range(NT)]
         x_second = keep.tile([P, 2, D], U8, name="x_codes_second", align_bytes=64)
-        x_tiles = [keep.tile([P, NT, D], U8, name=f"x_codes{b}", align_bytes=64) for b in range(B)]
+        x_tiles = [keep.tile([P, NT, D], U8, name=f"x_codes{b}", align_bytes=64) if b else None for b in range(B)]
         k_tiles = [keep.tile([P, NT, E], BF16, name=f"k_rows{b}", align_bytes=64) for b in range(B)]
         k_seam = keep.tile([P, E], BF16, name="k_seam", align_bytes=64)
 
@@ -105,15 +106,15 @@ def tile_localattention_pa_t_w4_kernel(tc, x_bytes, x_scale, Wq_words, Wq_scales
             nc.sync.dma_start(out=k_seam[Q : P - SHIFT, :], in_=kflat[seam + Q : B * S, :])
             nc.sync.dma_start(out=k_seam[P - SHIFT : P, :], in_=kflat[0:SHIFT, :])
 
-        nc.vector.memset(zeros[:, 0:256], 0.0)
         nc.vector.memset(ident[:], 0.0)
         nc.vector.memset(ws_raw[:].rearrange("p g n -> p (g n)").bitcast(I32), 0)
+        nc.vector.memset(zeros[:], 0.0)
         nc.sync.dma_start(out=x_first[0][:], in_=xv[0][:, 0, :])
-        nc.sync.dma_start(out=x_first[1][:], in_=xv[0][:, 1, :])
-        nc.sync.dma_start(out=w_raw[0][:].bitcast(I32), in_=Wq_words[0].bitcast(I32))
-        nc.sync.dma_start(out=x_tiles[0][:, 2:NT, :], in_=xv[0][:, 2:NT, :])
-        nc.sync.dma_start(out=w_raw[1][:].bitcast(I32), in_=Wq_words[1].bitcast(I32))
         nc.sync.dma_start(out=scale_p[:], in_=x_scale.rearrange("a b (g p c) -> p (a b g) c", p=P, c=4))
+        nc.sync.dma_start(out=x_first[1][:], in_=xv[0][:, 1, :])
+        for g in range(G):
+            nc.sync.dma_start(out=w_raw[g][:].bitcast(I32), in_=Wq_words[g].bitcast(I32))
+            nc.sync.dma_start(out=x_first[2 + g][:], in_=xv[0][:, 2 + g, :])
         nc.sync.dma_start(out=x_second[:], in_=xv[1][:, 0:2, :])
         for q in range(4):
             nc.sync.dma_start(
@@ -132,14 +133,10 @@ def tile_localattention_pa_t_w4_kernel(tc, x_bytes, x_scale, Wq_words, Wq_scales
         load_k(L)
 
         make_identity(nc, ident[:], nomemset=True)
-        nc.vector.memset(zeros[:, 256:], 0.0)
         nc.vector.memset(stencil[:], MASKED)
+        for padded in qc + qsc:
+            nc.vector.memset(padded[:].bitcast(I32).rearrange("p (i u n) -> p i u n", i=NT, u=3)[:, :, 1, :], 0)
         nc.vector.memset(stencil[:, Q + MARGIN - HALF : Q + MARGIN + HALF + 1], 0.0)
-        for j in range(2):
-            nc.vector.memset(qc[j][:].bitcast(I32).rearrange("p (i u n) -> p i u n", i=NT, u=3)[:, :, 1, :], 0)
-            nc.vector.memset(qsc[j][:].bitcast(I32).rearrange("p (i u n) -> p i u n", i=NT, u=3)[:, :, 1, :], 0)
-        for margin in (slice(0, LIVE.start), slice(LIVE.stop, STRIP)):
-            nc.vector.memset(strips[:].rearrange("p j i c -> p (j i) c")[:, :, margin], 0.0)
         for j in range(PAIRS):
             nc.scalar.activation(out=boxes[j][:], in_=zeros[:, 0 : ROWS * (BOX + 1)], func=ACT.Copy)
 
@@ -149,7 +146,7 @@ def tile_localattention_pa_t_w4_kernel(tc, x_bytes, x_scale, Wq_words, Wq_scales
             nc.sync.dma_start(out=rows, in_=zeros[:, 0:n].unsqueeze(1).to_broadcast([P, r, n]))
 
         def clear(b):
-            clear_words(b * S * S, (b + 1) * S * S, 2)
+            clear_words(b * S * S, (b + 1) * S * S, NT)
 
         def parked(b):
             return (L - 1) * S * S + b * ROOM
@@ -167,6 +164,10 @@ def tile_localattention_pa_t_w4_kernel(tc, x_bytes, x_scale, Wq_words, Wq_scales
                 nc.sync.dma_start(out=mask[Q * s : Q * (s + 1), inner, :], in_=rows.unsqueeze(1).to_broadcast([Q, NT - 1, STRIP]))
                 nc.sync.dma_start(out=mask[Q * s : Q * (s + 1), outer[0], outer[1]], in_=rows[:, outer[1]])
 
+        def clear_margins():
+            for margin in (slice(0, LIVE.start), slice(LIVE.stop, STRIP)):
+                nc.vector.memset(strips[:].rearrange("p j i c -> p (j i) c")[:, :, margin], 0.0)
+
         def mask_edges():
             nc.vector.memset(mask[0:Q, 0, 0:MARGIN], MASKED)
             nc.vector.memset(mask[Q:P, NT - 1, STRIP - MARGIN : STRIP], MASKED)
@@ -181,12 +182,10 @@ def tile_localattention_pa_t_w4_kernel(tc, x_bytes, x_scale, Wq_words, Wq_scales
                 cells = view.rearrange("b (r j) -> r b j", r=Q)[:, :, 0:MARGIN]
                 nc.sync.dma_start(out=cells, in_=stencil[Q * s : Q * (s + 1), 0 : PARKED * MARGIN].rearrange("p (b j) -> p b j", b=PARKED))
 
+        clear_margins()
         mask_edges()
         park_edges()
         lay_stencil()
-        clear(0)
-        load_mask()
-        clear(1)
 
         xt, xc, xsc, ktp, acc, qp = {}, {}, {}, {}, {}, {}
         sc, sm, nm, ss, rs = {}, {}, {}, {}, {}
@@ -208,7 +207,7 @@ def tile_localattention_pa_t_w4_kernel(tc, x_bytes, x_scale, Wq_words, Wq_scales
             return wides[b % WIDE][:, D * i : D * (i + n)]
 
         def widen(copy, b, i):
-            codes = x_tiles[b][:, i, :] if i > 1 else x_second[:, i, :] if b else x_first[i][:]
+            codes = x_first[i][:] if b == 0 else x_tiles[b][:, i, :] if i > 1 else x_second[:, i, :]
             copy(out=wide(b, i), in_=codes.bitcast(FP8))
 
         halves = [(b, u) for b in range(2, B) for u in [2 * NT - 1] + list(range(2 * NT - 1))]
@@ -504,6 +503,12 @@ def tile_localattention_pa_t_w4_kernel(tc, x_bytes, x_scale, Wq_words, Wq_scales
 
         on_s, on_v, on_g = nc.scalar.copy, nc.vector.tensor_copy, nc.gpsimd.tensor_copy
 
+        to_clear = [b for b in range(B) if b != L - 1]
+
+        def clear_next():
+            clear(to_clear[0])
+            to_clear.remove(to_clear[0])
+
         widen(on_v, 0, 0)
         widen(on_s, 0, 1)
         widen(on_s, 0, 2)
@@ -540,9 +545,6 @@ def tile_localattention_pa_t_w4_kernel(tc, x_bytes, x_scale, Wq_words, Wq_scales
                 quant_k(n - 1)
             if n == 2:
                 quant_seam()
-            if n == L - 2:
-                pair_shift(0, nc.vector)
-                pair_exp(0)
             step(quant_q, n - 2)
             if n == 0:
                 permute_scales()
@@ -561,16 +563,20 @@ def tile_localattention_pa_t_w4_kernel(tc, x_bytes, x_scale, Wq_words, Wq_scales
             turn_x(n + 1, 2, x_bank(turning(n + 1)))
             empty_x(n + 1, 0, 0, NT, 0, 1)
             step(empty_scores, n - 2)
-            if n == L - 2:
-                pair_sum(0)
+            if n == 4:
+                fetch(0)
+                fetch(1)
+            if n == 5:
+                load_mask()
+                clear_words(parked(0), parked(0) + FREED, 2)
             if n >= 2:
                 park(n - 2)
-                clear(n)
-            if n % 2 and n > 2:
-                fetch(n - 3)
-                fetch(n - 2)
-            if n == 3:
-                clear(L)
+                clear_next()
+                if n < 5:
+                    clear_next()
+            if n == 5:
+                fetch(2)
+                fetch(3)
             mixed = x_bank(turning(n - 1))
             turn_x(n + 1, 3, mixed, [0])
             turn_x(n + 2, 3, mixed, [1])
@@ -584,8 +590,6 @@ def tile_localattention_pa_t_w4_kernel(tc, x_bytes, x_scale, Wq_words, Wq_scales
             else:
                 turn_k(n, 2, "turn0")
             empty_x(n + 1, 1)
-            if n == L - 2:
-                pair_recip(0)
             project(n, 1, [0])
             project(n, 2)
             project(n, 3)
@@ -600,7 +604,7 @@ def tile_localattention_pa_t_w4_kernel(tc, x_bytes, x_scale, Wq_words, Wq_scales
             plane_q(n, 2)
             turn_k(n + 1, 0, turning(n))
             turn_x(n + 2, 0, x_bank("turn0"))
-            if n == L - 3:
+            if n == L - 2:
                 pair_max(0)
             turn_x(n + 2, 1, x_bank(turning(n + 1)))
             if n + 2 in SHARED:
@@ -609,12 +613,12 @@ def tile_localattention_pa_t_w4_kernel(tc, x_bytes, x_scale, Wq_words, Wq_scales
             empty_k(n + 1, 0)
         n = L - 1
         quant_k(n - 1)
-        pair_finish(0, nc.vector)
+        pair_shift(0, nc.vector)
+        quant_x(n, 0, NT, G, [0])
         quant_q(n - 2)
-        quant_x(n)
+        quant_x(n, 0, NT, G, [1])
         lace(L)
-        store_later_rows(0)
-        store_first_left(0)
+        pair_exp(0)
         scores(n - 2)
         project(n, 0, [1])
         project(n, 1, [1])
@@ -625,13 +629,13 @@ def tile_localattention_pa_t_w4_kernel(tc, x_bytes, x_scale, Wq_words, Wq_scales
         empty_x(L, 0, 0, 2, 0, 1)
         empty_scores(n - 2)
         park(n - 2)
-        store_first_right(0)
-        clear_words(parked(0), parked(4), 2)
         fetch(n - 2)
+        pair_sum(0)
         turn_x(L, 3, x_bank(turning(n - 1)), [0])
         empty_q(n, 0)
         empty_q(n, 1)
         empty_x(L, 1, 0, 2)
+        pair_recip(0)
         project(n, 2)
         project(n, 3)
         turn_k(n, 2, "turn0")
@@ -642,6 +646,9 @@ def tile_localattention_pa_t_w4_kernel(tc, x_bytes, x_scale, Wq_words, Wq_scales
         empty_x(L, 3, 3, 1, 0, 1)
         quant_x(L, 0, 2, 1)
         pair_shift(1, nc.vector)
+        pair_finish(0, nc.vector)
+        store_later_rows(0)
+        store_first_left(0)
         quant_x(L, 2, 1, 1)
         quant_x(L, 3, 1, 1)
         empty_q(n, 2)
@@ -665,8 +672,9 @@ def tile_localattention_pa_t_w4_kernel(tc, x_bytes, x_scale, Wq_words, Wq_scales
             project(L, t, ORDER, 3, 1, turning(n - 1))
         pair_finish(1, nc.vector)
         store_later_rows(1)
+        store_first_right(0)
+        clear_words(parked(0) + FREED, L * S * S, 4)
         store_first_left(1)
-        clear_words(parked(4), L * S * S, 1)
         pair_shift(2, nc.vector)
         pair_exp(2)
         quant_q(L - 1)
@@ -685,9 +693,9 @@ def tile_localattention_pa_t_w4_kernel(tc, x_bytes, x_scale, Wq_words, Wq_scales
         empty_q_v(L, 3)
         row_max(L - 2)
         exps(L - 2)
-        mask_scores(L - 1)
         quant_q(L, 2, 2)
         scores(L, 2, 2, turning(n))
+        mask_scores(L - 1)
         quant_q(L, 0, 2)
         scores(L, 0, 2, "scores")
         row_max(L - 1)
@@ -698,9 +706,9 @@ def tile_localattention_pa_t_w4_kernel(tc, x_bytes, x_scale, Wq_words, Wq_scales
         mask_scores(L, 2, 2)
         mask_scores(L, 0, 2)
         row_max(L, 2, 2)
-        recip(L - 1)
         row_max(L, 0, 2)
         exps(L, 2, 2)
+        recip(L - 1)
         exps(L, 0, 2)
         finish_v(L - 1)
         recip(L, 2, 2)

@@ -43,7 +43,7 @@ FREED = 2 * ROOM // 2048 * 2048
 STENCIL = Q + STRIP + 2 * MARGIN
 ORDER = (1, 0)
 COUNTS = [(0, 2, 2, 2, 4), (1, 2, 3, 2, 2), (1, 2, 3, 1, 0), (1, 2, 3, 1, 0), (1, 2, 3, 1, 0), (1, 2, 2, 1, 0)]
-SHARED = (1, 3, 4, 5, 6, 7)
+SHARES = (0, 128, 0, 128, 128, 128, 128, 128)
 WIDE = 4
 
 
@@ -60,7 +60,7 @@ def tile_localattention_pa_t_w4_kernel(tc, x_bytes, x_scale, Wq_words, Wq_scales
         wides = [keep.tile([P, NT * D], BF16, name=f"wide{j}", align_bytes=64) for j in range(WIDE)]
         rows = keep.tile([P, 4 * S * (G + 1)], BF16, name="rows", align_bytes=64)
         planes = [keep.tile([P, 4, P + S], BF16, name=f"planes{j}", align_bytes=64) for j in range(2)]
-        first_planes = keep.tile([P, G, 4, P], BF16, name="first_planes", align_bytes=64)
+        first_planes = [keep.tile([P, 4, P], BF16, name=f"first_planes{g}", align_bytes=64) for g in range(G)]
         q_tail = [keep.tile([P, S * 4], BF16, name=f"q_tail{j}", align_bytes=64) for j in range(2)]
         kt = [keep.tile([P, S * 4], BF16, name=f"kt{j}", align_bytes=64) for j in range(2)]
         k_last = keep.tile([P, S * 4], BF16, name="k_last", align_bytes=64)
@@ -248,13 +248,23 @@ def tile_localattention_pa_t_w4_kernel(tc, x_bytes, x_scale, Wq_words, Wq_scales
             scales = scale_p[:, g0:g1].rearrange("p g (h e) -> p g h e", e=2).unsqueeze(2).to_broadcast([P, g1 - g0, P, 2, 2])
             nc.vector.tensor_tensor(out=dst, in0=values, in1=scales, op=ALU.mult)
 
-        def plane_x(b, i, g, dst):
+        def empty_rest(b):
+            n = P - SHARES[b]
+            if n == 0:
+                return
+            at = 4 * (G * S - P)
+            dst = rows[:, at : at + 4 * n].rearrange("p (n h e) -> p n h e", h=2, e=2)
+            values = xt[b, NT - 1, G - 1][:].bitcast(BF16).rearrange("p h g (r e) -> p g r h e", e=2)[:, G - 1, 0:n]
+            scales = scale_p[:, G - 1].rearrange("p (h e) -> p h e", e=2).unsqueeze(1).to_broadcast([P, n, 2, 2])
+            nc.vector.tensor_tensor(out=dst, in0=values, in1=scales, op=ALU.mult)
+
+        def plane_x(b, i, g, dst, lo=0):
             for t in range(4):
-                values = xt[b, i, g][:, t // 2, g, :].bitcast(BF16)[:, t % 2 :: 2]
+                values = xt[b, i, g][:, t // 2, g, lo:].bitcast(BF16)[:, t % 2 :: 2]
                 nc.scalar.activation(out=dst[:, t, :], in_=values, func=ACT.Copy, scale=scale_p[:, g, t : t + 1])
 
         def share_x(b):
-            plane_x(b, NT - 1, G - 1, planes[b % 2][:, :, 0:P])
+            plane_x(b, NT - 1, G - 1, planes[b % 2][:, :, P - SHARES[b] : P], P - SHARES[b])
 
         def lace(b, lo=0, hi=P + S):
             at = 4 * (G * S - P)
@@ -263,7 +273,7 @@ def tile_localattention_pa_t_w4_kernel(tc, x_bytes, x_scale, Wq_words, Wq_scales
 
         def lace_first(i, g):
             dst = rows_x(0, NT)[:, g, P * i : P * (i + 1)].rearrange("p n h e -> p n (h e)")
-            nc.gpsimd.tensor_copy(out=dst, in_=first_planes[:, g].rearrange("p t n -> p n t"))
+            nc.gpsimd.tensor_copy(out=dst, in_=first_planes[g][:].rearrange("p t n -> p n t"))
 
         def quant_x(b, i0=0, n=NT, cuts=G, parts=ORDER):
             if b not in xc:
@@ -297,10 +307,10 @@ def tile_localattention_pa_t_w4_kernel(tc, x_bytes, x_scale, Wq_words, Wq_scales
             cols = slice(S * b + Q, S * (b + 1) + Q)
             nc.vector.quantize_mx(out=kc[:, cols].bitcast(FP8X4), scales=ksc[:, cols], in_=rows_k(b))
 
-        def project(b, t, passes=ORDER, i0=0, n=NT, name=None):
+        def project(b, t, passes=ORDER, i0=0, n=NT, name=None, order=ORDER):
             per = NT // n
             if (b, i0, t // per) not in acc:
-                acc[b, i0, t // per] = bank(name or f"sum{(4 * b + t) % 3}", [P, per, n * P])
+                acc[b, i0, t // per] = bank(name or f"sum{t % 3}", [P, per, n * P])
             for g in passes:
                 cols = slice(G * P * i0 + n * P * g, G * P * i0 + n * P * (g + 1))
                 nc.tensor.matmul_mx(
@@ -309,8 +319,8 @@ def tile_localattention_pa_t_w4_kernel(tc, x_bytes, x_scale, Wq_words, Wq_scales
                     lhsT_scale=ws_perm[:, g, P * t : P * (t + 1)],
                     rhs=xc[b][:, cols].bitcast(FP8X4),
                     rhs_scale=xsc[b][:, cols],
-                    start=(g == ORDER[0]),
-                    stop=(g == ORDER[-1]),
+                    start=(g == order[0]),
+                    stop=(g == order[-1]),
                 )
 
         def plane_q(b, t):
@@ -349,8 +359,10 @@ def tile_localattention_pa_t_w4_kernel(tc, x_bytes, x_scale, Wq_words, Wq_scales
 
         def scores(b, i0=0, n=NT, name="scores"):
             sc[b, i0] = bank(name, [P, n, P])
-            for i in range(i0, i0 + n):
-                for s in range(2):
+            halves_ = [(i, s) for i in range(i0, i0 + n) for s in range(2)]
+            first = int(b < PARKED)
+            for i, s in halves_[::-1] if first else halves_:
+                if True:
                     qcols = slice(Q * (3 * i + s), Q * (3 * i + s) + P)
                     kcols = slice(S * b + P * i + Q * s, S * b + P * i + Q * s + P)
                     nc.tensor.matmul_mx(
@@ -359,8 +371,8 @@ def tile_localattention_pa_t_w4_kernel(tc, x_bytes, x_scale, Wq_words, Wq_scales
                         lhsT_scale=qsc[b % 2][:, qcols],
                         rhs=kc[:, kcols].bitcast(FP8X4),
                         rhs_scale=ksc[:, kcols],
-                        start=(s == 0),
-                        stop=(s == 1),
+                        start=(s == first),
+                        stop=(s != first),
                     )
 
         def empty_scores(b):
@@ -499,7 +511,7 @@ def tile_localattention_pa_t_w4_kernel(tc, x_bytes, x_scale, Wq_words, Wq_scales
                 fn(b, *args)
 
         def turning(n):
-            return f"turn{1 + n % 3}"
+            return f"turn{n % 3}"
 
         on_s, on_v, on_g = nc.scalar.copy, nc.vector.tensor_copy, nc.gpsimd.tensor_copy
 
@@ -522,16 +534,16 @@ def tile_localattention_pa_t_w4_kernel(tc, x_bytes, x_scale, Wq_words, Wq_scales
         turn_x(0, 3, x_bank("scores"))
         empty_x(0, 0)
         for g in ORDER:
-            plane_x(0, 1, g, first_planes[:, g])
+            plane_x(0, 1, g, first_planes[g][:])
             lace_first(1, g)
         empty_x(0, 2)
         widen(on_s, 1, 3)
         widen(on_s, 1, 1)
-        turn_x(1, 0, x_bank("turn0"))
+        turn_x(1, 0, x_bank(turning(0)))
         turn_x(1, 3, x_bank("sum0"), [1])
-        turn_x(1, 1, x_bank(turning(0)))
+        turn_x(1, 1, x_bank(turning(-1)))
         turn_k(0, 0, turning(1))
-        turn_k(0, 2, turning(-1))
+        turn_k(0, 2, "mixed")
         empty_x(0, 3, 0, NT, 1, 2)
         empty_x(0, 3, 0, NT, 0, 1)
         share_x(1)
@@ -545,6 +557,9 @@ def tile_localattention_pa_t_w4_kernel(tc, x_bytes, x_scale, Wq_words, Wq_scales
                 quant_k(n - 1)
             if n == 2:
                 quant_seam()
+            if n == L - 2:
+                pair_shift(0, nc.vector)
+                pair_exp(0)
             step(quant_q, n - 2)
             if n == 0:
                 permute_scales()
@@ -557,98 +572,96 @@ def tile_localattention_pa_t_w4_kernel(tc, x_bytes, x_scale, Wq_words, Wq_scales
             project(n, 0, [1])
             project(n, 1, [1])
             project(n, 0, [0])
-            if n + 1 not in SHARED:
-                empty_x(n + 1, 3, 0, NT, 1, 2)
+            empty_rest(n + 1)
             empty_x(n + 1, 0, 0, NT, 1, 2)
             turn_x(n + 1, 2, x_bank(turning(n + 1)))
             empty_x(n + 1, 0, 0, NT, 0, 1)
             step(empty_scores, n - 2)
+            if n == L - 2:
+                pair_sum(0)
             if n == 4:
-                fetch(0)
-                fetch(1)
-            if n == 5:
                 load_mask()
                 clear_words(parked(0), parked(0) + FREED, 2)
             if n >= 2:
                 park(n - 2)
                 clear_next()
-                if n < 5:
+                if n % 2:
+                    fetch(n - 3)
+                    fetch(n - 2)
+                if n < L - 2:
                     clear_next()
-            if n == 5:
-                fetch(2)
-                fetch(3)
-            mixed = x_bank(turning(n - 1))
+            mixed = x_bank("mixed")
             turn_x(n + 1, 3, mixed, [0])
             turn_x(n + 2, 3, mixed, [1])
             widen_next(on_s, counts[1])
-            lace(n + 1, 0 if n + 1 in SHARED else P, P + S if n else P)
+            lace(n + 1, P - SHARES[n + 1], P + S if n else P)
             widen_next(on_g, counts[4])
             plane_q(n, 0)
             widen_next(on_s, counts[2])
             if n == 0:
                 turn_k(L, NT - 1, "scores", 1)
             else:
-                turn_k(n, 2, "turn0")
+                turn_k(n, 2, turning(n))
             empty_x(n + 1, 1)
-            project(n, 1, [0])
-            project(n, 2)
-            project(n, 3)
+            if n == L - 2:
+                pair_recip(0)
             if n == 0:
                 empty_k(L, NT - 1, 1)
             else:
                 empty_k(n, 2)
+            project(n, 1, [0])
+            project(n, 2)
+            project(n, 3)
             plane_q(n, 1)
             widen_next(on_s, counts[3])
             empty_x(n + 1, 2)
             empty_x(n + 1, 3, 0, NT, 0, 1)
             plane_q(n, 2)
-            turn_k(n + 1, 0, turning(n))
-            turn_x(n + 2, 0, x_bank("turn0"))
-            if n == L - 2:
+            turn_x(n + 2, 0, x_bank(turning(n + 1)))
+            turn_x(n + 2, 1, x_bank(turning(n)))
+            turn_k(n + 1, 0, turning(n - 1))
+            if n == L - 3:
                 pair_max(0)
-            turn_x(n + 2, 1, x_bank(turning(n + 1)))
-            if n + 2 in SHARED:
+            if SHARES[n + 2]:
                 share_x(n + 2)
             plane_q(n, 3)
             empty_k(n + 1, 0)
         n = L - 1
         quant_k(n - 1)
-        pair_shift(0, nc.vector)
+        pair_finish(0, nc.vector)
         quant_x(n, 0, NT, G, [0])
         quant_q(n - 2)
         quant_x(n, 0, NT, G, [1])
-        lace(L)
-        pair_exp(0)
+        lace(L, P - SHARES[L])
+        store_later_rows(0)
+        store_first_left(0)
         scores(n - 2)
         project(n, 0, [1])
         project(n, 1, [1])
         project(n, 0, [0])
         project(n, 1, [0])
+        empty_x(L, 0, 0, 2)
+        empty_rest(L)
         turn_x(L, 2, x_bank(turning(n + 1)))
-        empty_x(L, 0, 0, 2, 1, 2)
-        empty_x(L, 0, 0, 2, 0, 1)
         empty_scores(n - 2)
         park(n - 2)
+        store_first_right(0)
         fetch(n - 2)
-        pair_sum(0)
-        turn_x(L, 3, x_bank(turning(n - 1)), [0])
+        clear_words(parked(0) + FREED, L * S * S, 4)
+        turn_x(L, 3, x_bank("mixed"), [0])
         empty_q(n, 0)
         empty_q(n, 1)
         empty_x(L, 1, 0, 2)
-        pair_recip(0)
         project(n, 2)
         project(n, 3)
-        turn_k(n, 2, "turn0")
-        turn_k(L, 0, turning(n))
+        turn_k(n, 2, turning(n))
+        turn_k(L, 0, turning(n - 1))
         turn_k(L, 2, "scores", 1)
         empty_x(L, 2, 2, 1)
         pair_max(1)
         empty_x(L, 3, 3, 1, 0, 1)
         quant_x(L, 0, 2, 1)
         pair_shift(1, nc.vector)
-        pair_finish(0, nc.vector)
-        store_later_rows(0)
-        store_first_left(0)
         quant_x(L, 2, 1, 1)
         quant_x(L, 3, 1, 1)
         empty_q(n, 2)
@@ -669,11 +682,9 @@ def tile_localattention_pa_t_w4_kernel(tc, x_bytes, x_scale, Wq_words, Wq_scales
             project(L, t, ORDER, 2, 1, turning(n + 1))
         scores(L - 2, 0, NT, "sum0")
         for t in range(4):
-            project(L, t, ORDER, 3, 1, turning(n - 1))
+            project(L, t, ORDER, 3, 1, "mixed")
         pair_finish(1, nc.vector)
         store_later_rows(1)
-        store_first_right(0)
-        clear_words(parked(0) + FREED, L * S * S, 4)
         store_first_left(1)
         pair_shift(2, nc.vector)
         pair_exp(2)
@@ -685,7 +696,7 @@ def tile_localattention_pa_t_w4_kernel(tc, x_bytes, x_scale, Wq_words, Wq_scales
         for t in range(4):
             empty_q(L, t, 0, 2)
         weave_q(L, 0, 2)
-        scores(L - 1, 0, NT, "turn0")
+        scores(L - 1, 0, NT, turning(n))
         pair_finish(2)
         store_first_right(1)
         store_boxes(2, nc.sync)
@@ -694,7 +705,7 @@ def tile_localattention_pa_t_w4_kernel(tc, x_bytes, x_scale, Wq_words, Wq_scales
         row_max(L - 2)
         exps(L - 2)
         quant_q(L, 2, 2)
-        scores(L, 2, 2, turning(n))
+        scores(L, 2, 2, turning(n - 1))
         mask_scores(L - 1)
         quant_q(L, 0, 2)
         scores(L, 0, 2, "scores")

@@ -55,9 +55,9 @@ def tile_localattention_pa_t_w4_kernel(tc, x_bytes, x_scale, Wq_words, Wq_scales
         psum = ctx.enter_context(tc.psum_pool(name="psum", bufs=1))
         ctx.enter_context(tc.manual_schedule())
 
-        ident = keep.tile([P, P], F32, name="ident")
+        ident = keep.tile([P, P], F32, name="ident", align_bytes=256)
         scale_p = keep.tile([P, G, 4], F32, name="scale_p")
-        wides = [keep.tile([P, NT * D], BF16, name=f"wide{j}", align_bytes=64) for j in range(WIDE)]
+        wides = [keep.tile([P, NT * D], BF16, name=f"wide{j}", align_bytes=256) for j in range(WIDE)]
         rows = keep.tile([P, 4 * S * (G + 1)], BF16, name="rows", align_bytes=64)
         planes = [keep.tile([P, 4, P + S], BF16, name=f"planes{j}", align_bytes=64) for j in range(2)]
         first_planes = [keep.tile([P, 4, P], BF16, name=f"first_planes{g}", align_bytes=64) for g in range(G)]
@@ -66,17 +66,17 @@ def tile_localattention_pa_t_w4_kernel(tc, x_bytes, x_scale, Wq_words, Wq_scales
         k_last = keep.tile([P, S * 4], BF16, name="k_last", align_bytes=64)
         strips = keep.tile([P, B - PARKED, NT, STRIP], F32, name="strips")
         w_raw = [keep.tile([P, 2 * E], U8, name=f"w_raw{g}", align_bytes=64) for g in range(G)]
-        w_perm = keep.tile([P, G, 2 * E], U8, name="w_perm", align_bytes=64)
+        w_perm = keep.tile([P, G, 2 * E], U8, name="w_perm", align_bytes=256)
         ws_raw = keep.tile([P, G, E], U8, name="ws_raw", align_bytes=64)
-        ws_perm = keep.tile([P, G, E], U8, name="ws_perm", align_bytes=64)
+        ws_perm = keep.tile([P, G, E], U8, name="ws_perm", align_bytes=256)
         bias = keep.tile([P, 4], BF16, name="bias")
         stencil = keep.tile([P, STENCIL], F32, name="stencil")
         mask = keep.tile([P, NT, STRIP], F32, name="mask")
         zeros = keep.tile([P, S], F32, name="zeros")
-        kc = keep.tile([P, B * S + Q], U32, name="kc", align_bytes=64)
-        ksc = keep.tile([P, B * S + Q], U8, name="ksc", align_bytes=64)
-        qc = [keep.tile([P, NT * 3 * Q], U32, name=f"qc{j}", align_bytes=64) for j in range(2)]
-        qsc = [keep.tile([P, NT * 3 * Q], U8, name=f"qsc{j}", align_bytes=64) for j in range(2)]
+        kc = keep.tile([P, B * S + Q], U32, name="kc", align_bytes=256)
+        ksc = keep.tile([P, B * S + Q], U8, name="ksc", align_bytes=256)
+        qc = [keep.tile([P, NT * 3 * Q], U32, name=f"qc{j}", align_bytes=256) for j in range(2)]
+        qsc = [keep.tile([P, NT * 3 * Q], U8, name=f"qsc{j}", align_bytes=256) for j in range(2)]
 
         diag = [keep.tile([P, ROWS, PITCH], F32, name=f"diag{j}", align_bytes=64) for j in range(PAIRS)]
         boxes = [keep.tile([P, ROWS * BOX + ROWS], F32, name=f"boxes{j}", align_bytes=64) for j in range(PAIRS)]
@@ -84,8 +84,8 @@ def tile_localattention_pa_t_w4_kernel(tc, x_bytes, x_scale, Wq_words, Wq_scales
         x_first = [keep.tile([P, D], U8, name=f"x_codes_first{i}", align_bytes=64) for i in range(NT)]
         x_second = keep.tile([P, 2, D], U8, name="x_codes_second", align_bytes=64)
         x_tiles = [keep.tile([P, NT, D], U8, name=f"x_codes{b}", align_bytes=64) if b else None for b in range(B)]
-        k_tiles = [keep.tile([P, NT, E], BF16, name=f"k_rows{b}", align_bytes=64) for b in range(B)]
-        k_seam = keep.tile([P, E], BF16, name="k_seam", align_bytes=64)
+        k_tiles = [keep.tile([P, NT, E], BF16, name=f"k_rows{b}", align_bytes=256) for b in range(B)]
+        k_seam = keep.tile([P, E], BF16, name="k_seam", align_bytes=256)
 
         xv = x_bytes.rearrange("b (i p) k -> b p i k", p=P)
         kflat = k.rearrange("b s e -> (b s) e")
@@ -277,8 +277,8 @@ def tile_localattention_pa_t_w4_kernel(tc, x_bytes, x_scale, Wq_words, Wq_scales
 
         def quant_x(b, i0=0, n=NT, cuts=G, parts=ORDER):
             if b not in xc:
-                xc[b] = work.tile([P, G * S], U32, name="xc", align_bytes=64)
-                xsc[b] = work.tile([P, G * S], U8, name="xsc", align_bytes=64)
+                xc[b] = work.tile([P, G * S], U32, name="xc", align_bytes=256)
+                xsc[b] = work.tile([P, G * S], U8, name="xsc", align_bytes=256)
             w = G * P * n // cuts
             for g in parts if cuts > 1 else [0]:
                 cols = slice(G * P * i0 + w * g, G * P * i0 + w * (g + 1))

import math
from contextlib import ExitStack

import concourse.mybir as mybir
from concourse.masks import make_identity

B, S, D, E = 8, 512, 1024, 512
HALF = 5
FLOPS = 2 * B * S * D * E + 2 * B * S * S * E

F32 = mybir.dt.float32
BF16 = mybir.dt.bfloat16
I32 = mybir.dt.int32
U32 = mybir.dt.uint32
U8 = mybir.dt.uint8
FP8 = mybir.dt.float8_e4m3fn
FP8X4 = mybir.dt.float8_e4m3fn_x4
FP4X4 = mybir.dt.float4_e2m1fn_x4
ALU = mybir.AluOpType
ACT = mybir.ActivationFunctionType
AX = mybir.AxisListType

P = 128
NT = S // P
G = D // 512
Q = 64
SHIFT = 32
MARGIN = 8
STRIP = Q + 2 * MARGIN
LIVE = slice(MARGIN - HALF, STRIP - MARGIN + HALF)
WIDTH = Q + 2 * HALF
MASKED = -1e9
SCALE = 1.0 / math.sqrt(E)
L = B - 1
PARKED = 5
BAND = 2 * HALF + 1
ROWS = 8
PITCH = 16
BOX = 3 * MARGIN
PAIRS = (PARKED + 1) // 2
ROOM = S * (STRIP + 1)
FREED = 2 * ROOM // 2048 * 2048
STENCIL = Q + STRIP + 2 * MARGIN
ORDER = (1, 0)
COUNTS = [(0, 2, 2, 2, 4), (1, 2, 3, 2, 2), (1, 2, 3, 1, 0), (1, 2, 3, 1, 0), (1, 2, 3, 1, 0), (1, 2, 2, 1, 0)]
SHARES = (0, 128, 0, 128, 128, 128, 128, 128)
WIDE = 4


def tile_localattention_pa_t_w4_kernel(tc, x_bytes, x_scale, Wq_words, Wq_scales, bq, k, out):
    nc = tc.nc
    with ExitStack() as ctx:
        keep = ctx.enter_context(tc.tile_pool(name="keep", bufs=1))
        work = ctx.enter_context(tc.tile_pool(name="work", bufs=2))
        psum = ctx.enter_context(tc.psum_pool(name="psum", bufs=1))
        ctx.enter_context(tc.manual_schedule())

        ident = keep.tile([P, P], F32, name="ident", align_bytes=256)
        scale_p = keep.tile([P, G, 4], F32, name="scale_p")
        wides = [keep.tile([P, NT * D], BF16, name=f"wide{j}", align_bytes=256) for j in range(WIDE)]
        rows = keep.tile([P, 4 * S * (G + 1)], BF16, name="rows", align_bytes=64)
        planes = [keep.tile([P, 4, P + S], BF16, name=f"planes{j}", align_bytes=64) for j in range(2)]
        first_planes = [keep.tile([P, 4, P], BF16, name=f"first_planes{g}", align_bytes=64) for g in range(G)]
        q_tail = [keep.tile([P, S * 4], BF16, name=f"q_tail{j}", align_bytes=64) for j in range(2)]
        kt = [keep.tile([P, S * 4], BF16, name=f"kt{j}", align_bytes=64) for j in range(2)]
        k_last = keep.tile([P, S * 4], BF16, name="k_last", align_bytes=64)
        strips = keep.tile([P, B - PARKED, NT, STRIP], F32, name="strips")
        w_raw = [keep.tile([P, 2 * E], U8, name=f"w_raw{g}", align_bytes=64) for g in range(G)]
        w_perm = keep.tile([P, G, 2 * E], U8, name="w_perm", align_bytes=256)
        ws_raw = keep.tile([P, G, E], U8, name="ws_raw", align_bytes=64)
        ws_perm = keep.tile([P, G, E], U8, name="ws_perm", align_bytes=256)
        bias = keep.tile([P, 4], BF16, name="bias")
        stencil = keep.tile([P, STENCIL], F32, name="stencil")
        mask = keep.tile([P, NT, STRIP], F32, name="mask")
        zeros = keep.tile([P, S], F32, name="zeros")
        kc = keep.tile([P, B * S + Q], U32, name="kc", align_bytes=256)
        ksc = keep.tile([P, B * S + Q], U8, name="ksc", align_bytes=256)
        qc = [keep.tile([P, NT * 3 * Q], U32, name=f"qc{j}", align_bytes=256) for j in range(2)]
        qsc = [keep.tile([P, NT * 3 * Q], U8, name=f"qsc{j}", align_bytes=256) for j in range(2)]

        diag = [keep.tile([P, ROWS, PITCH], F32, name=f"diag{j}", align_bytes=64) for j in range(PAIRS)]
        boxes = [keep.tile([P, ROWS * BOX + ROWS], F32, name=f"boxes{j}", align_bytes=64) for j in range(PAIRS)]

        x_first = [keep.tile([P, D], U8, name=f"x_codes_first{i}", align_bytes=64) for i in range(NT)]
        x_second = keep.tile([P, 2, D], U8, name="x_codes_second", align_bytes=64)
        x_tiles = [keep.tile([P, NT, D], U8, name=f"x_codes{b}", align_bytes=64) if b else None for b in range(B)]
        k_tiles = [keep.tile([P, NT, E], BF16, name=f"k_rows{b}", align_bytes=256) for b in range(B)]
        k_seam = keep.tile([P, E], BF16, name="k_seam", align_bytes=256)

        xv = x_bytes.rearrange("b (i p) k -> b p i k", p=P)
        kflat = k.rearrange("b s e -> (b s) e")
        oflat = out.rearrange("b s j -> b (s j)")
        flat = out.rearrange("b s j -> (b s j)")

        def load_x(b):
            nc.sync.dma_start(out=x_tiles[b][:], in_=xv[b])

        def load_k(b):
            n = NT - (b == L)
            source = kflat[S * b + SHIFT : S * b + SHIFT + P * n, :]
            nc.sync.dma_start(out=k_tiles[b][:, 0:n, :], in_=source.rearrange("(i p) e -> p i e", p=P))

        def load_seam():
            seam = B * S - (P - SHIFT)
            nc.sync.dma_start(out=k_seam[0:Q, :], in_=kflat[seam : seam + Q, :])
            nc.sync.dma_start(out=k_seam[Q : P - SHIFT, :], in_=kflat[seam + Q : B * S, :])
            nc.sync.dma_start(out=k_seam[P - SHIFT : P, :], in_=kflat[0:SHIFT, :])

        nc.vector.memset(ident[:], 0.0)
        nc.vector.memset(ws_raw[:].rearrange("p g n -> p (g n)").bitcast(I32), 0)
        nc.vector.memset(zeros[:], 0.0)
        nc.sync.dma_start(out=x_first[0][:], in_=xv[0][:, 0, :])
        nc.sync.dma_start(out=scale_p[:], in_=x_scale.rearrange("a b (g p c) -> p (a b g) c", p=P, c=4))
        nc.sync.dma_start(out=x_first[1][:], in_=xv[0][:, 1, :])
        for g in range(G):
            nc.sync.dma_start(out=w_raw[g][:].bitcast(I32), in_=Wq_words[g].bitcast(I32))
            nc.sync.dma_start(out=x_first[2 + g][:], in_=xv[0][:, 2 + g, :])
        nc.sync.dma_start(out=x_second[:], in_=xv[1][:, 0:2, :])
        for q in range(4):
            nc.sync.dma_start(
                out=ws_raw[32 * q : 32 * q + 4].bitcast(I32),
                in_=Wq_scales[:, 4 * q : 4 * q + 4, :].rearrange("g r n -> r g n").bitcast(I32),
            )
        nc.sync.dma_start(out=x_tiles[1][:, 2:NT, :], in_=xv[1][:, 2:NT, :])
        load_k(0)
        load_x(2)
        nc.sync.dma_start(out=bias[:], in_=bq.rearrange("(p t) -> p t", t=4))
        load_seam()
        for b in range(3, B):
            load_k(b - 2)
            load_x(b)
        load_k(L - 1)
        load_k(L)

        make_identity(nc, ident[:], nomemset=True)
        nc.vector.memset(stencil[:], MASKED)
        for padded in qc + qsc:
            nc.vector.memset(padded[:].bitcast(I32).rearrange("p (i u n) -> p i u n", i=NT, u=3)[:, :, 1, :], 0)
        nc.vector.memset(stencil[:, Q + MARGIN - HALF : Q + MARGIN + HALF + 1], 0.0)
        for j in range(PAIRS):
            nc.scalar.activation(out=boxes[j][:], in_=zeros[:, 0 : ROWS * (BOX + 1)], func=ACT.Copy)

        def clear_words(lo, hi, r):
            n = (hi - lo) // (P * r)
            rows = flat[lo:hi].rearrange("(p r n) -> p r n", p=P, r=r)
            nc.sync.dma_start(out=rows, in_=zeros[:, 0:n].unsqueeze(1).to_broadcast([P, r, n]))

        def clear(b):
            clear_words(b * S * S, (b + 1) * S * S, NT)

        def parked(b):
            return (L - 1) * S * S + b * ROOM

        def lay_stencil():
            lo = parked(PARKED)
            nc.sync.dma_start(out=flat[lo : lo + P * STENCIL].rearrange("(p c) -> p c", p=P), in_=stencil[:])

        def load_mask():
            lo = parked(PARKED)
            for s in range(2):
                at = lo + Q * STENCIL * s + Q
                rows = flat[at : at + Q * (STENCIL - 1)].rearrange("(r c) -> r c", r=Q)[:, 0:STRIP]
                inner, outer = strip_parts(s)
                nc.sync.dma_start(out=mask[Q * s : Q * (s + 1), inner, :], in_=rows.unsqueeze(1).to_broadcast([Q, NT - 1, STRIP]))
                nc.sync.dma_start(out=mask[Q * s : Q * (s + 1), outer[0], outer[1]], in_=rows[:, outer[1]])

        def clear_margins():
            for margin in (slice(0, LIVE.start), slice(LIVE.stop, STRIP)):
                nc.vector.memset(strips[:].rearrange("p j i c -> p (j i) c")[:, :, margin], 0.0)

        def mask_edges():
            nc.vector.memset(mask[0:Q, 0, 0:MARGIN], MASKED)
            nc.vector.memset(mask[Q:P, NT - 1, STRIP - MARGIN : STRIP], MASKED)

        def strip_parts(s):
            return slice(1 - s, NT - s), (s * (NT - 1), slice(MARGIN * (1 - s), STRIP - MARGIN * s))

        def park_edges():
            for s in range(2):
                lo = parked(0) + s * (ROOM - Q * (STRIP + 1) + STRIP - MARGIN)
                view = flat[lo : lo + PARKED * ROOM].rearrange("(b y) -> b y", b=PARKED)[:, 0 : Q * STRIP]
                cells = view.rearrange("b (r j) -> r b j", r=Q)[:, :, 0:MARGIN]
                nc.sync.dma_start(out=cells, in_=stencil[Q * s : Q * (s + 1), 0 : PARKED * MARGIN].rearrange("p (b j) -> p b j", b=PARKED))

        clear_margins()
        mask_edges()
        park_edges()
        lay_stencil()

        xt, xc, xsc, ktp, acc, qp = {}, {}, {}, {}, {}, {}
        sc, sm, nm, ss, rs = {}, {}, {}, {}, {}
        raw, top, total, inverse = {}, {}, {}, {}

        def permute_codes(g):
            nc.vector.tensor_copy(
                out=w_perm[:, g, :].rearrange("p (t m c) -> p t m c", t=4, c=2),
                in_=w_raw[g][:].rearrange("p (m t c) -> p t m c", t=4, c=2),
            )

        def permute_scales():
            nc.vector.tensor_copy(
                out=ws_perm[:].rearrange("p g (t m) -> p g t m", t=4),
                in_=ws_raw[:].rearrange("p g (m t) -> p g t m", t=4),
            )

        def wide(b, i, n=1):
            return wides[b % WIDE][:, D * i : D * (i + n)]

        def widen(copy, b, i):
            codes = x_first[i][:] if b == 0 else x_tiles[b][:, i, :] if i > 1 else x_second[:, i, :]
            copy(out=wide(b, i), in_=codes.bitcast(FP8))

        halves = [(b, u) for b in range(2, B) for u in [2 * NT - 1] + list(range(2 * NT - 1))]

        def widen_next(copy, count):
            while count:
                b, u = halves[0]
                run = 1
                while run < count and halves[run] == (b, u + run):
                    run += 1
                cols = slice(512 * u, 512 * (u + run))
                codes = x_tiles[b][:].rearrange("p i k -> p (i k)")[:, cols]
                copy(out=wide(b, 0, NT)[:, cols], in_=codes.bitcast(FP8))
                for j in range(run):
                    halves.remove(halves[0])
                count -= run

        def bank(name, shape):
            return psum.tile(shape, F32, name=name, bufs=1)

        def turn_x(b, i, room, passes=range(G)):
            words = wide(b, i).bitcast(F32)
            for g in passes:
                xt[b, i, g] = room
                for h in range(2):
                    nc.tensor.transpose(room[:, h, g, :], words[:, 256 * g + h : 256 * (g + 1) : 2], ident[:])

        def x_bank(name):
            return bank(name, [P, 2, G, P])

        def rows_x(i0, n):
            room = rows[:, G * 4 * P * i0 : G * 4 * P * (i0 + n)]
            return room.rearrange("p (g n h e) -> p g n h e", g=G, h=2, e=2)

        def empty_x(b, i, i0=0, n=NT, g0=0, g1=G):
            dst = rows_x(i0, n)[:, g0:g1, P * (i - i0) : P * (i - i0 + 1)]
            values = xt[b, i, g0][:].bitcast(BF16).rearrange("p h g (r e) -> p g r h e", e=2)[:, g0:g1]
            scales = scale_p[:, g0:g1].rearrange("p g (h e) -> p g h e", e=2).unsqueeze(2).to_broadcast([P, g1 - g0, P, 2, 2])
            nc.vector.tensor_tensor(out=dst, in0=values, in1=scales, op=ALU.mult)

        def empty_rest(b):
            n = P - SHARES[b]
            if n == 0:
                return
            at = 4 * (G * S - P)
            dst = rows[:, at : at + 4 * n].rearrange("p (n h e) -> p n h e", h=2, e=2)
            values = xt[b, NT - 1, G - 1][:].bitcast(BF16).rearrange("p h g (r e) -> p g r h e", e=2)[:, G - 1, 0:n]
            scales = scale_p[:, G - 1].rearrange("p (h e) -> p h e", e=2).unsqueeze(1).to_broadcast([P, n, 2, 2])
            nc.vector.tensor_tensor(out=dst, in0=values, in1=scales, op=ALU.mult)

        def plane_x(b, i, g, dst, lo=0):
            for t in range(4):
                values = xt[b, i, g][:, t // 2, g, lo:].bitcast(BF16)[:, t % 2 :: 2]
                nc.scalar.activation(out=dst[:, t, :], in_=values, func=ACT.Copy, scale=scale_p[:, g, t : t + 1])

        def share_x(b):
            plane_x(b, NT - 1, G - 1, planes[b % 2][:, :, P - SHARES[b] : P], P - SHARES[b])

        def lace(b, lo=0, hi=P + S):
            at = 4 * (G * S - P)
            dst = rows[:, at + 4 * lo : at + 4 * hi].rearrange("p (n t) -> p n t", t=4)
            nc.gpsimd.tensor_copy(out=dst, in_=planes[b % 2][:, :, lo:hi].rearrange("p t n -> p n t"))

        def lace_first(i, g):
            dst = rows_x(0, NT)[:, g, P * i : P * (i + 1)].rearrange("p n h e -> p n (h e)")
            nc.gpsimd.tensor_copy(out=dst, in_=first_planes[g][:].rearrange("p t n -> p n t"))

        def quant_x(b, i0=0, n=NT, cuts=G, parts=ORDER):
            if b not in xc:
                xc[b] = work.tile([P, G * S], U32, name="xc", align_bytes=256)
                xsc[b] = work.tile([P, G * S], U8, name="xsc", align_bytes=256)
            w = G * P * n // cuts
            for g in parts if cuts > 1 else [0]:
                cols = slice(G * P * i0 + w * g, G * P * i0 + w * (g + 1))
                nc.vector.quantize_mx(
                    out=xc[b][:, cols].bitcast(FP8X4), scales=xsc[b][:, cols], in_=rows[:, 4 * cols.start : 4 * cols.stop]
                )

        def rows_k(b):
            return k_last[:] if b == L else kt[b % 2][:] if b else rows[:, 4 * G * S :]

        def turn_k(b, j0, name, n=2):
            ktp[b, j0] = bank(name, [P, n, 2, P])
            for j in range(n):
                words = (k_seam[:] if (b, j0 + j) == (L, NT - 1) else k_tiles[b][:, j0 + j, :]).bitcast(F32)
                for h in range(2):
                    nc.tensor.transpose(ktp[b, j0][:, j, h, :], words[:, h:256:2], ident[:])

        def empty_k(b, j0, n=2):
            dst = rows_k(b)[:, S * j0 : S * (j0 + n)].bitcast(F32).rearrange("p (j r h) -> p j r h", j=n, h=2)
            nc.scalar.copy(out=dst, in_=ktp[b, j0][:].rearrange("p j h r -> p j r h"))

        def quant_seam():
            nc.vector.quantize_mx(out=kc[:, 0:Q].bitcast(FP8X4), scales=ksc[:, 0:Q], in_=rows_k(L)[:, 4 * (S - Q) :])

        def quant_k(b):
            cols = slice(S * b + Q, S * (b + 1) + Q)
            nc.vector.quantize_mx(out=kc[:, cols].bitcast(FP8X4), scales=ksc[:, cols], in_=rows_k(b))

        def project(b, t, passes=ORDER, i0=0, n=NT, name=None, order=ORDER):
            per = NT // n
            if (b, i0, t // per) not in acc:
                acc[b, i0, t // per] = bank(name or f"sum{t % 3}", [P, per, n * P])
            for g in passes:
                cols = slice(G * P * i0 + n * P * g, G * P * i0 + n * P * (g + 1))
                nc.tensor.matmul_mx(
                    out=acc[b, i0, t // per][:, t % per, :],
                    lhsT=w_perm[:, g, 256 * t : 256 * (t + 1)].bitcast(FP4X4),
                    lhsT_scale=ws_perm[:, g, P * t : P * (t + 1)],
                    rhs=xc[b][:, cols].bitcast(FP8X4),
                    rhs_scale=xsc[b][:, cols],
                    start=(g == order[0]),
                    stop=(g == order[-1]),
                )

        def plane_q(b, t):
            nc.scalar.activation(out=planes[b % 2][:, t, P:], in_=acc[b, 0, t][:, 0, :], func=ACT.Identity, bias=bias[:, t : t + 1])

        def empty_q(b, t, i0=0, n=NT):
            if b not in qp:
                qp[b] = work.tile([P, 2, S], F32, name="qp", align_bytes=64)
            per = NT // n
            pair = qp[b][:, t // 2, P * i0 : P * (i0 + n)].bitcast(BF16)
            nc.scalar.activation(out=pair[:, t % 2 :: 2], in_=acc[b, i0, t // per][:, t % per, :], func=ACT.Identity, bias=bias[:, t : t + 1])

        def rows_q(b):
            return rows[:, 4 * G * S :] if b < L - 1 else q_tail[b % 2][:]

        def weave_q(b, i0=0, n=NT):
            dst = rows_q(b)[:, 4 * P * i0 : 4 * P * (i0 + n)].bitcast(F32).rearrange("p (n h) -> p n h", h=2)
            nc.scalar.copy(out=dst, in_=qp[b][:, :, P * i0 : P * (i0 + n)].rearrange("p h n -> p n h"))

        def empty_q_v(b, i):
            nc.vector.tensor_tensor(
                out=rows_q(b)[:, 4 * P * i : 4 * P * (i + 1)].rearrange("p (n t) -> p n t", t=4),
                in0=acc[b, i, 0][:].rearrange("p t n -> p n t"),
                in1=bias[:].unsqueeze(1).to_broadcast([P, P, 4]),
                op=ALU.add,
            )

        def quant_q(b, i0=0, n=NT):
            cuts = [P * i0] + list(range(P * i0 + Q, P * (i0 + n), P)) + [P * (i0 + n)]
            for lo, hi in zip(cuts[:-1], cuts[1:]):
                at = lo + Q * ((lo // Q + 1) // 2)
                cols = slice(at, at + hi - lo)
                nc.vector.quantize_mx(
                    out=qc[b % 2][:, cols].bitcast(FP8X4), scales=qsc[b % 2][:, cols], in_=rows_q(b)[:, 4 * lo : 4 * hi]
                )

        def scores(b, i0=0, n=NT, name="scores"):
            sc[b, i0] = bank(name, [P, n, P])
            halves_ = [(i, s) for i in range(i0, i0 + n) for s in range(2)]
            first = int(b < PARKED)
            for i, s in halves_[::-1] if first else halves_:
                if True:
                    qcols = slice(Q * (3 * i + s), Q * (3 * i + s) + P)
                    kcols = slice(S * b + P * i + Q * s, S * b + P * i + Q * s + P)
                    nc.tensor.matmul_mx(
                        out=sc[b, i0][:, i - i0, :],
                        lhsT=qc[b % 2][:, qcols].bitcast(FP8X4),
                        lhsT_scale=qsc[b % 2][:, qcols],
                        rhs=kc[:, kcols].bitcast(FP8X4),
                        rhs_scale=ksc[:, kcols],
                        start=(s == first),
                        stop=(s != first),
                    )

        def empty_scores(b):
            raw[b] = work.tile([P, NT, STRIP], F32, name="raw", bufs=4, align_bytes=64)
            window = sc[b, 0][:, :, SHIFT - MARGIN : SHIFT - MARGIN + STRIP]
            nc.scalar.activation(out=raw[b][:], in_=window, func=ACT.Copy, scale=SCALE)

        def park(b):
            for s in range(2):
                lo = parked(b) + (STRIP + 1) * Q * s
                view = flat[lo : lo + ROOM].rearrange("(i y) -> i y", i=NT)[:, 0 : Q * STRIP].rearrange("i (r j) -> r i j", r=Q)
                rows = raw[b][Q * s : Q * (s + 1)]
                inner, outer = strip_parts(s)
                nc.sync.dma_start(out=view[:, inner, :], in_=rows[:, inner, :])
                nc.sync.dma_start(out=view[:, outer[0], outer[1]], in_=rows[:, outer[0], outer[1]])

        def fetch(b):
            lo = parked(b) + MARGIN - HALF
            view = flat[lo : lo + ROOM].rearrange("(p r y) -> p r y", r=ROWS, y=STRIP + 1)[:, :, 0:BAND]
            nc.sync.dma_start(out=diag[b // 2][Q * (b % 2) : Q * (b % 2 + 1), :, 0:BAND], in_=view)

        def members(j):
            return min(2, PARKED - 2 * j)

        def held(j):
            return slice(0, Q * members(j))

        def pair_max(j):
            top[j] = work.tile([P, ROWS], F32, name="top")
            nc.vector.tensor_reduce(out=top[j][held(j)], in_=diag[j][held(j), :, 0:BAND], axis=AX.X, op=ALU.max, negate=True)

        def pair_shift(j, eng=nc.gpsimd):
            live = diag[j][held(j), :, 0:BAND]
            eng.tensor_tensor(out=live, in0=live, in1=top[j][held(j)].unsqueeze(2).to_broadcast([Q * members(j), ROWS, BAND]), op=ALU.add)

        def pair_exp(j):
            live = diag[j][held(j), :, 0:BAND]
            nc.scalar.activation(out=live, in_=live, func=ACT.Exp)

        def pair_sum(j):
            total[j] = work.tile([P, ROWS], F32, name="total")
            nc.vector.tensor_reduce(out=total[j][held(j)], in_=diag[j][held(j), :, 0:BAND], axis=AX.X, op=ALU.add)

        def pair_recip(j):
            inverse[j] = work.tile([P, ROWS], F32, name="inverse")
            nc.vector.reciprocal(out=inverse[j][held(j)], in_=total[j][held(j)])

        def pair_finish(j, eng=nc.gpsimd):
            first = MARGIN - HALF
            skew = boxes[j][held(j)].rearrange("p (r c) -> p r c", r=ROWS)[:, :, first : first + BAND]
            eng.tensor_tensor(
                out=skew, in0=diag[j][held(j), :, 0:BAND], in1=inverse[j][held(j)].unsqueeze(2).to_broadcast([Q * members(j), ROWS, BAND]), op=ALU.mult
            )

        def box_rows(b, at, n, r):
            lo = b * S * S - MARGIN + at
            return flat[lo : lo + n * ROWS * (S + 1)].rearrange("(p y) -> p y", p=n)[:, 0 : r * S].rearrange("p (r j) -> p r j", r=r)

        def box_view(j):
            return boxes[j][:, 0 : ROWS * BOX].rearrange("p (r c) -> p r c", r=ROWS)

        def store_later_rows(j, eng=nc.sync):
            for u in range(members(j)):
                eng.dma_start(out=box_rows(2 * j + u, S, Q, ROWS - 1)[:, :, 0:BOX], in_=box_view(j)[Q * u : Q * (u + 1), 1:ROWS, :])

        def store_first_left(j, eng=nc.sync):
            for u in range(members(j)):
                eng.dma_start(out=box_rows(2 * j + u, ROWS * (S + 1), Q - 1, 1)[:, 0, 0:MARGIN], in_=box_view(j)[Q * u + 1 : Q * (u + 1), 0, 0:MARGIN])

        def store_first_right(j, eng=nc.sync):
            for u in range(members(j)):
                eng.dma_start(out=box_rows(2 * j + u, MARGIN, Q, 1)[:, 0, 0 : BOX - MARGIN], in_=box_view(j)[Q * u : Q * (u + 1), 0, MARGIN:BOX])

        def store_boxes(j, eng):
            store_later_rows(j, eng)
            store_first_left(j, eng)
            store_first_right(j, eng)

        def mask_scores(b, i0=0, n=NT):
            sm[b, i0] = work.tile([P, n, WIDTH], F32, name="sm", bufs=6)
            window = sc[b, i0][:, :, SHIFT - HALF : SHIFT - HALF + WIDTH]
            nc.vector.scalar_tensor_tensor(
                out=sm[b, i0][:], in0=window, scalar=SCALE, in1=mask[:, i0 : i0 + n, LIVE], op0=ALU.mult, op1=ALU.add
            )

        def row_max(b, i0=0, n=NT):
            nm[b, i0] = work.tile([P, n], F32, name="nm", bufs=6)
            nc.vector.tensor_reduce(out=nm[b, i0][:], in_=sm[b, i0][:], axis=AX.X, op=ALU.max, negate=True)

        def exps(b, i0=0, n=NT):
            ss[b, i0] = work.tile([P, n], F32, name="ss", bufs=6)
            for i in range(n):
                row = sm[b, i0][:, i, :]
                nc.scalar.activation(out=row, in_=row, func=ACT.Exp, bias=nm[b, i0][:, i : i + 1], accum_out=ss[b, i0][:, i : i + 1])

        def recip(b, i0=0, n=NT):
            rs[b, i0] = work.tile([P, n], F32, name="rs", bufs=6)
            nc.vector.reciprocal(out=rs[b, i0][:], in_=ss[b, i0][:])

        def strip_rows(b, i0, n, s):
            diag = P * S + P
            back = 2 * S
            lo = diag * i0 + (Q * S + Q) * s - MARGIN - back
            view = oflat[b][lo : lo + n * diag].rearrange("(i y) -> i y", i=n)[:, back : back + Q * S]
            return view.rearrange("i (r j) -> r i j", r=Q)[:, :, 0:STRIP]

        def store_inner(b, other=nc.sync):
            nc.sync.dma_start(out=strip_rows(b, 1, NT - 1, 0), in_=strips[0:Q, b - PARKED, 1:NT, :])
            other.dma_start(out=strip_rows(b, 0, NT - 1, 1), in_=strips[Q:P, b - PARKED, 0 : NT - 1, :])

        def store_edges(b, n=1, other=nc.sync):
            first = out[b : b + n, 0:Q, 0 : STRIP - MARGIN].rearrange("b r j -> r b j")
            last = out[b : b + n, S - Q : S, S - STRIP + MARGIN : S].rearrange("b r j -> r b j")
            nc.sync.dma_start(out=first, in_=strips[0:Q, b - PARKED : b - PARKED + n, 0, MARGIN:STRIP])
            other.dma_start(out=last, in_=strips[Q:P, b - PARKED : b - PARKED + n, NT - 1, 0 : STRIP - MARGIN])

        def store(b):
            store_inner(b)
            store_edges(b)

        def finish(b, i0=0, n=NT):
            strip = strips[:, b - PARKED, i0 : i0 + n, LIVE]
            for i in range(n):
                nc.scalar.activation(out=strip[:, i, :], in_=sm[b, i0][:, i, :], func=ACT.Copy, scale=rs[b, i0][:, i : i + 1])

        def finish_v(b, i0=0, n=NT, lo=0, eng=nc.vector):
            eng.tensor_tensor(
                out=strips[:, b - PARKED, i0 + lo : i0 + n, LIVE],
                in0=sm[b, i0][:, lo:n],
                in1=rs[b, i0][:, lo:n].unsqueeze(2).to_broadcast([P, n - lo, WIDTH]),
                op=ALU.mult,
            )

        def step(fn, b, *args):
            if 0 <= b < B:
                fn(b, *args)

        def turning(n):
            return f"turn{n % 3}"

        on_s, on_v, on_g = nc.scalar.copy, nc.vector.tensor_copy, nc.gpsimd.tensor_copy

        to_clear = [b for b in range(B) if b != L - 1]

        def clear_next():
            clear(to_clear[0])
            to_clear.remove(to_clear[0])

        widen(on_v, 0, 0)
        widen(on_s, 0, 1)
        widen(on_s, 0, 2)
        widen(on_s, 0, 3)
        for g in range(G):
            permute_codes(g)
        widen(on_g, 1, 0)
        turn_x(0, 0, x_bank("sum0"))
        turn_x(0, 1, x_bank("sum1"))
        turn_x(0, 2, x_bank("sum2"))
        turn_x(0, 3, x_bank("scores"))
        empty_x(0, 0)
        for g in ORDER:
            plane_x(0, 1, g, first_planes[g][:])
            lace_first(1, g)
        empty_x(0, 2)
        widen(on_s, 1, 3)
        widen(on_s, 1, 1)
        turn_x(1, 0, x_bank(turning(0)))
        turn_x(1, 3, x_bank("sum0"), [1])
        turn_x(1, 1, x_bank(turning(-1)))
        turn_k(0, 0, turning(1))
        turn_k(0, 2, "mixed")
        empty_x(0, 3, 0, NT, 1, 2)
        empty_x(0, 3, 0, NT, 0, 1)
        share_x(1)
        widen(on_s, 1, 2)
        empty_k(0, 0)
        empty_k(0, 2)
        widen_next(on_s, 1)
        for n in range(L - 1):
            counts = COUNTS[n]
            if n > 1:
                quant_k(n - 1)
            if n == 2:
                quant_seam()
            if n == L - 2:
                pair_shift(0, nc.vector)
                pair_exp(0)
            step(quant_q, n - 2)
            if n == 0:
                permute_scales()
            quant_x(n, 0, NT, G, [1])
            if n == 1:
                quant_k(0)
            quant_x(n, 0, NT, G, [0])
            widen_next(on_s, counts[0])
            step(scores, n - 2)
            project(n, 0, [1])
            project(n, 1, [1])
            project(n, 0, [0])
            empty_rest(n + 1)
            empty_x(n + 1, 0, 0, NT, 1, 2)
            turn_x(n + 1, 2, x_bank(turning(n + 1)))
            empty_x(n + 1, 0, 0, NT, 0, 1)
            step(empty_scores, n - 2)
            if n == L - 2:
                pair_sum(0)
            if n == 4:
                load_mask()
                clear_words(parked(0), parked(0) + FREED, 2)
            if n >= 2:
                park(n - 2)
                clear_next()
                if n % 2:
                    fetch(n - 3)
                    fetch(n - 2)
                if n < L - 2:
                    clear_next()
            mixed = x_bank("mixed")
            turn_x(n + 1, 3, mixed, [0])
            turn_x(n + 2, 3, mixed, [1])
            widen_next(on_s, counts[1])
            lace(n + 1, P - SHARES[n + 1], P + S if n else P)
            widen_next(on_g, counts[4])
            plane_q(n, 0)
            widen_next(on_s, counts[2])
            if n == 0:
                turn_k(L, NT - 1, "scores", 1)
            else:
                turn_k(n, 2, turning(n))
            empty_x(n + 1, 1)
            if n == L - 2:
                pair_recip(0)
            if n == 0:
                empty_k(L, NT - 1, 1)
            else:
                empty_k(n, 2)
            project(n, 1, [0])
            project(n, 2)
            project(n, 3)
            plane_q(n, 1)
            widen_next(on_s, counts[3])
            empty_x(n + 1, 2)
            empty_x(n + 1, 3, 0, NT, 0, 1)
            plane_q(n, 2)
            turn_x(n + 2, 0, x_bank(turning(n + 1)))
            turn_x(n + 2, 1, x_bank(turning(n)))
            turn_k(n + 1, 0, turning(n - 1))
            if n == L - 3:
                pair_max(0)
            if SHARES[n + 2]:
                share_x(n + 2)
            plane_q(n, 3)
            empty_k(n + 1, 0)
        n = L - 1
        quant_k(n - 1)
        pair_finish(0, nc.vector)
        quant_x(n, 0, NT, G, [0])
        quant_q(n - 2)
        quant_x(n, 0, NT, G, [1])
        lace(L, P - SHARES[L])
        store_later_rows(0)
        store_first_left(0)
        scores(n - 2)
        project(n, 0, [1])
        project(n, 1, [1])
        project(n, 0, [0])
        project(n, 1, [0])
        empty_x(L, 0, 0, 2)
        empty_rest(L)
        turn_x(L, 2, x_bank(turning(n + 1)))
        empty_scores(n - 2)
        park(n - 2)
        store_first_right(0)
        fetch(n - 2)
        clear_words(parked(0) + FREED, L * S * S, 4)
        turn_x(L, 3, x_bank("mixed"), [0])
        empty_q(n, 0)
        empty_q(n, 1)
        empty_x(L, 1, 0, 2)
        project(n, 2)
        project(n, 3)
        turn_k(n, 2, turning(n))
        turn_k(L, 0, turning(n - 1))
        turn_k(L, 2, "scores", 1)
        empty_x(L, 2, 2, 1)
        pair_max(1)
        empty_x(L, 3, 3, 1, 0, 1)
        quant_x(L, 0, 2, 1)
        pair_shift(1, nc.vector)
        quant_x(L, 2, 1, 1)
        quant_x(L, 3, 1, 1)
        empty_q(n, 2)
        empty_q(n, 3)
        pair_exp(1)
        empty_k(n, 2)
        weave_q(n)
        quant_q(L - 2)
        pair_sum(1)
        quant_k(L - 1)
        pair_recip(1)
        pair_max(2)
        empty_k(L, 0)
        empty_k(L, 2, 1)
        for t in range(4):
            project(L, t, ORDER, 0, 2, f"sum{1 + t // 2}")
        for t in range(4):
            project(L, t, ORDER, 2, 1, turning(n + 1))
        scores(L - 2, 0, NT, "sum0")
        for t in range(4):
            project(L, t, ORDER, 3, 1, "mixed")
        pair_finish(1, nc.vector)
        store_later_rows(1)
        store_first_left(1)
        pair_shift(2, nc.vector)
        pair_exp(2)
        quant_q(L - 1)
        quant_k(L)
        pair_sum(2)
        empty_q_v(L, 2)
        pair_recip(2)
        for t in range(4):
            empty_q(L, t, 0, 2)
        weave_q(L, 0, 2)
        scores(L - 1, 0, NT, turning(n))
        pair_finish(2)
        store_first_right(1)
        store_boxes(2, nc.sync)
        mask_scores(L - 2)
        empty_q_v(L, 3)
        row_max(L - 2)
        exps(L - 2)
        quant_q(L, 2, 2)
        scores(L, 2, 2, turning(n - 1))
        mask_scores(L - 1)
        quant_q(L, 0, 2)
        scores(L, 0, 2, "scores")
        row_max(L - 1)
        recip(L - 2)
        exps(L - 1)
        finish_v(L - 2, 0, NT, 0, nc.gpsimd)
        store_inner(L - 2)
        mask_scores(L, 2, 2)
        mask_scores(L, 0, 2)
        row_max(L, 2, 2)
        row_max(L, 0, 2)
        exps(L, 2, 2)
        recip(L - 1)
        exps(L, 0, 2)
        finish_v(L - 1)
        recip(L, 2, 2)
        store_inner(L - 1)
        recip(L, 0, 2)
        finish(L, 2, 2)
        finish_v(L, 0, 2)
        store_edges(L - 2, 3, nc.scalar)
        store_inner(L, nc.scalar)
